import numpy as np
import ml_dtypes


def mxq(x, axis, fmt="e4m3"):
    dtype, down = {"e4m3": (ml_dtypes.float8_e4m3fn, 7), "e5m2": (ml_dtypes.float8_e5m2, 14)}[fmt]
    v = np.moveaxis(np.asarray(x, np.float32).astype(ml_dtypes.bfloat16).astype(np.float64), axis, -1)
    blocks = v.reshape(v.shape[:-1] + (-1, 32))
    amax = np.abs(blocks).max(-1, keepdims=True)
    byte = np.maximum(np.where(amax > 0, np.frexp(amax)[1] - 1 + 127, 0) - down, 1)
    scale = np.exp2(byte - 127.0)
    codes = (blocks / scale).astype(np.float32).astype(dtype).astype(np.float64)
    return np.moveaxis((codes * scale).reshape(v.shape), -1, axis)


WIDE = False


def mx_kscale(k):
    if not WIDE:
        return np.ones(k)
    levels = np.array([20, -20, 10, -10, 0])
    a = np.random.permutation(np.resize(levels, k // 512 * 4)).reshape(k // 512, 4)
    idx = np.arange(k)
    return np.exp2(a[idx // 512, idx % 128 // 32])


BF16 = ml_dtypes.bfloat16


def bf(x):
    return np.asarray(x, np.float32).astype(BF16)


def f64(x):
    return np.asarray(x).astype(np.float64)


B, DIN, H1, H2, N, I, K, O = 1024, 2048, 1024, 512, 32, 16, 256, 16
NI = N * I
KO = K * O
SQ_EPS = 1e-8
G_SCALE = 16.0


def squash(t):
    sq = np.sum(t * t, axis=-1, keepdims=True)
    return (sq / (1.0 + sq)) * t / np.sqrt(sq + SQ_EPS)


def presquash(p, Wr):
    pf = f64(p).reshape(B, NI)
    wf = f64(Wr).transpose(0, 3, 1, 2).reshape(NI, KO)
    return (pf @ wf).reshape(B, K, O) * (1.0 / K)


def setup_inputs():
    u = mx_kscale(KO).reshape(K, O)[:, :1]
    p = bf(np.random.standard_normal((B, N, I)))
    Wr0 = bf(np.random.standard_normal((N, K, O, I)) * K / np.sqrt(NI * O))
    g = bf(np.random.standard_normal((B, K, O)) * np.exp2(np.random.randint(-12, 1, (B, 1, 1))) * G_SCALE * u)
    s = presquash(p, Wr0)
    return {"p": p,
            "Wr": bf(f64(Wr0) / u[None, :, :, None]),
            "s": np.asarray(s, np.float32),
            "grad_out": g}


def reference(p, Wr, s, grad_out):
    t = f64(s)
    g = f64(grad_out)
    q = np.sum(t * t, axis=-1, keepdims=True)
    r = 1.0 / np.sqrt(q + SQ_EPS)
    h = q / (1.0 + q) * r
    dh = r / (1.0 + q) ** 2 - 0.5 * q / (1.0 + q) * r ** 3
    dot = np.sum(t * g, axis=-1, keepdims=True)
    ds = h * g + 2.0 * dh * dot * t
    wf = f64(Wr).transpose(0, 3, 1, 2).reshape(NI, KO)
    dp = (mxq(ds.reshape(B, KO), 1, "e5m2") @ mxq(wf, 1, "e4m3").T) * (1.0 / K)
    return dp.reshape(B, N, I)

@@ -1,0 +1,195 @@
+from contextlib import ExitStack
+
+import concourse.mybir as mybir
+from concourse.masks import make_identity
+
+F32 = mybir.dt.float32
+BF16 = mybir.dt.bfloat16
+U32 = mybir.dt.uint32
+U8 = mybir.dt.uint8
+E5M2_X4 = mybir.dt.float8_e5m2_x4
+E4M3_X4 = mybir.dt.float8_e4m3fn_x4
+ACT = mybir.ActivationFunctionType
+ALU = mybir.AluOpType
+
+P = 128
+PACK = 4
+K_PASS = P * PACK
+
+BATCH = 1024
+N_PRIM = 32
+IN_DIM = 16
+CAPS = 256
+OUT_DIM = 16
+NI = N_PRIM * IN_DIM
+SQ_EPS = 1e-8
+
+CAPS_CHUNK = P
+COLS = CAPS_CHUNK * OUT_DIM
+PASSES = COLS // K_PASS
+HALVES = CAPS // CAPS_CHUNK
+N_CHUNKS = (BATCH // P) * HALVES
+W_PASSES = CAPS * OUT_DIM // K_PASS
+CAPS_PASS = K_PASS // OUT_DIM
+QUADS = OUT_DIM // PACK
+
+FLOPS = 2 * BATCH * CAPS * OUT_DIM * NI
+BYTES = BATCH * CAPS * OUT_DIM * (4 + 2) + NI * CAPS * OUT_DIM * 2 + BATCH * NI * 4
+
+
+def tile_capsulenetwork_pb_v_kernel(tc, p, Wr, s, grad_out, out):
+    nc = tc.nc
+    with ExitStack() as pools:
+        const = pools.enter_context(tc.tile_pool(name="const", bufs=1))
+        w_stage = pools.enter_context(tc.tile_pool(name="w_stage", bufs=2))
+        loads = pools.enter_context(tc.tile_pool(name="loads", bufs=4))
+        prods = pools.enter_context(tc.tile_pool(name="prods", bufs=2))
+        small = pools.enter_context(tc.tile_pool(name="small", bufs=2))
+        scaled = pools.enter_context(tc.tile_pool(name="scaled", bufs=2))
+        coded = pools.enter_context(tc.tile_pool(name="coded", bufs=2))
+        results = pools.enter_context(tc.tile_pool(name="results", bufs=2))
+        psum_sums = pools.enter_context(tc.psum_pool(name="psum_sums", bufs=2))
+        psum_hc = pools.enter_context(tc.psum_pool(name="psum_hc", bufs=1))
+        psum_ds = pools.enter_context(tc.psum_pool(name="psum_ds", bufs=3))
+        psum_acc = pools.enter_context(tc.psum_pool(name="psum_acc", bufs=2))
+
+        ident = const.tile([P, P], F32, name="ident")
+        make_identity(nc, ident[:])
+        eps_col = const.tile([P, 1], F32, name="eps_col")
+        nc.vector.memset(eps_col[:], SQ_EPS)
+        one_col = const.tile([P, 1], F32, name="one_col")
+        nc.vector.memset(one_col[:], 1.0)
+        minus_one_col = const.tile([P, 1], F32, name="minus_one_col")
+        nc.vector.memset(minus_one_col[:], -1.0)
+
+        w_codes = const.tile([P, W_PASSES, NI], U32, name="w_codes", align_bytes=64)
+        w_scales = const.tile([P, W_PASSES, NI], U8, name="w_scales", align_bytes=64)
+        w_view = Wr.rearrange("n (c pj) (pq t) i -> c (pj pq) n (t i)", c=W_PASSES, pq=QUADS)
+
+        def quantise_weights(c):
+            raw = w_stage.tile([P, N_PRIM, PACK * IN_DIM], BF16, name="raw")
+            nc.sync.dma_start(out=raw[:], in_=w_view[c])
+            w_grouped = w_stage.tile([P, N_PRIM, IN_DIM, PACK], BF16, name="w_grouped", align_bytes=64)
+            nc.scalar.copy(out=w_grouped[:], in_=raw[:].rearrange("q n (t i) -> q n i t", t=PACK))
+            nc.vector.quantize_mx(
+                out=w_codes[:, c, :].bitcast(E4M3_X4),
+                scales=w_scales[:, c, :],
+                in_=w_grouped[:].rearrange("q n i t -> q (n i t)"),
+            )
+
+        acc = None
+        for chunk in range(N_CHUNKS):
+            half = chunk % HALVES
+            rows = slice((chunk // HALVES) * P, (chunk // HALVES + 1) * P)
+            caps = slice(half * CAPS_CHUNK, (half + 1) * CAPS_CHUNK)
+
+            t_sb = loads.tile([P, COLS], F32, name="t_sb")
+            nc.sync.dma_start(out=t_sb[:], in_=s[rows, caps, :].rearrange("b j o -> b (j o)"))
+            g_sb = loads.tile([P, COLS], BF16, name="g_sb")
+            nc.sync.dma_start(out=g_sb[:], in_=grad_out[rows, caps, :].rearrange("b j o -> b (j o)"))
+
+            tt = prods.tile([P, COLS], F32, name="tt")
+            nc.scalar.activation(out=tt[:], in_=t_sb[:], func=ACT.Square)
+            tg = prods.tile([P, COLS], F32, name="tg")
+            nc.gpsimd.tensor_tensor(out=tg[:], in0=t_sb[:], in1=g_sb[:], op=ALU.mult)
+
+            sums = psum_sums.tile([P, 2, P], F32, name="sums")
+            for which, prod in enumerate((tt, tg)):
+                by_o = prod[:].rearrange("b (j o) -> b o j", o=OUT_DIM)
+                for o in range(OUT_DIM):
+                    nc.tensor.matmul(
+                        out=sums[:, which, :],
+                        lhsT=by_o[:, o, :],
+                        rhs=ident[:],
+                        start=(o == 0),
+                        stop=(o == OUT_DIM - 1),
+                        is_transpose=True,
+                    )
+            q = sums[:, 0, :]
+            dot = sums[:, 1, :]
+
+            root = small.tile([P, P], F32, name="root")
+            nc.scalar.activation(out=root[:], in_=q, func=ACT.Sqrt, bias=eps_col[:])
+            q1 = small.tile([P, P], F32, name="q1")
+            nc.scalar.activation(out=q1[:], in_=q, func=ACT.Identity, bias=one_col[:])
+            den = small.tile([P, P], F32, name="den")
+            nc.vector.tensor_tensor(out=den[:], in0=root[:], in1=q1[:], op=ALU.mult)
+            rw = small.tile([P, P], F32, name="rw")
+            nc.vector.reciprocal(out=rw[:], in_=den[:])
+            w = small.tile([P, P], F32, name="w")
+            nc.vector.tensor_tensor(out=w[:], in0=rw[:], in1=root[:], op=ALU.mult)
+            r = small.tile([P, P], F32, name="r")
+            nc.vector.tensor_tensor(out=r[:], in0=rw[:], in1=q1[:], op=ALU.mult)
+            eps_rr = small.tile([P, P], F32, name="eps_rr")
+            nc.scalar.activation(out=eps_rr[:], in_=r[:], func=ACT.Square, scale=SQ_EPS**0.5)
+            w2m1 = small.tile([P, P], F32, name="w2m1")
+            nc.scalar.activation(out=w2m1[:], in_=w[:], func=ACT.Identity, scale=2.0, bias=minus_one_col[:])
+            hc_t = small.tile([P, 2, P], F32, name="hc_t")
+            nc.vector.tensor_tensor(out=hc_t[:, 0, :], in0=q, in1=rw[:], op=ALU.mult)
+            rw_dot = small.tile([P, P], F32, name="rw_dot")
+            nc.vector.tensor_tensor(out=rw_dot[:], in0=dot, in1=rw[:], op=ALU.mult)
+            z = small.tile([P, P], F32, name="z")
+            nc.vector.tensor_tensor(out=z[:], in0=w2m1[:], in1=eps_rr[:], op=ALU.add)
+            nc.vector.tensor_tensor(out=hc_t[:, 1, :], in0=z[:], in1=rw_dot[:], op=ALU.mult)
+
+            hc = psum_hc.tile([P, 2, P], F32, name="hc")
+            for which in range(2):
+                nc.tensor.transpose(out=hc[:, which, :], in_=hc_t[:, which, :], identity=ident[:])
+
+            hg = scaled.tile([P, COLS], F32, name="hg")
+            ct = scaled.tile([P, COLS], F32, name="ct")
+            for which, (dst, src) in enumerate(((hg, g_sb), (ct, t_sb))):
+                dst_v = dst[:].rearrange("b (c t pj pq) -> b c t pj pq", c=PASSES, t=PACK, pq=QUADS)
+                src_v = src[:].rearrange("b (c pj pq t) -> b c t pj pq", c=PASSES, t=PACK, pq=QUADS)
+                for c in range(PASSES):
+                    factor = hc[:, which, c * CAPS_PASS : (c + 1) * CAPS_PASS]
+                    nc.vector.tensor_tensor(
+                        out=dst_v[:, c],
+                        in0=src_v[:, c],
+                        in1=factor.unsqueeze(1).unsqueeze(3).to_broadcast([P, PACK, CAPS_PASS, QUADS]),
+                        op=ALU.mult,
+                    )
+
+            grouped = coded.tile([P, PASSES, P, PACK], BF16, name="grouped", align_bytes=64)
+            hg_v = hg[:].rearrange("b (c t q) -> b c t q", c=PASSES, t=PACK)
+            ct_v = ct[:].rearrange("b (c t q) -> b c t q", c=PASSES, t=PACK)
+            for c in range(PASSES):
+                ds_t = psum_ds.tile([P, PACK, P], F32, name="ds_t")
+                for t in range(PACK):
+                    nc.tensor.matmul(
+                        out=ds_t[:, t, :], lhsT=hg_v[:, c, t, :], rhs=ident[:], start=True, stop=False, is_transpose=True
+                    )
+                    nc.tensor.matmul(
+                        out=ds_t[:, t, :], lhsT=ct_v[:, c, t, :], rhs=ident[:], start=False, stop=True, is_transpose=True
+                    )
+                nc.scalar.copy(out=grouped[:, c], in_=ds_t[:].rearrange("q t b -> q b t"))
+
+            codes = coded.tile([P, PASSES * P], U32, name="codes", align_bytes=64)
+            scales = coded.tile([P, PASSES * P], U8, name="scales", align_bytes=64)
+            nc.vector.quantize_mx(
+                out=codes[:].bitcast(E5M2_X4),
+                scales=scales[:],
+                in_=grouped[:].rearrange("q c b t -> q (c b t)"),
+            )
+
+            if chunk < HALVES:
+                for c in range(PASSES):
+                    quantise_weights(half * PASSES + c)
+
+            if half == 0:
+                acc = psum_acc.tile([P, NI], F32, name="acc")
+            for c in range(PASSES):
+                tokens = slice(c * P, (c + 1) * P)
+                nc.tensor.matmul_mx(
+                    out=acc[:],
+                    lhsT=codes[:, tokens].bitcast(E5M2_X4),
+                    lhsT_scale=scales[:, tokens],
+                    rhs=w_codes[:, half * PASSES + c, :].bitcast(E4M3_X4),
+                    rhs_scale=w_scales[:, half * PASSES + c, :],
+                    start=(half == 0 and c == 0),
+                    stop=(half == HALVES - 1 and c == PASSES - 1),
+                )
+            if half == HALVES - 1:
+                result = results.tile([P, NI], F32, name="result")
+                nc.scalar.mul(out=result[:], in_=acc[:], mul=1.0 / CAPS)
+                nc.scalar.dma_start(out=out[rows].rearrange("b n i -> b (n i)"), in_=result[:])

@@ -33,25 +33,47 @@ W_PASSES = CAPS * OUT_DIM // K_PASS
 CAPS_PASS = K_PASS // OUT_DIM
 QUADS = OUT_DIM // PACK
 
+N_PASSES = N_CHUNKS * PASSES
+SUMS_PART = 2 * OUT_DIM // PASSES
+W_PIECE = N_PRIM // PASSES
+
+LEAD_LOAD = 13
+LEAD_W_LOAD = 8
+LEAD_PRODUCTS = 5
+LAG_ROOTS = 3
+LAG_INVERSE = 4
+LAG_FACTORS = 5
+LAG_COEFFICIENTS = 6
+LAG_SCALE = 7
+LAG_TRANSPOSE = 8
+LAG_QUANTISE = 9
+LAG_W_REGROUP = 2
+LAG_W_QUANTISE = 6
+LAG_MULTIPLY = 28
+LAG_STORE = LAG_MULTIPLY + 1
+
 FLOPS = 2 * BATCH * CAPS * OUT_DIM * NI
 BYTES = BATCH * CAPS * OUT_DIM * (4 + 2) + NI * CAPS * OUT_DIM * 2 + BATCH * NI * 4
 
 
 def tile_capsulenetwork_pb_v_kernel(tc, p, Wr, s, grad_out, out):
     nc = tc.nc
-    with ExitStack() as pools:
-        const = pools.enter_context(tc.tile_pool(name="const", bufs=1))
-        w_stage = pools.enter_context(tc.tile_pool(name="w_stage", bufs=2))
-        loads = pools.enter_context(tc.tile_pool(name="loads", bufs=4))
-        prods = pools.enter_context(tc.tile_pool(name="prods", bufs=2))
-        small = pools.enter_context(tc.tile_pool(name="small", bufs=2))
-        scaled = pools.enter_context(tc.tile_pool(name="scaled", bufs=2))
-        coded = pools.enter_context(tc.tile_pool(name="coded", bufs=2))
-        results = pools.enter_context(tc.tile_pool(name="results", bufs=2))
-        psum_sums = pools.enter_context(tc.psum_pool(name="psum_sums", bufs=2))
-        psum_hc = pools.enter_context(tc.psum_pool(name="psum_hc", bufs=1))
-        psum_ds = pools.enter_context(tc.psum_pool(name="psum_ds", bufs=3))
-        psum_acc = pools.enter_context(tc.psum_pool(name="psum_acc", bufs=2))
+    with ExitStack() as stack:
+        const = stack.enter_context(tc.tile_pool(name="const", bufs=1))
+        w_raw = stack.enter_context(tc.tile_pool(name="w_raw", bufs=4))
+        w_stage = stack.enter_context(tc.tile_pool(name="w_stage", bufs=2))
+        loads = stack.enter_context(tc.tile_pool(name="loads", bufs=6))
+        prods = stack.enter_context(tc.tile_pool(name="prods", bufs=3))
+        small = stack.enter_context(tc.tile_pool(name="small", bufs=2))
+        scaled = stack.enter_context(tc.tile_pool(name="scaled", bufs=3))
+        rounded = stack.enter_context(tc.tile_pool(name="rounded", bufs=3))
+        coded = stack.enter_context(tc.tile_pool(name="coded", bufs=LAG_MULTIPLY - LAG_QUANTISE + 2))
+        results = stack.enter_context(tc.tile_pool(name="results", bufs=2))
+        psum_sums = stack.enter_context(tc.psum_pool(name="psum_sums", bufs=2))
+        psum_hc = stack.enter_context(tc.psum_pool(name="psum_hc", bufs=2))
+        psum_ds = stack.enter_context(tc.psum_pool(name="psum_ds", bufs=2))
+        psum_acc = stack.enter_context(tc.psum_pool(name="psum_acc", bufs=2))
+        stack.enter_context(tc.manual_schedule())
 
         ident = const.tile([P, P], F32, name="ident")
         make_identity(nc, ident[:])
@@ -61,135 +83,225 @@ def tile_capsulenetwork_pb_v_kernel(tc, p, Wr, s, grad_out, out):
         nc.vector.memset(one_col[:], 1.0)
         minus_one_col = const.tile([P, 1], F32, name="minus_one_col")
         nc.vector.memset(minus_one_col[:], -1.0)
-
         w_codes = const.tile([P, W_PASSES, NI], U32, name="w_codes", align_bytes=64)
         w_scales = const.tile([P, W_PASSES, NI], U8, name="w_scales", align_bytes=64)
         w_view = Wr.rearrange("n (c pj) (pq t) i -> c (pj pq) n (t i)", c=W_PASSES, pq=QUADS)
 
-        def quantise_weights(c):
-            raw = w_stage.tile([P, N_PRIM, PACK * IN_DIM], BF16, name="raw")
-            nc.sync.dma_start(out=raw[:], in_=w_view[c])
-            w_grouped = w_stage.tile([P, N_PRIM, IN_DIM, PACK], BF16, name="w_grouped", align_bytes=64)
-            nc.scalar.copy(out=w_grouped[:], in_=raw[:].rearrange("q n (t i) -> q n i t", t=PACK))
-            nc.vector.quantize_mx(
-                out=w_codes[:, c, :].bitcast(E4M3_X4),
-                scales=w_scales[:, c, :],
-                in_=w_grouped[:].rearrange("q n i t -> q (n i t)"),
-            )
+        tiles = {}
 
-        acc = None
-        for chunk in range(N_CHUNKS):
-            half = chunk % HALVES
-            rows = slice((chunk // HALVES) * P, (chunk // HALVES + 1) * P)
-            caps = slice(half * CAPS_CHUNK, (half + 1) * CAPS_CHUNK)
-
+        def load_chunk(n):
+            rows = slice((n // HALVES) * P, (n // HALVES + 1) * P)
+            caps = slice((n % HALVES) * CAPS_CHUNK, (n % HALVES + 1) * CAPS_CHUNK)
             t_sb = loads.tile([P, COLS], F32, name="t_sb")
             nc.sync.dma_start(out=t_sb[:], in_=s[rows, caps, :].rearrange("b j o -> b (j o)"))
             g_sb = loads.tile([P, COLS], BF16, name="g_sb")
             nc.sync.dma_start(out=g_sb[:], in_=grad_out[rows, caps, :].rearrange("b j o -> b (j o)"))
+            tiles["t", n] = t_sb
+            tiles["g", n] = g_sb
 
-            tt = prods.tile([P, COLS], F32, name="tt")
-            nc.scalar.activation(out=tt[:], in_=t_sb[:], func=ACT.Square)
-            tg = prods.tile([P, COLS], F32, name="tg")
-            nc.gpsimd.tensor_tensor(out=tg[:], in0=t_sb[:], in1=g_sb[:], op=ALU.mult)
+        def load_weights(c):
+            raw = w_raw.tile([P, N_PRIM, PACK * IN_DIM], BF16, name="raw")
+            nc.sync.dma_start(out=raw[:], in_=w_view[c])
+            tiles["raw", c] = raw
 
-            sums = psum_sums.tile([P, 2, P], F32, name="sums")
-            for which, prod in enumerate((tt, tg)):
-                by_o = prod[:].rearrange("b (j o) -> b o j", o=OUT_DIM)
-                for o in range(OUT_DIM):
-                    nc.tensor.matmul(
-                        out=sums[:, which, :],
-                        lhsT=by_o[:, o, :],
-                        rhs=ident[:],
-                        start=(o == 0),
-                        stop=(o == OUT_DIM - 1),
-                        is_transpose=True,
-                    )
-            q = sums[:, 0, :]
-            dot = sums[:, 1, :]
+        def regroup_weights(c, x):
+            if x == 0:
+                w_grouped = w_stage.tile([P, N_PRIM, IN_DIM, PACK], BF16, name="w_grouped", align_bytes=64)
+                tiles["w_grouped", c] = w_grouped
+            part = slice(x * W_PIECE, (x + 1) * W_PIECE)
+            nc.scalar.copy(
+                out=tiles["w_grouped", c][:, part],
+                in_=tiles["raw", c][:, part].rearrange("q n (t i) -> q n i t", t=PACK),
+            )
 
-            root = small.tile([P, P], F32, name="root")
-            nc.scalar.activation(out=root[:], in_=q, func=ACT.Sqrt, bias=eps_col[:])
-            q1 = small.tile([P, P], F32, name="q1")
-            nc.scalar.activation(out=q1[:], in_=q, func=ACT.Identity, bias=one_col[:])
+        def quantise_weights(c):
+            nc.vector.quantize_mx(
+                out=w_codes[:, c, :].bitcast(E4M3_X4),
+                scales=w_scales[:, c, :],
+                in_=tiles["w_grouped", c][:].rearrange("q n i t -> q (n i t)"),
+            )
+
+        def products(n, k):
+            if k == 0:
+                tt = prods.tile([P, COLS], F32, name="tt")
+                tg = prods.tile([P, COLS], F32, name="tg")
+                tiles["tt", n] = tt
+                tiles["tg", n] = tg
+            cols = slice(k * K_PASS, (k + 1) * K_PASS)
+            nc.scalar.activation(out=tiles["tt", n][:, cols], in_=tiles["t", n][:, cols], func=ACT.Square)
+            nc.gpsimd.tensor_tensor(
+                out=tiles["tg", n][:, cols], in0=tiles["t", n][:, cols], in1=tiles["g", n][:, cols], op=ALU.mult
+            )
+
+        def add_over_o(n, k):
+            if k == 0:
+                sums = psum_sums.tile([P, 2, P], F32, name="sums")
+                tiles["sums", n] = sums
+            for i in range(k * SUMS_PART, (k + 1) * SUMS_PART):
+                which, o = divmod(i, OUT_DIM)
+                prod = tiles[("tt", "tg")[which], n]
+                nc.tensor.matmul(
+                    out=tiles["sums", n][:, which, :],
+                    lhsT=prod[:].rearrange("b (j o) -> b o j", o=OUT_DIM)[:, o, :],
+                    rhs=ident[:],
+                    start=(o == 0),
+                    stop=(o == OUT_DIM - 1),
+                    is_transpose=True,
+                )
+
+        def roots(n):
+            root_q1 = small.tile([P, 2, P], F32, name="root_q1")
+            q = tiles["sums", n][:, 0, :]
+            nc.scalar.activation(out=root_q1[:, 0, :], in_=q, func=ACT.Sqrt, bias=eps_col[:])
+            nc.scalar.activation(out=root_q1[:, 1, :], in_=q, func=ACT.Identity, bias=one_col[:])
+            tiles["root_q1", n] = root_q1
+
+        def inverse(n):
+            root_q1 = tiles["root_q1", n]
             den = small.tile([P, P], F32, name="den")
-            nc.vector.tensor_tensor(out=den[:], in0=root[:], in1=q1[:], op=ALU.mult)
+            nc.vector.tensor_tensor(out=den[:], in0=root_q1[:, 0, :], in1=root_q1[:, 1, :], op=ALU.mult)
             rw = small.tile([P, P], F32, name="rw")
             nc.vector.reciprocal(out=rw[:], in_=den[:])
-            w = small.tile([P, P], F32, name="w")
-            nc.vector.tensor_tensor(out=w[:], in0=rw[:], in1=root[:], op=ALU.mult)
-            r = small.tile([P, P], F32, name="r")
-            nc.vector.tensor_tensor(out=r[:], in0=rw[:], in1=q1[:], op=ALU.mult)
-            eps_rr = small.tile([P, P], F32, name="eps_rr")
-            nc.scalar.activation(out=eps_rr[:], in_=r[:], func=ACT.Square, scale=SQ_EPS**0.5)
-            w2m1 = small.tile([P, P], F32, name="w2m1")
-            nc.scalar.activation(out=w2m1[:], in_=w[:], func=ACT.Identity, scale=2.0, bias=minus_one_col[:])
-            hc_t = small.tile([P, 2, P], F32, name="hc_t")
-            nc.vector.tensor_tensor(out=hc_t[:, 0, :], in0=q, in1=rw[:], op=ALU.mult)
-            rw_dot = small.tile([P, P], F32, name="rw_dot")
-            nc.vector.tensor_tensor(out=rw_dot[:], in0=dot, in1=rw[:], op=ALU.mult)
-            z = small.tile([P, P], F32, name="z")
-            nc.vector.tensor_tensor(out=z[:], in0=w2m1[:], in1=eps_rr[:], op=ALU.add)
-            nc.vector.tensor_tensor(out=hc_t[:, 1, :], in0=z[:], in1=rw_dot[:], op=ALU.mult)
+            tiles["rw", n] = rw
 
+        def factors(n):
+            twice = tiles["rw", n][:].unsqueeze(1).to_broadcast([P, 2, P])
+            w_r = small.tile([P, 2, P], F32, name="w_r")
+            nc.vector.tensor_tensor(out=w_r[:], in0=tiles["root_q1", n][:], in1=twice, op=ALU.mult)
+            h_c = small.tile([P, 2, P], F32, name="h_c")
+            nc.vector.tensor_tensor(out=h_c[:], in0=tiles["sums", n][:], in1=twice, op=ALU.mult)
+            tiles["w_r", n] = w_r
+            tiles["h_c", n] = h_c
+
+        def corrections(n):
+            w_r = tiles["w_r", n]
+            w2m1 = small.tile([P, P], F32, name="w2m1")
+            nc.scalar.activation(out=w2m1[:], in_=w_r[:, 0, :], func=ACT.Identity, scale=2.0, bias=minus_one_col[:])
+            eps_rr = small.tile([P, P], F32, name="eps_rr")
+            nc.scalar.activation(out=eps_rr[:], in_=w_r[:, 1, :], func=ACT.Square, scale=SQ_EPS**0.5)
+            tiles["w2m1", n] = w2m1
+            tiles["eps_rr", n] = eps_rr
+
+        def coefficients(n):
+            z = small.tile([P, P], F32, name="z")
+            nc.vector.tensor_tensor(out=z[:], in0=tiles["w2m1", n][:], in1=tiles["eps_rr", n][:], op=ALU.add)
+            coef = tiles["h_c", n][:, 1, :]
+            nc.vector.tensor_tensor(out=coef, in0=z[:], in1=coef, op=ALU.mult)
+
+        def to_tokens(n):
             hc = psum_hc.tile([P, 2, P], F32, name="hc")
             for which in range(2):
-                nc.tensor.transpose(out=hc[:, which, :], in_=hc_t[:, which, :], identity=ident[:])
+                nc.tensor.transpose(out=hc[:, which, :], in_=tiles["h_c", n][:, which, :], identity=ident[:])
+            tiles["hc", n] = hc
 
-            hg = scaled.tile([P, COLS], F32, name="hg")
-            ct = scaled.tile([P, COLS], F32, name="ct")
-            for which, (dst, src) in enumerate(((hg, g_sb), (ct, t_sb))):
-                dst_v = dst[:].rearrange("b (c t pj pq) -> b c t pj pq", c=PASSES, t=PACK, pq=QUADS)
-                src_v = src[:].rearrange("b (c pj pq t) -> b c t pj pq", c=PASSES, t=PACK, pq=QUADS)
-                for c in range(PASSES):
-                    factor = hc[:, which, c * CAPS_PASS : (c + 1) * CAPS_PASS]
-                    nc.vector.tensor_tensor(
-                        out=dst_v[:, c],
-                        in0=src_v[:, c],
-                        in1=factor.unsqueeze(1).unsqueeze(3).to_broadcast([P, PACK, CAPS_PASS, QUADS]),
-                        op=ALU.mult,
-                    )
+        def scale(n, k):
+            cols = slice(k * K_PASS, (k + 1) * K_PASS)
+            caps = slice(k * CAPS_PASS, (k + 1) * CAPS_PASS)
+            hg = scaled.tile([P, PACK, P], F32, name="hg")
+            ct = scaled.tile([P, PACK, P], F32, name="ct")
+            for which, (dst, src) in enumerate(((hg, tiles["g", n]), (ct, tiles["t", n]))):
+                nc.vector.tensor_tensor(
+                    out=dst[:].rearrange("b t (pj pq) -> b pj pq t", pq=QUADS),
+                    in0=src[:, cols].rearrange("b (pj pq t) -> b pj pq t", pq=QUADS, t=PACK),
+                    in1=tiles["hc", n][:, which, caps]
+                    .unsqueeze(2)
+                    .unsqueeze(3)
+                    .to_broadcast([P, CAPS_PASS, QUADS, PACK]),
+                    op=ALU.mult,
+                )
+            tiles["hg", n, k] = hg
+            tiles["ct", n, k] = ct
 
-            grouped = coded.tile([P, PASSES, P, PACK], BF16, name="grouped", align_bytes=64)
-            hg_v = hg[:].rearrange("b (c t q) -> b c t q", c=PASSES, t=PACK)
-            ct_v = ct[:].rearrange("b (c t q) -> b c t q", c=PASSES, t=PACK)
-            for c in range(PASSES):
-                ds_t = psum_ds.tile([P, PACK, P], F32, name="ds_t")
-                for t in range(PACK):
-                    nc.tensor.matmul(
-                        out=ds_t[:, t, :], lhsT=hg_v[:, c, t, :], rhs=ident[:], start=True, stop=False, is_transpose=True
-                    )
-                    nc.tensor.matmul(
-                        out=ds_t[:, t, :], lhsT=ct_v[:, c, t, :], rhs=ident[:], start=False, stop=True, is_transpose=True
-                    )
-                nc.scalar.copy(out=grouped[:, c], in_=ds_t[:].rearrange("q t b -> q b t"))
+        def transpose_add(n, k):
+            ds_t = psum_ds.tile([P, PACK, P], F32, name="ds_t")
+            for t in range(PACK):
+                nc.tensor.matmul(
+                    out=ds_t[:, t, :], lhsT=tiles["hg", n, k][:, t, :], rhs=ident[:],
+                    start=True, stop=False, is_transpose=True,
+                )
+                nc.tensor.matmul(
+                    out=ds_t[:, t, :], lhsT=tiles["ct", n, k][:, t, :], rhs=ident[:],
+                    start=False, stop=True, is_transpose=True,
+                )
+            tiles["ds_t", n, k] = ds_t
 
-            codes = coded.tile([P, PASSES * P], U32, name="codes", align_bytes=64)
-            scales = coded.tile([P, PASSES * P], U8, name="scales", align_bytes=64)
+        def round_and_group(n, k):
+            grouped = rounded.tile([P, P, PACK], BF16, name="grouped", align_bytes=64)
+            nc.scalar.copy(out=grouped[:], in_=tiles["ds_t", n, k][:].rearrange("q t b -> q b t"))
+            tiles["grouped", n, k] = grouped
+
+        def quantise(n, k):
+            codes = coded.tile([P, P], U32, name="codes", align_bytes=64)
+            scales = coded.tile([P, P], U8, name="scales", align_bytes=64)
             nc.vector.quantize_mx(
                 out=codes[:].bitcast(E5M2_X4),
                 scales=scales[:],
-                in_=grouped[:].rearrange("q c b t -> q (c b t)"),
+                in_=tiles["grouped", n, k][:].rearrange("q b t -> q (b t)"),
+            )
+            tiles["codes", n, k] = codes
+            tiles["scales", n, k] = scales
+
+        def multiply(n, k):
+            block, half = divmod(n, HALVES)
+            c = half * PASSES + k
+            if c == 0:
+                acc = psum_acc.tile([P, NI], F32, name="acc")
+                tiles["acc", block] = acc
+            nc.tensor.matmul_mx(
+                out=tiles["acc", block][:],
+                lhsT=tiles["codes", n, k][:].bitcast(E5M2_X4),
+                lhsT_scale=tiles["scales", n, k][:],
+                rhs=w_codes[:, c, :].bitcast(E4M3_X4),
+                rhs_scale=w_scales[:, c, :],
+                start=(c == 0),
+                stop=(c == W_PASSES - 1),
             )
 
-            if chunk < HALVES:
-                for c in range(PASSES):
-                    quantise_weights(half * PASSES + c)
+        def store(block):
+            result = results.tile([P, NI], F32, name="result")
+            nc.scalar.mul(out=result[:], in_=tiles["acc", block][:], mul=1.0 / CAPS)
+            nc.scalar.dma_start(out=out[block * P : (block + 1) * P].rearrange("b n i -> b (n i)"), in_=result[:])
 
-            if half == 0:
-                acc = psum_acc.tile([P, NI], F32, name="acc")
-            for c in range(PASSES):
-                tokens = slice(c * P, (c + 1) * P)
-                nc.tensor.matmul_mx(
-                    out=acc[:],
-                    lhsT=codes[:, tokens].bitcast(E5M2_X4),
-                    lhsT_scale=scales[:, tokens],
-                    rhs=w_codes[:, half * PASSES + c, :].bitcast(E4M3_X4),
-                    rhs_scale=w_scales[:, half * PASSES + c, :],
-                    start=(half == 0 and c == 0),
-                    stop=(half == HALVES - 1 and c == PASSES - 1),
-                )
-            if half == HALVES - 1:
-                result = results.tile([P, NI], F32, name="result")
-                nc.scalar.mul(out=result[:], in_=acc[:], mul=1.0 / CAPS)
-                nc.scalar.dma_start(out=out[rows].rearrange("b n i -> b (n i)"), in_=result[:])
+        def live(v):
+            return 0 <= v < N_PASSES
+
+        def starts_chunk(v):
+            return live(v) and v % PASSES == 0
+
+        for u in range(-LEAD_LOAD, N_PASSES + LAG_STORE):
+            if starts_chunk(u + LEAD_LOAD):
+                load_chunk((u + LEAD_LOAD) // PASSES)
+            if starts_chunk(u + LEAD_W_LOAD) and (u + LEAD_W_LOAD) // PASSES < W_PASSES:
+                load_weights((u + LEAD_W_LOAD) // PASSES)
+            if live(u - LAG_QUANTISE):
+                round_and_group(*divmod(u - LAG_QUANTISE, PASSES))
+            if starts_chunk(u - LAG_INVERSE):
+                inverse((u - LAG_INVERSE) // PASSES)
+            if starts_chunk(u - LAG_FACTORS):
+                factors((u - LAG_FACTORS) // PASSES)
+            if starts_chunk(u - LAG_COEFFICIENTS):
+                coefficients((u - LAG_COEFFICIENTS) // PASSES)
+            if live(u):
+                add_over_o(*divmod(u, PASSES))
+            if starts_chunk(u - LAG_COEFFICIENTS):
+                to_tokens((u - LAG_COEFFICIENTS) // PASSES)
+            if live(u - LAG_SCALE):
+                scale(*divmod(u - LAG_SCALE, PASSES))
+            if starts_chunk(u - LAG_ROOTS):
+                roots((u - LAG_ROOTS) // PASSES)
+            if starts_chunk(u - LAG_FACTORS):
+                corrections((u - LAG_FACTORS) // PASSES)
+            if live(u + LEAD_PRODUCTS):
+                products(*divmod(u + LEAD_PRODUCTS, PASSES))
+            if live(u - LAG_MULTIPLY):
+                multiply(*divmod(u - LAG_MULTIPLY, PASSES))
+            if live(u - LAG_STORE) and (u - LAG_STORE) % W_PASSES == W_PASSES - 1:
+                store((u - LAG_STORE) // W_PASSES)
+            if live(u - LAG_TRANSPOSE):
+                transpose_add(*divmod(u - LAG_TRANSPOSE, PASSES))
+            if live(u - LAG_QUANTISE):
+                quantise(*divmod(u - LAG_QUANTISE, PASSES))
+            if starts_chunk(u - LAG_W_QUANTISE) and (u - LAG_W_QUANTISE) // PASSES < W_PASSES:
+                quantise_weights((u - LAG_W_QUANTISE) // PASSES)
+            if 0 <= u - LAG_W_REGROUP < W_PASSES * PASSES:
+                regroup_weights(*divmod(u - LAG_W_REGROUP, PASSES))

@@ -33,24 +33,17 @@ W_PASSES = CAPS * OUT_DIM // K_PASS
 CAPS_PASS = K_PASS // OUT_DIM
 QUADS = OUT_DIM // PACK
 
-N_PASSES = N_CHUNKS * PASSES
-SUMS_PART = 2 * OUT_DIM // PASSES
-W_PIECE = N_PRIM // PASSES
+W_HALF = N_PRIM // 2
 
-LEAD_LOAD = 13
-LEAD_W_LOAD = 8
-LEAD_PRODUCTS = 5
-LAG_ROOTS = 3
-LAG_INVERSE = 4
-LAG_FACTORS = 5
-LAG_COEFFICIENTS = 6
-LAG_SCALE = 7
-LAG_TRANSPOSE = 8
-LAG_QUANTISE = 9
-LAG_W_REGROUP = 2
-LAG_W_QUANTISE = 6
-LAG_MULTIPLY = 28
-LAG_STORE = LAG_MULTIPLY + 1
+LEAD_LOAD = 3
+LEAD_W_LOAD = 2
+LEAD_PRODUCTS = 1
+LAG_COEFFICIENTS = 1
+LAG_SCALE = 2
+LAG_TRANSPOSE = 3
+LAG_QUANTISE = 4
+LAG_W_QUANTISE = 1
+LAG_MULTIPLY = 7
 
 FLOPS = 2 * BATCH * CAPS * OUT_DIM * NI
 BYTES = BATCH * CAPS * OUT_DIM * (4 + 2) + NI * CAPS * OUT_DIM * 2 + BATCH * NI * 4
@@ -60,19 +53,19 @@ def tile_capsulenetwork_pb_v_kernel(tc, p, Wr, s, grad_out, out):
     nc = tc.nc
     with ExitStack() as stack:
         const = stack.enter_context(tc.tile_pool(name="const", bufs=1))
-        w_raw = stack.enter_context(tc.tile_pool(name="w_raw", bufs=4))
+        w_raw = stack.enter_context(tc.tile_pool(name="w_raw", bufs=3))
         w_stage = stack.enter_context(tc.tile_pool(name="w_stage", bufs=2))
         loads = stack.enter_context(tc.tile_pool(name="loads", bufs=6))
-        prods = stack.enter_context(tc.tile_pool(name="prods", bufs=3))
+        prods = stack.enter_context(tc.tile_pool(name="prods", bufs=2))
         small = stack.enter_context(tc.tile_pool(name="small", bufs=2))
-        scaled = stack.enter_context(tc.tile_pool(name="scaled", bufs=3))
-        rounded = stack.enter_context(tc.tile_pool(name="rounded", bufs=3))
-        coded = stack.enter_context(tc.tile_pool(name="coded", bufs=LAG_MULTIPLY - LAG_QUANTISE + 2))
+        scaled = stack.enter_context(tc.tile_pool(name="scaled", bufs=2))
+        rounded = stack.enter_context(tc.tile_pool(name="rounded", bufs=2))
+        coded = stack.enter_context(tc.tile_pool(name="coded", bufs=LAG_MULTIPLY - LAG_QUANTISE + 1))
         results = stack.enter_context(tc.tile_pool(name="results", bufs=2))
         psum_sums = stack.enter_context(tc.psum_pool(name="psum_sums", bufs=2))
-        psum_hc = stack.enter_context(tc.psum_pool(name="psum_hc", bufs=2))
-        psum_ds = stack.enter_context(tc.psum_pool(name="psum_ds", bufs=2))
-        psum_acc = stack.enter_context(tc.psum_pool(name="psum_acc", bufs=2))
+        psum_hc = stack.enter_context(tc.psum_pool(name="psum_hc", bufs=1))
+        psum_ds = stack.enter_context(tc.psum_pool(name="psum_ds", bufs=PASSES))
+        psum_acc = stack.enter_context(tc.psum_pool(name="psum_acc", bufs=1))
         stack.enter_context(tc.manual_schedule())
 
         ident = const.tile([P, P], F32, name="ident")
@@ -108,7 +101,7 @@ def tile_capsulenetwork_pb_v_kernel(tc, p, Wr, s, grad_out, out):
             if x == 0:
                 w_grouped = w_stage.tile([P, N_PRIM, IN_DIM, PACK], BF16, name="w_grouped", align_bytes=64)
                 tiles["w_grouped", c] = w_grouped
-            part = slice(x * W_PIECE, (x + 1) * W_PIECE)
+            part = slice(x * W_HALF, (x + 1) * W_HALF)
             nc.scalar.copy(
                 out=tiles["w_grouped", c][:, part],
                 in_=tiles["raw", c][:, part].rearrange("q n (t i) -> q n i t", t=PACK),
@@ -121,33 +114,24 @@ def tile_capsulenetwork_pb_v_kernel(tc, p, Wr, s, grad_out, out):
                 in_=tiles["w_grouped", c][:].rearrange("q n i t -> q (n i t)"),
             )
 
-        def products(n, k):
-            if k == 0:
-                tt = prods.tile([P, COLS], F32, name="tt")
-                tg = prods.tile([P, COLS], F32, name="tg")
-                tiles["tt", n] = tt
-                tiles["tg", n] = tg
-            cols = slice(k * K_PASS, (k + 1) * K_PASS)
-            nc.scalar.activation(out=tiles["tt", n][:, cols], in_=tiles["t", n][:, cols], func=ACT.Square)
-            nc.gpsimd.tensor_tensor(
-                out=tiles["tg", n][:, cols], in0=tiles["t", n][:, cols], in1=tiles["g", n][:, cols], op=ALU.mult
-            )
+        def products(n):
+            tt = prods.tile([P, COLS], F32, name="tt")
+            nc.scalar.activation(out=tt[:], in_=tiles["t", n][:], func=ACT.Square)
+            tg = prods.tile([P, COLS], F32, name="tg")
+            nc.gpsimd.tensor_tensor(out=tg[:], in0=tiles["t", n][:], in1=tiles["g", n][:], op=ALU.mult)
+            tiles["tt", n] = tt
+            tiles["tg", n] = tg
 
-        def add_over_o(n, k):
-            if k == 0:
-                sums = psum_sums.tile([P, 2, P], F32, name="sums")
-                tiles["sums", n] = sums
-            for i in range(k * SUMS_PART, (k + 1) * SUMS_PART):
-                which, o = divmod(i, OUT_DIM)
-                prod = tiles[("tt", "tg")[which], n]
-                nc.tensor.matmul(
-                    out=tiles["sums", n][:, which, :],
-                    lhsT=prod[:].rearrange("b (j o) -> b o j", o=OUT_DIM)[:, o, :],
-                    rhs=ident[:],
-                    start=(o == 0),
-                    stop=(o == OUT_DIM - 1),
-                    is_transpose=True,
-                )
+        def add_over_o(n):
+            sums = psum_sums.tile([P, 2, P], F32, name="sums")
+            for which, prod in enumerate((tiles["tt", n], tiles["tg", n])):
+                by_o = prod[:].rearrange("b (j o) -> b o j", o=OUT_DIM)
+                for o in range(OUT_DIM):
+                    nc.tensor.matmul(
+                        out=sums[:, which, :], lhsT=by_o[:, o, :], rhs=ident[:],
+                        start=(o == 0), stop=(o == OUT_DIM - 1), is_transpose=True,
+                    )
+            tiles["sums", n] = sums
 
         def roots(n):
             root_q1 = small.tile([P, 2, P], F32, name="root_q1")
@@ -194,114 +178,103 @@ def tile_capsulenetwork_pb_v_kernel(tc, p, Wr, s, grad_out, out):
                 nc.tensor.transpose(out=hc[:, which, :], in_=tiles["h_c", n][:, which, :], identity=ident[:])
             tiles["hc", n] = hc
 
-        def scale(n, k):
-            cols = slice(k * K_PASS, (k + 1) * K_PASS)
-            caps = slice(k * CAPS_PASS, (k + 1) * CAPS_PASS)
-            hg = scaled.tile([P, PACK, P], F32, name="hg")
-            ct = scaled.tile([P, PACK, P], F32, name="ct")
-            for which, (dst, src) in enumerate(((hg, tiles["g", n]), (ct, tiles["t", n]))):
-                nc.vector.tensor_tensor(
-                    out=dst[:].rearrange("b t (pj pq) -> b pj pq t", pq=QUADS),
-                    in0=src[:, cols].rearrange("b (pj pq t) -> b pj pq t", pq=QUADS, t=PACK),
-                    in1=tiles["hc", n][:, which, caps]
-                    .unsqueeze(2)
-                    .unsqueeze(3)
-                    .to_broadcast([P, CAPS_PASS, QUADS, PACK]),
-                    op=ALU.mult,
-                )
-            tiles["hg", n, k] = hg
-            tiles["ct", n, k] = ct
+        def scale(n, which):
+            scaled_to = scaled.tile([P, PASSES, PACK, P], F32, name=("hg", "ct")[which])
+            nc.vector.tensor_tensor(
+                out=scaled_to[:].rearrange("b c t (pj pq) -> b c pj pq t", pq=QUADS),
+                in0=tiles[("g", "t")[which], n][:].rearrange("b (c pj pq t) -> b c pj pq t", c=PASSES, pq=QUADS, t=PACK),
+                in1=tiles["hc", n][:, which, :]
+                .rearrange("b (c pj) -> b c pj", c=PASSES)
+                .unsqueeze(3)
+                .unsqueeze(4)
+                .to_broadcast([P, PASSES, CAPS_PASS, QUADS, PACK]),
+                op=ALU.mult,
+            )
+            tiles[("hg", "ct")[which], n] = scaled_to
 
-        def transpose_add(n, k):
+        def transpose_add(n, c):
             ds_t = psum_ds.tile([P, PACK, P], F32, name="ds_t")
             for t in range(PACK):
                 nc.tensor.matmul(
-                    out=ds_t[:, t, :], lhsT=tiles["hg", n, k][:, t, :], rhs=ident[:],
+                    out=ds_t[:, t, :], lhsT=tiles["hg", n][:, c, t, :], rhs=ident[:],
                     start=True, stop=False, is_transpose=True,
                 )
                 nc.tensor.matmul(
-                    out=ds_t[:, t, :], lhsT=tiles["ct", n, k][:, t, :], rhs=ident[:],
+                    out=ds_t[:, t, :], lhsT=tiles["ct", n][:, c, t, :], rhs=ident[:],
                     start=False, stop=True, is_transpose=True,
                 )
-            tiles["ds_t", n, k] = ds_t
-
-        def round_and_group(n, k):
-            grouped = rounded.tile([P, P, PACK], BF16, name="grouped", align_bytes=64)
-            nc.scalar.copy(out=grouped[:], in_=tiles["ds_t", n, k][:].rearrange("q t b -> q b t"))
-            tiles["grouped", n, k] = grouped
-
-        def quantise(n, k):
-            codes = coded.tile([P, P], U32, name="codes", align_bytes=64)
-            scales = coded.tile([P, P], U8, name="scales", align_bytes=64)
-            nc.vector.quantize_mx(
-                out=codes[:].bitcast(E5M2_X4),
-                scales=scales[:],
-                in_=tiles["grouped", n, k][:].rearrange("q b t -> q (b t)"),
-            )
-            tiles["codes", n, k] = codes
-            tiles["scales", n, k] = scales
-
-        def multiply(n, k):
-            block, half = divmod(n, HALVES)
-            c = half * PASSES + k
             if c == 0:
+                grouped = rounded.tile([P, PASSES, P, PACK], BF16, name="grouped", align_bytes=64)
+                tiles["grouped", n] = grouped
+            nc.scalar.copy(out=tiles["grouped", n][:, c], in_=ds_t[:].rearrange("q t b -> q b t"))
+
+        def quantise(n):
+            codes = coded.tile([P, PASSES, P], U32, name="codes", align_bytes=64)
+            scales = coded.tile([P, PASSES, P], U8, name="scales", align_bytes=64)
+            nc.vector.quantize_mx(
+                out=codes[:].rearrange("q c b -> q (c b)").bitcast(E5M2_X4),
+                scales=scales[:].rearrange("q c b -> q (c b)"),
+                in_=tiles["grouped", n][:].rearrange("q c b t -> q (c b t)"),
+            )
+            tiles["codes", n] = codes
+            tiles["scales", n] = scales
+
+        def multiply(n):
+            block, half = divmod(n, HALVES)
+            if half == 0:
                 acc = psum_acc.tile([P, NI], F32, name="acc")
                 tiles["acc", block] = acc
-            nc.tensor.matmul_mx(
-                out=tiles["acc", block][:],
-                lhsT=tiles["codes", n, k][:].bitcast(E5M2_X4),
-                lhsT_scale=tiles["scales", n, k][:],
-                rhs=w_codes[:, c, :].bitcast(E4M3_X4),
-                rhs_scale=w_scales[:, c, :],
-                start=(c == 0),
-                stop=(c == W_PASSES - 1),
-            )
+            for c in range(PASSES):
+                nc.tensor.matmul_mx(
+                    out=tiles["acc", block][:],
+                    lhsT=tiles["codes", n][:, c, :].bitcast(E5M2_X4),
+                    lhsT_scale=tiles["scales", n][:, c, :],
+                    rhs=w_codes[:, half * PASSES + c, :].bitcast(E4M3_X4),
+                    rhs_scale=w_scales[:, half * PASSES + c, :],
+                    start=(half == 0 and c == 0),
+                    stop=(half == HALVES - 1 and c == PASSES - 1),
+                )
+            if half == HALVES - 1:
+                result = results.tile([P, NI], F32, name="result")
+                nc.scalar.mul(out=result[:], in_=tiles["acc", block][:], mul=1.0 / CAPS)
+                nc.scalar.dma_start(out=out[block * P : (block + 1) * P].rearrange("b n i -> b (n i)"), in_=result[:])
 
-        def store(block):
-            result = results.tile([P, NI], F32, name="result")
-            nc.scalar.mul(out=result[:], in_=tiles["acc", block][:], mul=1.0 / CAPS)
-            nc.scalar.dma_start(out=out[block * P : (block + 1) * P].rearrange("b n i -> b (n i)"), in_=result[:])
+        def live(n):
+            return 0 <= n < N_CHUNKS
 
-        def live(v):
-            return 0 <= v < N_PASSES
-
-        def starts_chunk(v):
-            return live(v) and v % PASSES == 0
-
-        for u in range(-LEAD_LOAD, N_PASSES + LAG_STORE):
-            if starts_chunk(u + LEAD_LOAD):
-                load_chunk((u + LEAD_LOAD) // PASSES)
-            if starts_chunk(u + LEAD_W_LOAD) and (u + LEAD_W_LOAD) // PASSES < W_PASSES:
-                load_weights((u + LEAD_W_LOAD) // PASSES)
-            if live(u - LAG_QUANTISE):
-                round_and_group(*divmod(u - LAG_QUANTISE, PASSES))
-            if starts_chunk(u - LAG_INVERSE):
-                inverse((u - LAG_INVERSE) // PASSES)
-            if starts_chunk(u - LAG_FACTORS):
-                factors((u - LAG_FACTORS) // PASSES)
-            if starts_chunk(u - LAG_COEFFICIENTS):
-                coefficients((u - LAG_COEFFICIENTS) // PASSES)
-            if live(u):
-                add_over_o(*divmod(u, PASSES))
-            if starts_chunk(u - LAG_COEFFICIENTS):
-                to_tokens((u - LAG_COEFFICIENTS) // PASSES)
-            if live(u - LAG_SCALE):
-                scale(*divmod(u - LAG_SCALE, PASSES))
-            if starts_chunk(u - LAG_ROOTS):
-                roots((u - LAG_ROOTS) // PASSES)
-            if starts_chunk(u - LAG_FACTORS):
-                corrections((u - LAG_FACTORS) // PASSES)
-            if live(u + LEAD_PRODUCTS):
-                products(*divmod(u + LEAD_PRODUCTS, PASSES))
-            if live(u - LAG_MULTIPLY):
-                multiply(*divmod(u - LAG_MULTIPLY, PASSES))
-            if live(u - LAG_STORE) and (u - LAG_STORE) % W_PASSES == W_PASSES - 1:
-                store((u - LAG_STORE) // W_PASSES)
-            if live(u - LAG_TRANSPOSE):
-                transpose_add(*divmod(u - LAG_TRANSPOSE, PASSES))
-            if live(u - LAG_QUANTISE):
-                quantise(*divmod(u - LAG_QUANTISE, PASSES))
-            if starts_chunk(u - LAG_W_QUANTISE) and (u - LAG_W_QUANTISE) // PASSES < W_PASSES:
-                quantise_weights((u - LAG_W_QUANTISE) // PASSES)
-            if 0 <= u - LAG_W_REGROUP < W_PASSES * PASSES:
-                regroup_weights(*divmod(u - LAG_W_REGROUP, PASSES))
+        for step in range(-LEAD_LOAD, N_CHUNKS + LAG_MULTIPLY):
+            if live(step + LEAD_LOAD):
+                load_chunk(step + LEAD_LOAD)
+            if 0 <= step + LEAD_W_LOAD < W_PASSES:
+                load_weights(step + LEAD_W_LOAD)
+            if live(step + LEAD_PRODUCTS):
+                products(step + LEAD_PRODUCTS)
+            if live(step - LAG_SCALE):
+                scale(step - LAG_SCALE, 0)
+            if live(step - LAG_COEFFICIENTS):
+                inverse(step - LAG_COEFFICIENTS)
+                factors(step - LAG_COEFFICIENTS)
+            if live(step - LAG_SCALE):
+                scale(step - LAG_SCALE, 1)
+            if live(step):
+                add_over_o(step)
+            if 0 <= step < W_PASSES:
+                regroup_weights(step, 0)
+            if live(step):
+                roots(step)
+            if live(step - LAG_COEFFICIENTS):
+                corrections(step - LAG_COEFFICIENTS)
+                coefficients(step - LAG_COEFFICIENTS)
+            if live(step - LAG_QUANTISE):
+                quantise(step - LAG_QUANTISE)
+            if 0 <= step - LAG_W_QUANTISE < W_PASSES:
+                quantise_weights(step - LAG_W_QUANTISE)
+            if 0 <= step < W_PASSES:
+                regroup_weights(step, 1)
+            if live(step - LAG_MULTIPLY):
+                multiply(step - LAG_MULTIPLY)
+            for c in range(PASSES):
+                if c == PASSES // 2 and live(step - LAG_COEFFICIENTS):
+                    to_tokens(step - LAG_COEFFICIENTS)
+                if live(step - LAG_TRANSPOSE):
+                    transpose_add(step - LAG_TRANSPOSE, c)

@@ -179,15 +179,11 @@ def tile_capsulenetwork_pb_v_kernel(tc, p, Wr, s, grad_out, out):
             tiles["hc", n] = hc
 
         def scale(n, which):
-            scaled_to = scaled.tile([P, PASSES, PACK, P], F32, name=("hg", "ct")[which])
+            scaled_to = scaled.tile([P, CAPS_CHUNK, OUT_DIM], F32, name=("hg", "ct")[which])
             nc.vector.tensor_tensor(
-                out=scaled_to[:].rearrange("b c t (pj pq) -> b c pj pq t", pq=QUADS),
-                in0=tiles[("g", "t")[which], n][:].rearrange("b (c pj pq t) -> b c pj pq t", c=PASSES, pq=QUADS, t=PACK),
-                in1=tiles["hc", n][:, which, :]
-                .rearrange("b (c pj) -> b c pj", c=PASSES)
-                .unsqueeze(3)
-                .unsqueeze(4)
-                .to_broadcast([P, PASSES, CAPS_PASS, QUADS, PACK]),
+                out=scaled_to[:],
+                in0=tiles[("g", "t")[which], n][:].rearrange("b (j o) -> b j o", o=OUT_DIM),
+                in1=tiles["hc", n][:, which, :].unsqueeze(2).to_broadcast([P, CAPS_CHUNK, OUT_DIM]),
                 op=ALU.mult,
             )
             tiles[("hg", "ct")[which], n] = scaled_to
@@ -195,14 +191,14 @@ def tile_capsulenetwork_pb_v_kernel(tc, p, Wr, s, grad_out, out):
         def transpose_add(n, c):
             ds_t = psum_ds.tile([P, PACK, P], F32, name="ds_t")
             for t in range(PACK):
-                nc.tensor.matmul(
-                    out=ds_t[:, t, :], lhsT=tiles["hg", n][:, c, t, :], rhs=ident[:],
-                    start=True, stop=False, is_transpose=True,
-                )
-                nc.tensor.matmul(
-                    out=ds_t[:, t, :], lhsT=tiles["ct", n][:, c, t, :], rhs=ident[:],
-                    start=False, stop=True, is_transpose=True,
-                )
+                for which, name in enumerate(("hg", "ct")):
+                    by_t = tiles[name, n][:].rearrange("b j o -> b (j o)").rearrange(
+                        "b (c q t) -> b c t q", c=PASSES, t=PACK
+                    )
+                    nc.tensor.matmul(
+                        out=ds_t[:, t, :], lhsT=by_t[:, c, t, :], rhs=ident[:],
+                        start=(which == 0), stop=(which == 1), is_transpose=True,
+                    )
             if c == 0:
                 grouped = rounded.tile([P, PASSES, P, PACK], BF16, name="grouped", align_bytes=64)
                 tiles["grouped", n] = grouped

@@ -115,20 +115,21 @@ def tile_capsulenetwork_pb_v_kernel(tc, p, Wr, s, grad_out, out):
             )
 
         def products(n):
-            tt = prods.tile([P, COLS], F32, name="tt")
-            nc.scalar.activation(out=tt[:], in_=tiles["t", n][:], func=ACT.Square)
-            tg = prods.tile([P, COLS], F32, name="tg")
-            nc.gpsimd.tensor_tensor(out=tg[:], in0=tiles["t", n][:], in1=tiles["g", n][:], op=ALU.mult)
+            tt = prods.tile([P, QUADS, CAPS_CHUNK, PACK], F32, name="tt")
+            tg = prods.tile([P, QUADS, CAPS_CHUNK, PACK], F32, name="tg")
+            t_v = tiles["t", n][:].rearrange("b (j oh ol) -> b j oh ol", oh=QUADS, ol=PACK)
+            g_v = tiles["g", n][:].rearrange("b (j oh ol) -> b j oh ol", oh=QUADS, ol=PACK)
+            nc.scalar.activation(out=tt[:].rearrange("b oh j ol -> b j oh ol"), in_=t_v, func=ACT.Square)
+            nc.gpsimd.tensor_tensor(out=tg[:].rearrange("b oh j ol -> b j oh ol"), in0=t_v, in1=g_v, op=ALU.mult)
             tiles["tt", n] = tt
             tiles["tg", n] = tg
 
         def add_over_o(n):
             sums = psum_sums.tile([P, 2, P], F32, name="sums")
             for which, prod in enumerate((tiles["tt", n], tiles["tg", n])):
-                by_o = prod[:].rearrange("b (j o) -> b o j", o=OUT_DIM)
                 for o in range(OUT_DIM):
                     nc.tensor.matmul(
-                        out=sums[:, which, :], lhsT=by_o[:, o, :], rhs=ident[:],
+                        out=sums[:, which, :], lhsT=prod[:, o // PACK, :, o % PACK], rhs=ident[:],
                         start=(o == 0), stop=(o == OUT_DIM - 1), is_transpose=True,
                     )
             tiles["sums", n] = sums
@@ -179,11 +180,15 @@ def tile_capsulenetwork_pb_v_kernel(tc, p, Wr, s, grad_out, out):
             tiles["hc", n] = hc
 
         def scale(n, which):
-            scaled_to = scaled.tile([P, CAPS_CHUNK, OUT_DIM], F32, name=("hg", "ct")[which])
+            scaled_to = scaled.tile([P, PASSES, PACK, P], F32, name=("hg", "ct")[which])
             nc.vector.tensor_tensor(
-                out=scaled_to[:],
-                in0=tiles[("g", "t")[which], n][:].rearrange("b (j o) -> b j o", o=OUT_DIM),
-                in1=tiles["hc", n][:, which, :].unsqueeze(2).to_broadcast([P, CAPS_CHUNK, OUT_DIM]),
+                out=scaled_to[:].rearrange("b c t (pj pq) -> b c pj pq t", pq=QUADS),
+                in0=tiles[("g", "t")[which], n][:].rearrange("b (c pj pq t) -> b c pj pq t", c=PASSES, pq=QUADS, t=PACK),
+                in1=tiles["hc", n][:, which, :]
+                .rearrange("b (c pj) -> b c pj", c=PASSES)
+                .unsqueeze(3)
+                .unsqueeze(4)
+                .to_broadcast([P, PASSES, CAPS_PASS, QUADS, PACK]),
                 op=ALU.mult,
             )
             tiles[("hg", "ct")[which], n] = scaled_to
@@ -191,14 +196,14 @@ def tile_capsulenetwork_pb_v_kernel(tc, p, Wr, s, grad_out, out):
         def transpose_add(n, c):
             ds_t = psum_ds.tile([P, PACK, P], F32, name="ds_t")
             for t in range(PACK):
-                for which, name in enumerate(("hg", "ct")):
-                    by_t = tiles[name, n][:].rearrange("b j o -> b (j o)").rearrange(
-                        "b (c q t) -> b c t q", c=PASSES, t=PACK
-                    )
-                    nc.tensor.matmul(
-                        out=ds_t[:, t, :], lhsT=by_t[:, c, t, :], rhs=ident[:],
-                        start=(which == 0), stop=(which == 1), is_transpose=True,
-                    )
+                nc.tensor.matmul(
+                    out=ds_t[:, t, :], lhsT=tiles["hg", n][:, c, t, :], rhs=ident[:],
+                    start=True, stop=False, is_transpose=True,
+                )
+                nc.tensor.matmul(
+                    out=ds_t[:, t, :], lhsT=tiles["ct", n][:, c, t, :], rhs=ident[:],
+                    start=False, stop=True, is_transpose=True,
+                )
             if c == 0:
                 grouped = rounded.tile([P, PASSES, P, PACK], BF16, name="grouped", align_bytes=64)
                 tiles["grouped", n] = grouped

@@ -33,17 +33,17 @@ W_PASSES = CAPS * OUT_DIM // K_PASS
 CAPS_PASS = K_PASS // OUT_DIM
 QUADS = OUT_DIM // PACK
 
-W_HALF = N_PRIM // 2
+W_STEP = 2
 
-LEAD_LOAD = 3
-LEAD_W_LOAD = 2
+LEAD_LOAD = 2
 LEAD_PRODUCTS = 1
 LAG_COEFFICIENTS = 1
 LAG_SCALE = 2
 LAG_TRANSPOSE = 3
 LAG_QUANTISE = 4
+LAG_MULTIPLY = 5
+LEAD_W_LOAD = 1
 LAG_W_QUANTISE = 1
-LAG_MULTIPLY = 7
 
 FLOPS = 2 * BATCH * CAPS * OUT_DIM * NI
 BYTES = BATCH * CAPS * OUT_DIM * (4 + 2) + NI * CAPS * OUT_DIM * 2 + BATCH * NI * 4
@@ -53,10 +53,11 @@ def tile_capsulenetwork_pb_v_kernel(tc, p, Wr, s, grad_out, out):
     nc = tc.nc
     with ExitStack() as stack:
         const = stack.enter_context(tc.tile_pool(name="const", bufs=1))
-        w_raw = stack.enter_context(tc.tile_pool(name="w_raw", bufs=3))
-        w_stage = stack.enter_context(tc.tile_pool(name="w_stage", bufs=2))
-        loads = stack.enter_context(tc.tile_pool(name="loads", bufs=6))
+        w_raw = stack.enter_context(tc.tile_pool(name="w_raw", bufs=2 * W_STEP))
+        w_stage = stack.enter_context(tc.tile_pool(name="w_stage", bufs=2 * W_STEP))
+        loads = stack.enter_context(tc.tile_pool(name="loads", bufs=5))
         prods = stack.enter_context(tc.tile_pool(name="prods", bufs=2))
+        scratch = stack.enter_context(tc.tile_pool(name="scratch", bufs=1))
         small = stack.enter_context(tc.tile_pool(name="small", bufs=2))
         scaled = stack.enter_context(tc.tile_pool(name="scaled", bufs=2))
         rounded = stack.enter_context(tc.tile_pool(name="rounded", bufs=2))
@@ -97,15 +98,10 @@ def tile_capsulenetwork_pb_v_kernel(tc, p, Wr, s, grad_out, out):
             nc.sync.dma_start(out=raw[:], in_=w_view[c])
             tiles["raw", c] = raw
 
-        def regroup_weights(c, x):
-            if x == 0:
-                w_grouped = w_stage.tile([P, N_PRIM, IN_DIM, PACK], BF16, name="w_grouped", align_bytes=64)
-                tiles["w_grouped", c] = w_grouped
-            part = slice(x * W_HALF, (x + 1) * W_HALF)
-            nc.scalar.copy(
-                out=tiles["w_grouped", c][:, part],
-                in_=tiles["raw", c][:, part].rearrange("q n (t i) -> q n i t", t=PACK),
-            )
+        def regroup_weights(c):
+            w_grouped = w_stage.tile([P, N_PRIM, IN_DIM, PACK], BF16, name="w_grouped", align_bytes=64)
+            nc.scalar.copy(out=w_grouped[:], in_=tiles["raw", c][:].rearrange("q n (t i) -> q n i t", t=PACK))
+            tiles["w_grouped", c] = w_grouped
 
         def quantise_weights(c):
             nc.vector.quantize_mx(
@@ -114,23 +110,35 @@ def tile_capsulenetwork_pb_v_kernel(tc, p, Wr, s, grad_out, out):
                 in_=tiles["w_grouped", c][:].rearrange("q n i t -> q (n i t)"),
             )
 
+        def halves_added(engine, pool, name, src, width):
+            dst = pool.tile([P, CAPS_CHUNK, width // 2], F32, name=name)
+            engine.tensor_tensor(out=dst[:], in0=src[:, :, : width // 2], in1=src[:, :, width // 2 :], op=ALU.add)
+            return dst
+
         def products(n):
-            tt = prods.tile([P, QUADS, CAPS_CHUNK, PACK], F32, name="tt")
-            tg = prods.tile([P, QUADS, CAPS_CHUNK, PACK], F32, name="tg")
-            t_v = tiles["t", n][:].rearrange("b (j oh ol) -> b j oh ol", oh=QUADS, ol=PACK)
-            g_v = tiles["g", n][:].rearrange("b (j oh ol) -> b j oh ol", oh=QUADS, ol=PACK)
-            nc.scalar.activation(out=tt[:].rearrange("b oh j ol -> b j oh ol"), in_=t_v, func=ACT.Square)
-            nc.gpsimd.tensor_tensor(out=tg[:].rearrange("b oh j ol -> b j oh ol"), in0=t_v, in1=g_v, op=ALU.mult)
+            tt = prods.tile([P, CAPS_CHUNK, OUT_DIM], F32, name="tt")
+            nc.scalar.activation(
+                out=tt[:].rearrange("b j o -> b (j o)"), in_=tiles["t", n][:], func=ACT.Square
+            )
+            tg = scratch.tile([P, CAPS_CHUNK, OUT_DIM], F32, name="tg")
+            nc.gpsimd.tensor_tensor(
+                out=tg[:].rearrange("b j o -> b (j o)"), in0=tiles["t", n][:], in1=tiles["g", n][:], op=ALU.mult
+            )
+            tg8 = halves_added(nc.gpsimd, scratch, "tg8", tg, OUT_DIM)
             tiles["tt", n] = tt
-            tiles["tg", n] = tg
+            tiles["tg4", n] = halves_added(nc.gpsimd, prods, "tg4", tg8, OUT_DIM // 2)
+
+        def halve_squares(n):
+            tiles["tt8", n] = halves_added(nc.vector, prods, "tt8", tiles["tt", n], OUT_DIM)
 
         def add_over_o(n):
             sums = psum_sums.tile([P, 2, P], F32, name="sums")
-            for which, prod in enumerate((tiles["tt", n], tiles["tg", n])):
-                for o in range(OUT_DIM):
+            for which, part in enumerate((tiles["tt8", n], tiles["tg4", n])):
+                width = part.shape[2]
+                for o in range(width):
                     nc.tensor.matmul(
-                        out=sums[:, which, :], lhsT=prod[:, o // PACK, :, o % PACK], rhs=ident[:],
-                        start=(o == 0), stop=(o == OUT_DIM - 1), is_transpose=True,
+                        out=sums[:, which, :], lhsT=part[:, :, o], rhs=ident[:],
+                        start=(o == 0), stop=(o == width - 1), is_transpose=True,
                     )
             tiles["sums", n] = sums
 
@@ -141,12 +149,15 @@ def tile_capsulenetwork_pb_v_kernel(tc, p, Wr, s, grad_out, out):
             nc.scalar.activation(out=root_q1[:, 1, :], in_=q, func=ACT.Identity, bias=one_col[:])
             tiles["root_q1", n] = root_q1
 
-        def inverse(n):
+        def denominator(n):
             root_q1 = tiles["root_q1", n]
             den = small.tile([P, P], F32, name="den")
             nc.vector.tensor_tensor(out=den[:], in0=root_q1[:, 0, :], in1=root_q1[:, 1, :], op=ALU.mult)
+            tiles["den", n] = den
+
+        def invert(n):
             rw = small.tile([P, P], F32, name="rw")
-            nc.vector.reciprocal(out=rw[:], in_=den[:])
+            nc.vector.reciprocal(out=rw[:], in_=tiles["den", n][:])
             tiles["rw", n] = rw
 
         def factors(n):
@@ -167,11 +178,14 @@ def tile_capsulenetwork_pb_v_kernel(tc, p, Wr, s, grad_out, out):
             tiles["w2m1", n] = w2m1
             tiles["eps_rr", n] = eps_rr
 
-        def coefficients(n):
+        def bracket(n):
             z = small.tile([P, P], F32, name="z")
             nc.vector.tensor_tensor(out=z[:], in0=tiles["w2m1", n][:], in1=tiles["eps_rr", n][:], op=ALU.add)
+            tiles["z", n] = z
+
+        def coefficient(n):
             coef = tiles["h_c", n][:, 1, :]
-            nc.vector.tensor_tensor(out=coef, in0=z[:], in1=coef, op=ALU.mult)
+            nc.vector.tensor_tensor(out=coef, in0=tiles["z", n][:], in1=coef, op=ALU.mult)
 
         def to_tokens(n):
             hc = psum_hc.tile([P, 2, P], F32, name="hc")
@@ -179,19 +193,24 @@ def tile_capsulenetwork_pb_v_kernel(tc, p, Wr, s, grad_out, out):
                 nc.tensor.transpose(out=hc[:, which, :], in_=tiles["h_c", n][:, which, :], identity=ident[:])
             tiles["hc", n] = hc
 
-        def scale(n, which):
-            scaled_to = scaled.tile([P, PASSES, PACK, P], F32, name=("hg", "ct")[which])
+        def scale(n, which, half):
+            name = ("hg", "ct")[which]
+            if half == 0:
+                scaled_to = scaled.tile([P, PASSES, PACK, P], F32, name=name)
+                tiles[name, n] = scaled_to
+            some = slice(half * PASSES // 2, (half + 1) * PASSES // 2)
             nc.vector.tensor_tensor(
-                out=scaled_to[:].rearrange("b c t (pj pq) -> b c pj pq t", pq=QUADS),
-                in0=tiles[("g", "t")[which], n][:].rearrange("b (c pj pq t) -> b c pj pq t", c=PASSES, pq=QUADS, t=PACK),
+                out=tiles[name, n][:, some].rearrange("b c t (pj pq) -> b c pj pq t", pq=QUADS),
+                in0=tiles[("g", "t")[which], n][:].rearrange(
+                    "b (c pj pq t) -> b c pj pq t", c=PASSES, pq=QUADS, t=PACK
+                )[:, some],
                 in1=tiles["hc", n][:, which, :]
-                .rearrange("b (c pj) -> b c pj", c=PASSES)
+                .rearrange("b (c pj) -> b c pj", c=PASSES)[:, some]
                 .unsqueeze(3)
                 .unsqueeze(4)
-                .to_broadcast([P, PASSES, CAPS_PASS, QUADS, PACK]),
+                .to_broadcast([P, PASSES // 2, CAPS_PASS, QUADS, PACK]),
                 op=ALU.mult,
             )
-            tiles[("hg", "ct")[which], n] = scaled_to
 
         def transpose_add(n, c):
             ds_t = psum_ds.tile([P, PACK, P], F32, name="ds_t")
@@ -243,39 +262,51 @@ def tile_capsulenetwork_pb_v_kernel(tc, p, Wr, s, grad_out, out):
         def live(n):
             return 0 <= n < N_CHUNKS
 
+        def weights_of(step):
+            return [c for c in range(step * W_STEP, (step + 1) * W_STEP) if 0 <= c < W_PASSES]
+
         for step in range(-LEAD_LOAD, N_CHUNKS + LAG_MULTIPLY):
+            new, old = step - LAG_COEFFICIENTS, step - LAG_SCALE
             if live(step + LEAD_LOAD):
                 load_chunk(step + LEAD_LOAD)
-            if 0 <= step + LEAD_W_LOAD < W_PASSES:
-                load_weights(step + LEAD_W_LOAD)
+            for c in weights_of(step + LEAD_W_LOAD):
+                load_weights(c)
             if live(step + LEAD_PRODUCTS):
                 products(step + LEAD_PRODUCTS)
-            if live(step - LAG_SCALE):
-                scale(step - LAG_SCALE, 0)
-            if live(step - LAG_COEFFICIENTS):
-                inverse(step - LAG_COEFFICIENTS)
-                factors(step - LAG_COEFFICIENTS)
-            if live(step - LAG_SCALE):
-                scale(step - LAG_SCALE, 1)
+            if live(new):
+                denominator(new)
+            if live(old):
+                scale(old, 0, 0)
+            if live(new):
+                invert(new)
+            if live(old):
+                scale(old, 0, 1)
+            if live(new):
+                factors(new)
+            if live(old):
+                scale(old, 1, 0)
             if live(step):
                 add_over_o(step)
-            if 0 <= step < W_PASSES:
-                regroup_weights(step, 0)
-            if live(step):
                 roots(step)
-            if live(step - LAG_COEFFICIENTS):
-                corrections(step - LAG_COEFFICIENTS)
-                coefficients(step - LAG_COEFFICIENTS)
+            if live(new):
+                corrections(new)
+                bracket(new)
+            if live(old):
+                scale(old, 1, 1)
+            if live(new):
+                coefficient(new)
             if live(step - LAG_QUANTISE):
                 quantise(step - LAG_QUANTISE)
-            if 0 <= step - LAG_W_QUANTISE < W_PASSES:
-                quantise_weights(step - LAG_W_QUANTISE)
-            if 0 <= step < W_PASSES:
-                regroup_weights(step, 1)
+            for c in weights_of(step - LAG_W_QUANTISE):
+                quantise_weights(c)
+            if live(step + LEAD_PRODUCTS):
+                halve_squares(step + LEAD_PRODUCTS)
+            for c in weights_of(step):
+                regroup_weights(c)
             if live(step - LAG_MULTIPLY):
                 multiply(step - LAG_MULTIPLY)
             for c in range(PASSES):
-                if c == PASSES // 2 and live(step - LAG_COEFFICIENTS):
-                    to_tokens(step - LAG_COEFFICIENTS)
+                if c == PASSES - 1 and live(new):
+                    to_tokens(new)
                 if live(step - LAG_TRANSPOSE):
                     transpose_add(step - LAG_TRANSPOSE, c)

@@ -39,9 +39,9 @@ LEAD_LOAD = 2
 LEAD_PRODUCTS = 1
 LAG_COEFFICIENTS = 1
 LAG_SCALE = 2
-LAG_TRANSPOSE = 3
-LAG_QUANTISE = 4
-LAG_MULTIPLY = 5
+LAG_TRANSPOSE = 2
+LAG_QUANTISE = 3
+LAG_MULTIPLY = 4
 LEAD_W_LOAD = 1
 LAG_W_QUANTISE = 1
 
@@ -273,6 +273,9 @@ def tile_capsulenetwork_pb_v_kernel(tc, p, Wr, s, grad_out, out):
                 load_weights(c)
             if live(step + LEAD_PRODUCTS):
                 products(step + LEAD_PRODUCTS)
+            if live(step - LAG_TRANSPOSE - 1):
+                for c in range(PASSES // 2, PASSES):
+                    transpose_add(step - LAG_TRANSPOSE - 1, c)
             if live(new):
                 denominator(new)
             if live(old):
@@ -280,17 +283,18 @@ def tile_capsulenetwork_pb_v_kernel(tc, p, Wr, s, grad_out, out):
             if live(new):
                 invert(new)
             if live(old):
-                scale(old, 0, 1)
+                scale(old, 1, 0)
             if live(new):
                 factors(new)
             if live(old):
-                scale(old, 1, 0)
+                scale(old, 0, 1)
             if live(step):
                 add_over_o(step)
-                roots(step)
             if live(new):
                 corrections(new)
                 bracket(new)
+            if live(step):
+                roots(step)
             if live(old):
                 scale(old, 1, 1)
             if live(new):
@@ -305,8 +309,8 @@ def tile_capsulenetwork_pb_v_kernel(tc, p, Wr, s, grad_out, out):
                 regroup_weights(c)
             if live(step - LAG_MULTIPLY):
                 multiply(step - LAG_MULTIPLY)
-            for c in range(PASSES):
-                if c == PASSES - 1 and live(new):
-                    to_tokens(new)
-                if live(step - LAG_TRANSPOSE):
+            if live(step - LAG_TRANSPOSE):
+                for c in range(PASSES // 2):
                     transpose_add(step - LAG_TRANSPOSE, c)
+            if live(new):
+                to_tokens(new)

@@ -32,7 +32,6 @@ N_CHUNKS = (BATCH // P) * HALVES
 W_PASSES = CAPS * OUT_DIM // K_PASS
 CAPS_PASS = K_PASS // OUT_DIM
 QUADS = OUT_DIM // PACK
-
 W_STEP = 2
 
 LEAD_LOAD = 2
@@ -52,21 +51,28 @@ BYTES = BATCH * CAPS * OUT_DIM * (4 + 2) + NI * CAPS * OUT_DIM * 2 + BATCH * NI 
 def tile_capsulenetwork_pb_v_kernel(tc, p, Wr, s, grad_out, out):
     nc = tc.nc
     with ExitStack() as stack:
-        const = stack.enter_context(tc.tile_pool(name="const", bufs=1))
-        w_raw = stack.enter_context(tc.tile_pool(name="w_raw", bufs=2 * W_STEP))
-        w_stage = stack.enter_context(tc.tile_pool(name="w_stage", bufs=2 * W_STEP))
-        loads = stack.enter_context(tc.tile_pool(name="loads", bufs=5))
-        prods = stack.enter_context(tc.tile_pool(name="prods", bufs=2))
-        scratch = stack.enter_context(tc.tile_pool(name="scratch", bufs=1))
-        small = stack.enter_context(tc.tile_pool(name="small", bufs=2))
-        scaled = stack.enter_context(tc.tile_pool(name="scaled", bufs=2))
-        rounded = stack.enter_context(tc.tile_pool(name="rounded", bufs=2))
-        coded = stack.enter_context(tc.tile_pool(name="coded", bufs=LAG_MULTIPLY - LAG_QUANTISE + 1))
-        results = stack.enter_context(tc.tile_pool(name="results", bufs=2))
-        psum_sums = stack.enter_context(tc.psum_pool(name="psum_sums", bufs=2))
-        psum_hc = stack.enter_context(tc.psum_pool(name="psum_hc", bufs=1))
-        psum_ds = stack.enter_context(tc.psum_pool(name="psum_ds", bufs=PASSES))
-        psum_acc = stack.enter_context(tc.psum_pool(name="psum_acc", bufs=1))
+
+        def sbuf(name, bufs):
+            return stack.enter_context(tc.tile_pool(name=name, bufs=bufs))
+
+        def psum(name, bufs):
+            return stack.enter_context(tc.psum_pool(name=name, bufs=bufs))
+
+        const = sbuf("const", 1)
+        w_raw = sbuf("w_raw", 2 * W_STEP)
+        w_stage = sbuf("w_stage", 2 * W_STEP)
+        loads = sbuf("loads", LEAD_LOAD + LAG_SCALE + 1)
+        prods = sbuf("prods", 2)
+        scratch = sbuf("scratch", 1)
+        small = sbuf("small", 2)
+        scaled = sbuf("scaled", 2)
+        rounded = sbuf("rounded", 2)
+        coded = sbuf("coded", LAG_MULTIPLY - LAG_QUANTISE + 1)
+        results = sbuf("results", 2)
+        psum_sums = psum("psum_sums", 2)
+        psum_factors = psum("psum_factors", 1)
+        psum_ds = psum("psum_ds", PASSES)
+        psum_acc = psum("psum_acc", 1)
         stack.enter_context(tc.manual_schedule())
 
         ident = const.tile([P, P], F32, name="ident")
@@ -79,35 +85,40 @@ def tile_capsulenetwork_pb_v_kernel(tc, p, Wr, s, grad_out, out):
         nc.vector.memset(minus_one_col[:], -1.0)
         w_codes = const.tile([P, W_PASSES, NI], U32, name="w_codes", align_bytes=64)
         w_scales = const.tile([P, W_PASSES, NI], U8, name="w_scales", align_bytes=64)
-        w_view = Wr.rearrange("n (c pj) (pq t) i -> c (pj pq) n (t i)", c=W_PASSES, pq=QUADS)
+        w_view = Wr.rearrange(
+            "n (wp j) (quad slot) i -> wp (j quad) n (slot i)", wp=W_PASSES, quad=QUADS
+        )
 
         tiles = {}
 
         def load_chunk(n):
-            rows = slice((n // HALVES) * P, (n // HALVES + 1) * P)
+            tokens = slice((n // HALVES) * P, (n // HALVES + 1) * P)
             caps = slice((n % HALVES) * CAPS_CHUNK, (n % HALVES + 1) * CAPS_CHUNK)
             t_sb = loads.tile([P, COLS], F32, name="t_sb")
-            nc.sync.dma_start(out=t_sb[:], in_=s[rows, caps, :].rearrange("b j o -> b (j o)"))
+            nc.sync.dma_start(out=t_sb[:], in_=s[tokens, caps, :].rearrange("b j o -> b (j o)"))
             g_sb = loads.tile([P, COLS], BF16, name="g_sb")
-            nc.sync.dma_start(out=g_sb[:], in_=grad_out[rows, caps, :].rearrange("b j o -> b (j o)"))
+            nc.sync.dma_start(out=g_sb[:], in_=grad_out[tokens, caps, :].rearrange("b j o -> b (j o)"))
             tiles["t", n] = t_sb
             tiles["g", n] = g_sb
 
-        def load_weights(c):
-            raw = w_raw.tile([P, N_PRIM, PACK * IN_DIM], BF16, name="raw")
-            nc.sync.dma_start(out=raw[:], in_=w_view[c])
-            tiles["raw", c] = raw
+        def load_weights(wp):
+            w_loaded = w_raw.tile([P, N_PRIM, PACK * IN_DIM], BF16, name="w_loaded")
+            nc.sync.dma_start(out=w_loaded[:], in_=w_view[wp])
+            tiles["w_loaded", wp] = w_loaded
 
-        def regroup_weights(c):
+        def regroup_weights(wp):
             w_grouped = w_stage.tile([P, N_PRIM, IN_DIM, PACK], BF16, name="w_grouped", align_bytes=64)
-            nc.scalar.copy(out=w_grouped[:], in_=tiles["raw", c][:].rearrange("q n (t i) -> q n i t", t=PACK))
-            tiles["w_grouped", c] = w_grouped
+            nc.scalar.copy(
+                out=w_grouped[:],
+                in_=tiles["w_loaded", wp][:].rearrange("row n (slot i) -> row n i slot", slot=PACK),
+            )
+            tiles["w_grouped", wp] = w_grouped
 
-        def quantise_weights(c):
+        def quantise_weights(wp):
             nc.vector.quantize_mx(
-                out=w_codes[:, c, :].bitcast(E4M3_X4),
-                scales=w_scales[:, c, :],
-                in_=tiles["w_grouped", c][:].rearrange("q n i t -> q (n i t)"),
+                out=w_codes[:, wp, :].bitcast(E4M3_X4),
+                scales=w_scales[:, wp, :],
+                in_=tiles["w_grouped", wp][:].rearrange("row n i slot -> row (n i slot)"),
             )
 
         def halves_added(engine, pool, name, src, width):
@@ -156,56 +167,60 @@ def tile_capsulenetwork_pb_v_kernel(tc, p, Wr, s, grad_out, out):
             tiles["den", n] = den
 
         def invert(n):
-            rw = small.tile([P, P], F32, name="rw")
-            nc.vector.reciprocal(out=rw[:], in_=tiles["den", n][:])
-            tiles["rw", n] = rw
+            ru = small.tile([P, P], F32, name="ru")
+            nc.vector.reciprocal(out=ru[:], in_=tiles["den", n][:])
+            tiles["ru", n] = ru
 
         def factors(n):
-            twice = tiles["rw", n][:].unsqueeze(1).to_broadcast([P, 2, P])
-            w_r = small.tile([P, 2, P], F32, name="w_r")
-            nc.vector.tensor_tensor(out=w_r[:], in0=tiles["root_q1", n][:], in1=twice, op=ALU.mult)
-            h_c = small.tile([P, 2, P], F32, name="h_c")
-            nc.vector.tensor_tensor(out=h_c[:], in0=tiles["sums", n][:], in1=twice, op=ALU.mult)
-            tiles["w_r", n] = w_r
-            tiles["h_c", n] = h_c
+            ru_twice = tiles["ru", n][:].unsqueeze(1).to_broadcast([P, 2, P])
+            u_r = small.tile([P, 2, P], F32, name="u_r")
+            nc.vector.tensor_tensor(out=u_r[:], in0=tiles["root_q1", n][:], in1=ru_twice, op=ALU.mult)
+            h_coef = small.tile([P, 2, P], F32, name="h_coef")
+            nc.vector.tensor_tensor(out=h_coef[:], in0=tiles["sums", n][:], in1=ru_twice, op=ALU.mult)
+            tiles["u_r", n] = u_r
+            tiles["h_coef", n] = h_coef
 
         def corrections(n):
-            w_r = tiles["w_r", n]
-            w2m1 = small.tile([P, P], F32, name="w2m1")
-            nc.scalar.activation(out=w2m1[:], in_=w_r[:, 0, :], func=ACT.Identity, scale=2.0, bias=minus_one_col[:])
+            u_r = tiles["u_r", n]
+            two_u_less_1 = small.tile([P, P], F32, name="two_u_less_1")
+            nc.scalar.activation(
+                out=two_u_less_1[:], in_=u_r[:, 0, :], func=ACT.Identity, scale=2.0, bias=minus_one_col[:]
+            )
             eps_rr = small.tile([P, P], F32, name="eps_rr")
-            nc.scalar.activation(out=eps_rr[:], in_=w_r[:, 1, :], func=ACT.Square, scale=SQ_EPS**0.5)
-            tiles["w2m1", n] = w2m1
+            nc.scalar.activation(out=eps_rr[:], in_=u_r[:, 1, :], func=ACT.Square, scale=SQ_EPS**0.5)
+            tiles["two_u_less_1", n] = two_u_less_1
             tiles["eps_rr", n] = eps_rr
 
         def bracket(n):
-            z = small.tile([P, P], F32, name="z")
-            nc.vector.tensor_tensor(out=z[:], in0=tiles["w2m1", n][:], in1=tiles["eps_rr", n][:], op=ALU.add)
-            tiles["z", n] = z
+            in_brackets = small.tile([P, P], F32, name="in_brackets")
+            nc.vector.tensor_tensor(
+                out=in_brackets[:], in0=tiles["two_u_less_1", n][:], in1=tiles["eps_rr", n][:], op=ALU.add
+            )
+            tiles["in_brackets", n] = in_brackets
 
         def coefficient(n):
-            coef = tiles["h_c", n][:, 1, :]
-            nc.vector.tensor_tensor(out=coef, in0=tiles["z", n][:], in1=coef, op=ALU.mult)
+            coef = tiles["h_coef", n][:, 1, :]
+            nc.vector.tensor_tensor(out=coef, in0=tiles["in_brackets", n][:], in1=coef, op=ALU.mult)
 
         def to_tokens(n):
-            hc = psum_hc.tile([P, 2, P], F32, name="hc")
+            by_token = psum_factors.tile([P, 2, P], F32, name="by_token")
             for which in range(2):
-                nc.tensor.transpose(out=hc[:, which, :], in_=tiles["h_c", n][:, which, :], identity=ident[:])
-            tiles["hc", n] = hc
+                nc.tensor.transpose(out=by_token[:, which, :], in_=tiles["h_coef", n][:, which, :], identity=ident[:])
+            tiles["by_token", n] = by_token
 
         def scale(n, which, half):
             name = ("hg", "ct")[which]
             if half == 0:
-                scaled_to = scaled.tile([P, PASSES, PACK, P], F32, name=name)
-                tiles[name, n] = scaled_to
+                planes = scaled.tile([P, PASSES, PACK, P], F32, name=name)
+                tiles[name, n] = planes
             some = slice(half * PASSES // 2, (half + 1) * PASSES // 2)
             nc.vector.tensor_tensor(
-                out=tiles[name, n][:, some].rearrange("b c t (pj pq) -> b c pj pq t", pq=QUADS),
+                out=tiles[name, n][:, some].rearrange("b c slot (j quad) -> b c j quad slot", quad=QUADS),
                 in0=tiles[("g", "t")[which], n][:].rearrange(
-                    "b (c pj pq t) -> b c pj pq t", c=PASSES, pq=QUADS, t=PACK
+                    "b (c j quad slot) -> b c j quad slot", c=PASSES, quad=QUADS, slot=PACK
                 )[:, some],
-                in1=tiles["hc", n][:, which, :]
-                .rearrange("b (c pj) -> b c pj", c=PASSES)[:, some]
+                in1=tiles["by_token", n][:, which, :]
+                .rearrange("b (c j) -> b c j", c=PASSES)[:, some]
                 .unsqueeze(3)
                 .unsqueeze(4)
                 .to_broadcast([P, PASSES // 2, CAPS_PASS, QUADS, PACK]),
@@ -214,27 +229,27 @@ def tile_capsulenetwork_pb_v_kernel(tc, p, Wr, s, grad_out, out):
 
         def transpose_add(n, c):
             ds_t = psum_ds.tile([P, PACK, P], F32, name="ds_t")
-            for t in range(PACK):
+            for slot in range(PACK):
                 nc.tensor.matmul(
-                    out=ds_t[:, t, :], lhsT=tiles["hg", n][:, c, t, :], rhs=ident[:],
+                    out=ds_t[:, slot, :], lhsT=tiles["hg", n][:, c, slot, :], rhs=ident[:],
                     start=True, stop=False, is_transpose=True,
                 )
                 nc.tensor.matmul(
-                    out=ds_t[:, t, :], lhsT=tiles["ct", n][:, c, t, :], rhs=ident[:],
+                    out=ds_t[:, slot, :], lhsT=tiles["ct", n][:, c, slot, :], rhs=ident[:],
                     start=False, stop=True, is_transpose=True,
                 )
             if c == 0:
                 grouped = rounded.tile([P, PASSES, P, PACK], BF16, name="grouped", align_bytes=64)
                 tiles["grouped", n] = grouped
-            nc.scalar.copy(out=tiles["grouped", n][:, c], in_=ds_t[:].rearrange("q t b -> q b t"))
+            nc.scalar.copy(out=tiles["grouped", n][:, c], in_=ds_t[:].rearrange("row slot b -> row b slot"))
 
         def quantise(n):
             codes = coded.tile([P, PASSES, P], U32, name="codes", align_bytes=64)
             scales = coded.tile([P, PASSES, P], U8, name="scales", align_bytes=64)
             nc.vector.quantize_mx(
-                out=codes[:].rearrange("q c b -> q (c b)").bitcast(E5M2_X4),
-                scales=scales[:].rearrange("q c b -> q (c b)"),
-                in_=tiles["grouped", n][:].rearrange("q c b t -> q (c b t)"),
+                out=codes[:].rearrange("row c b -> row (c b)").bitcast(E5M2_X4),
+                scales=scales[:].rearrange("row c b -> row (c b)"),
+                in_=tiles["grouped", n][:].rearrange("row c b slot -> row (c b slot)"),
             )
             tiles["codes", n] = codes
             tiles["scales", n] = scales
@@ -263,14 +278,14 @@ def tile_capsulenetwork_pb_v_kernel(tc, p, Wr, s, grad_out, out):
             return 0 <= n < N_CHUNKS
 
         def weights_of(step):
-            return [c for c in range(step * W_STEP, (step + 1) * W_STEP) if 0 <= c < W_PASSES]
+            return [wp for wp in range(step * W_STEP, (step + 1) * W_STEP) if 0 <= wp < W_PASSES]
 
         for step in range(-LEAD_LOAD, N_CHUNKS + LAG_MULTIPLY):
             new, old = step - LAG_COEFFICIENTS, step - LAG_SCALE
             if live(step + LEAD_LOAD):
                 load_chunk(step + LEAD_LOAD)
-            for c in weights_of(step + LEAD_W_LOAD):
-                load_weights(c)
+            for wp in weights_of(step + LEAD_W_LOAD):
+                load_weights(wp)
             if live(step + LEAD_PRODUCTS):
                 products(step + LEAD_PRODUCTS)
             if live(step - LAG_TRANSPOSE - 1):
@@ -301,12 +316,12 @@ def tile_capsulenetwork_pb_v_kernel(tc, p, Wr, s, grad_out, out):
                 coefficient(new)
             if live(step - LAG_QUANTISE):
                 quantise(step - LAG_QUANTISE)
-            for c in weights_of(step - LAG_W_QUANTISE):
-                quantise_weights(c)
+            for wp in weights_of(step - LAG_W_QUANTISE):
+                quantise_weights(wp)
             if live(step + LEAD_PRODUCTS):
                 halve_squares(step + LEAD_PRODUCTS)
-            for c in weights_of(step):
-                regroup_weights(c)
+            for wp in weights_of(step):
+                regroup_weights(wp)
             if live(step - LAG_MULTIPLY):
                 multiply(step - LAG_MULTIPLY)
             if live(step - LAG_TRANSPOSE):

@@ -27,22 +27,13 @@ SQ_EPS = 1e-8
 CAPS_CHUNK = P
 COLS = CAPS_CHUNK * OUT_DIM
 PASSES = COLS // K_PASS
+HALF = PASSES // 2
 HALVES = CAPS // CAPS_CHUNK
 N_CHUNKS = (BATCH // P) * HALVES
 W_PASSES = CAPS * OUT_DIM // K_PASS
 CAPS_PASS = K_PASS // OUT_DIM
 QUADS = OUT_DIM // PACK
 W_STEP = 2
-
-LEAD_LOAD = 2
-LEAD_PRODUCTS = 1
-LAG_COEFFICIENTS = 1
-LAG_SCALE = 2
-LAG_TRANSPOSE = 2
-LAG_QUANTISE = 3
-LAG_MULTIPLY = 4
-LEAD_W_LOAD = 1
-LAG_W_QUANTISE = 1
 
 FLOPS = 2 * BATCH * CAPS * OUT_DIM * NI
 BYTES = BATCH * CAPS * OUT_DIM * (4 + 2) + NI * CAPS * OUT_DIM * 2 + BATCH * NI * 4
@@ -61,17 +52,18 @@ def tile_capsulenetwork_pb_v_kernel(tc, p, Wr, s, grad_out, out):
         const = sbuf("const", 1)
         w_raw = sbuf("w_raw", 2 * W_STEP)
         w_stage = sbuf("w_stage", 2 * W_STEP)
-        loads = sbuf("loads", LEAD_LOAD + LAG_SCALE + 1)
+        t_pool = sbuf("t_pool", 5)
+        g_pool = sbuf("g_pool", 4)
         prods = sbuf("prods", 2)
-        scratch = sbuf("scratch", 1)
         small = sbuf("small", 2)
         scaled = sbuf("scaled", 2)
         rounded = sbuf("rounded", 2)
-        coded = sbuf("coded", LAG_MULTIPLY - LAG_QUANTISE + 1)
+        coded = sbuf("coded", 2)
         results = sbuf("results", 2)
-        psum_sums = psum("psum_sums", 2)
-        psum_factors = psum("psum_factors", 1)
-        psum_ds = psum("psum_ds", PASSES)
+        psum_q = psum("psum_q", 1)
+        psum_dot = psum("psum_dot", 1)
+        psum_factors = psum("psum_factors", 2)
+        psum_ds = psum("psum_ds", 3)
         psum_acc = psum("psum_acc", 1)
         stack.enter_context(tc.manual_schedule())
 
@@ -91,14 +83,21 @@ def tile_capsulenetwork_pb_v_kernel(tc, p, Wr, s, grad_out, out):
 
         tiles = {}
 
-        def load_chunk(n):
+        def rows_of(n):
             tokens = slice((n // HALVES) * P, (n // HALVES + 1) * P)
             caps = slice((n % HALVES) * CAPS_CHUNK, (n % HALVES + 1) * CAPS_CHUNK)
-            t_sb = loads.tile([P, COLS], F32, name="t_sb")
+            return tokens, caps
+
+        def load_t(n):
+            tokens, caps = rows_of(n)
+            t_sb = t_pool.tile([P, COLS], F32, name="t_sb")
             nc.sync.dma_start(out=t_sb[:], in_=s[tokens, caps, :].rearrange("b j o -> b (j o)"))
-            g_sb = loads.tile([P, COLS], BF16, name="g_sb")
-            nc.sync.dma_start(out=g_sb[:], in_=grad_out[tokens, caps, :].rearrange("b j o -> b (j o)"))
             tiles["t", n] = t_sb
+
+        def load_g(n):
+            tokens, caps = rows_of(n)
+            g_sb = g_pool.tile([P, COLS], BF16, name="g_sb")
+            nc.sync.dma_start(out=g_sb[:], in_=grad_out[tokens, caps, :].rearrange("b j o -> b (j o)"))
             tiles["g", n] = g_sb
 
         def load_weights(wp):
@@ -121,86 +120,109 @@ def tile_capsulenetwork_pb_v_kernel(tc, p, Wr, s, grad_out, out):
                 in_=tiles["w_grouped", wp][:].rearrange("row n i slot -> row (n i slot)"),
             )
 
-        def halves_added(engine, pool, name, src, width):
-            dst = pool.tile([P, CAPS_CHUNK, width // 2], F32, name=name)
-            engine.tensor_tensor(out=dst[:], in0=src[:, :, : width // 2], in1=src[:, :, width // 2 :], op=ALU.add)
-            return dst
-
-        def products(n):
+        def squares(n):
             tt = prods.tile([P, CAPS_CHUNK, OUT_DIM], F32, name="tt")
             nc.scalar.activation(
                 out=tt[:].rearrange("b j o -> b (j o)"), in_=tiles["t", n][:], func=ACT.Square
             )
-            tg = scratch.tile([P, CAPS_CHUNK, OUT_DIM], F32, name="tg")
+            tiles["tt", n] = tt
+
+        def halve_squares(n):
+            tt = tiles["tt", n]
+            tt8 = prods.tile([P, CAPS_CHUNK, OUT_DIM // 2], F32, name="tt8")
+            nc.vector.tensor_tensor(
+                out=tt8[:], in0=tt[:, :, : OUT_DIM // 2], in1=tt[:, :, OUT_DIM // 2 :], op=ALU.add
+            )
+            tiles["tt8", n] = tt8
+
+        def t_times_g(n):
+            tg = prods.tile([P, CAPS_CHUNK, OUT_DIM], F32, name="tg")
             nc.gpsimd.tensor_tensor(
                 out=tg[:].rearrange("b j o -> b (j o)"), in0=tiles["t", n][:], in1=tiles["g", n][:], op=ALU.mult
             )
-            tg8 = halves_added(nc.gpsimd, scratch, "tg8", tg, OUT_DIM)
-            tiles["tt", n] = tt
-            tiles["tg4", n] = halves_added(nc.gpsimd, prods, "tg4", tg8, OUT_DIM // 2)
+            tiles["tg", n] = tg
 
-        def halve_squares(n):
-            tiles["tt8", n] = halves_added(nc.vector, prods, "tt8", tiles["tt", n], OUT_DIM)
+        def sum_squares(n):
+            q_ps = psum_q.tile([P, P], F32, name="q_ps")
+            width = OUT_DIM // 2
+            for o in range(width):
+                nc.tensor.matmul(
+                    out=q_ps[:], lhsT=tiles["tt8", n][:, :, o], rhs=ident[:],
+                    start=(o == 0), stop=(o == width - 1), is_transpose=True,
+                )
+            tiles["q", n] = q_ps
 
-        def add_over_o(n):
-            sums = psum_sums.tile([P, 2, P], F32, name="sums")
-            for which, part in enumerate((tiles["tt8", n], tiles["tg4", n])):
-                width = part.shape[2]
-                for o in range(width):
-                    nc.tensor.matmul(
-                        out=sums[:, which, :], lhsT=part[:, :, o], rhs=ident[:],
-                        start=(o == 0), stop=(o == width - 1), is_transpose=True,
-                    )
-            tiles["sums", n] = sums
+        def sum_products(n, part):
+            if part == 0:
+                dot_ps = psum_dot.tile([P, P], F32, name="dot_ps")
+                tiles["dot", n] = dot_ps
+            for o in range(part * OUT_DIM // 2, (part + 1) * OUT_DIM // 2):
+                nc.tensor.matmul(
+                    out=tiles["dot", n][:], lhsT=tiles["tg", n][:, :, o], rhs=ident[:],
+                    start=(o == 0), stop=(o == OUT_DIM - 1), is_transpose=True,
+                )
 
         def roots(n):
-            root_q1 = small.tile([P, 2, P], F32, name="root_q1")
-            q = tiles["sums", n][:, 0, :]
-            nc.scalar.activation(out=root_q1[:, 0, :], in_=q, func=ACT.Sqrt, bias=eps_col[:])
-            nc.scalar.activation(out=root_q1[:, 1, :], in_=q, func=ACT.Identity, bias=one_col[:])
-            tiles["root_q1", n] = root_q1
+            q = tiles["q", n][:]
+            root = small.tile([P, P], F32, name="root")
+            nc.scalar.activation(out=root[:], in_=q, func=ACT.Sqrt, bias=eps_col[:])
+            den_q1 = small.tile([P, 2, P], F32, name="den_q1")
+            nc.scalar.activation(out=den_q1[:, 1, :], in_=q, func=ACT.Identity, bias=one_col[:])
+            tiles["root", n] = root
+            tiles["den_q1", n] = den_q1
 
         def denominator(n):
-            root_q1 = tiles["root_q1", n]
-            den = small.tile([P, P], F32, name="den")
-            nc.vector.tensor_tensor(out=den[:], in0=root_q1[:, 0, :], in1=root_q1[:, 1, :], op=ALU.mult)
-            tiles["den", n] = den
+            nc.vector.scalar_tensor_tensor(
+                out=tiles["den_q1", n][:, 0, :], in0=tiles["q", n][:], scalar=1.0, in1=tiles["root", n][:],
+                op0=ALU.add, op1=ALU.mult,
+            )
 
         def invert(n):
-            ru = small.tile([P, P], F32, name="ru")
-            nc.vector.reciprocal(out=ru[:], in_=tiles["den", n][:])
-            tiles["ru", n] = ru
+            ru_u = small.tile([P, 2, P], F32, name="ru_u")
+            nc.vector.reciprocal(out=ru_u[:], in_=tiles["den_q1", n][:])
+            tiles["ru_u", n] = ru_u
 
-        def factors(n):
-            ru_twice = tiles["ru", n][:].unsqueeze(1).to_broadcast([P, 2, P])
-            u_r = small.tile([P, 2, P], F32, name="u_r")
-            nc.vector.tensor_tensor(out=u_r[:], in0=tiles["root_q1", n][:], in1=ru_twice, op=ALU.mult)
+        def r_and_h(n):
+            ru = tiles["ru_u", n][:, 0, :]
+            r = small.tile([P, P], F32, name="r")
+            nc.vector.scalar_tensor_tensor(
+                out=r[:], in0=tiles["q", n][:], scalar=1.0, in1=ru, op0=ALU.add, op1=ALU.mult
+            )
             h_coef = small.tile([P, 2, P], F32, name="h_coef")
-            nc.vector.tensor_tensor(out=h_coef[:], in0=tiles["sums", n][:], in1=ru_twice, op=ALU.mult)
-            tiles["u_r", n] = u_r
+            nc.vector.tensor_tensor(out=h_coef[:, 0, :], in0=tiles["q", n][:], in1=ru, op=ALU.mult)
+            tiles["r", n] = r
             tiles["h_coef", n] = h_coef
 
         def corrections(n):
-            u_r = tiles["u_r", n]
             two_u_less_1 = small.tile([P, P], F32, name="two_u_less_1")
             nc.scalar.activation(
-                out=two_u_less_1[:], in_=u_r[:, 0, :], func=ACT.Identity, scale=2.0, bias=minus_one_col[:]
+                out=two_u_less_1[:], in_=tiles["ru_u", n][:, 1, :], func=ACT.Identity, scale=2.0,
+                bias=minus_one_col[:],
             )
             eps_rr = small.tile([P, P], F32, name="eps_rr")
-            nc.scalar.activation(out=eps_rr[:], in_=u_r[:, 1, :], func=ACT.Square, scale=SQ_EPS**0.5)
+            nc.scalar.activation(out=eps_rr[:], in_=tiles["r", n][:], func=ACT.Square, scale=SQ_EPS**0.5)
             tiles["two_u_less_1", n] = two_u_less_1
             tiles["eps_rr", n] = eps_rr
 
         def bracket(n):
             in_brackets = small.tile([P, P], F32, name="in_brackets")
-            nc.vector.tensor_tensor(
+            nc.gpsimd.tensor_tensor(
                 out=in_brackets[:], in0=tiles["two_u_less_1", n][:], in1=tiles["eps_rr", n][:], op=ALU.add
             )
             tiles["in_brackets", n] = in_brackets
 
+        def dot_ru(n):
+            dru = small.tile([P, P], F32, name="dru")
+            nc.vector.tensor_tensor(
+                out=dru[:], in0=tiles["dot", n][:], in1=tiles["ru_u", n][:, 0, :], op=ALU.mult
+            )
+            tiles["dru", n] = dru
+
         def coefficient(n):
-            coef = tiles["h_coef", n][:, 1, :]
-            nc.vector.tensor_tensor(out=coef, in0=tiles["in_brackets", n][:], in1=coef, op=ALU.mult)
+            nc.gpsimd.tensor_tensor(
+                out=tiles["h_coef", n][:, 1, :], in0=tiles["in_brackets", n][:], in1=tiles["dru", n][:],
+                op=ALU.mult,
+            )
 
         def to_tokens(n):
             by_token = psum_factors.tile([P, 2, P], F32, name="by_token")
@@ -210,12 +232,11 @@ def tile_capsulenetwork_pb_v_kernel(tc, p, Wr, s, grad_out, out):
 
         def scale(n, which, half):
             name = ("hg", "ct")[which]
-            if half == 0:
-                planes = scaled.tile([P, PASSES, PACK, P], F32, name=name)
-                tiles[name, n] = planes
-            some = slice(half * PASSES // 2, (half + 1) * PASSES // 2)
+            planes = scaled.tile([P, HALF, PACK, P], F32, name=name)
+            tiles[name, n, half] = planes
+            some = slice(half * HALF, (half + 1) * HALF)
             nc.vector.tensor_tensor(
-                out=tiles[name, n][:, some].rearrange("b c slot (j quad) -> b c j quad slot", quad=QUADS),
+                out=planes[:].rearrange("b c slot (j quad) -> b c j quad slot", quad=QUADS),
                 in0=tiles[("g", "t")[which], n][:].rearrange(
                     "b (c j quad slot) -> b c j quad slot", c=PASSES, quad=QUADS, slot=PACK
                 )[:, some],
@@ -223,19 +244,20 @@ def tile_capsulenetwork_pb_v_kernel(tc, p, Wr, s, grad_out, out):
                 .rearrange("b (c j) -> b c j", c=PASSES)[:, some]
                 .unsqueeze(3)
                 .unsqueeze(4)
-                .to_broadcast([P, PASSES // 2, CAPS_PASS, QUADS, PACK]),
+                .to_broadcast([P, HALF, CAPS_PASS, QUADS, PACK]),
                 op=ALU.mult,
             )
 
         def transpose_add(n, c):
+            half, ch = divmod(c, HALF)
             ds_t = psum_ds.tile([P, PACK, P], F32, name="ds_t")
             for slot in range(PACK):
                 nc.tensor.matmul(
-                    out=ds_t[:, slot, :], lhsT=tiles["hg", n][:, c, slot, :], rhs=ident[:],
+                    out=ds_t[:, slot, :], lhsT=tiles["hg", n, half][:, ch, slot, :], rhs=ident[:],
                     start=True, stop=False, is_transpose=True,
                 )
                 nc.tensor.matmul(
-                    out=ds_t[:, slot, :], lhsT=tiles["ct", n][:, c, slot, :], rhs=ident[:],
+                    out=ds_t[:, slot, :], lhsT=tiles["ct", n, half][:, ch, slot, :], rhs=ident[:],
                     start=False, stop=True, is_transpose=True,
                 )
             if c == 0:
@@ -269,6 +291,9 @@ def tile_capsulenetwork_pb_v_kernel(tc, p, Wr, s, grad_out, out):
                     start=(half == 0 and c == 0),
                     stop=(half == HALVES - 1 and c == PASSES - 1),
                 )
+
+        def store(n):
+            block, half = divmod(n, HALVES)
             if half == HALVES - 1:
                 result = results.tile([P, NI], F32, name="result")
                 nc.scalar.mul(out=result[:], in_=tiles["acc", block][:], mul=1.0 / CAPS)
@@ -280,52 +305,59 @@ def tile_capsulenetwork_pb_v_kernel(tc, p, Wr, s, grad_out, out):
         def weights_of(step):
             return [wp for wp in range(step * W_STEP, (step + 1) * W_STEP) if 0 <= wp < W_PASSES]
 
-        for step in range(-LEAD_LOAD, N_CHUNKS + LAG_MULTIPLY):
-            new, old = step - LAG_COEFFICIENTS, step - LAG_SCALE
-            if live(step + LEAD_LOAD):
-                load_chunk(step + LEAD_LOAD)
-            for wp in weights_of(step + LEAD_W_LOAD):
-                load_weights(wp)
-            if live(step + LEAD_PRODUCTS):
-                products(step + LEAD_PRODUCTS)
-            if live(step - LAG_TRANSPOSE - 1):
-                for c in range(PASSES // 2, PASSES):
-                    transpose_add(step - LAG_TRANSPOSE - 1, c)
-            if live(new):
-                denominator(new)
-            if live(old):
-                scale(old, 0, 0)
-            if live(new):
-                invert(new)
-            if live(old):
-                scale(old, 1, 0)
-            if live(new):
-                factors(new)
-            if live(old):
-                scale(old, 0, 1)
+        for step in range(-3, N_CHUNKS + 3):
+            if live(step + 1):
+                halve_squares(step + 1)
             if live(step):
-                add_over_o(step)
-            if live(new):
-                corrections(new)
-                bracket(new)
-            if live(step):
+                sum_squares(step)
                 roots(step)
-            if live(old):
-                scale(old, 1, 1)
-            if live(new):
-                coefficient(new)
-            if live(step - LAG_QUANTISE):
-                quantise(step - LAG_QUANTISE)
-            for wp in weights_of(step - LAG_W_QUANTISE):
-                quantise_weights(wp)
-            if live(step + LEAD_PRODUCTS):
-                halve_squares(step + LEAD_PRODUCTS)
+            if live(step - 2):
+                transpose_add(step - 2, 0)
+                transpose_add(step - 2, 1)
+            if live(step - 3):
+                quantise(step - 3)
             for wp in weights_of(step):
+                quantise_weights(wp)
+            if live(step - 1):
+                dot_ru(step - 1)
+                coefficient(step - 1)
+            if live(step):
+                denominator(step)
+            if live(step - 3):
+                multiply(step - 3)
+            if live(step - 1):
+                to_tokens(step - 1)
+            if live(step - 2):
+                scale(step - 2, 0, 1)
+            if live(step):
+                invert(step)
+            if live(step - 2):
+                scale(step - 2, 1, 1)
+            if live(step):
+                r_and_h(step)
+            if live(step + 1):
+                t_times_g(step + 1)
+            if live(step + 2):
+                squares(step + 2)
+            if live(step - 3):
+                store(step - 3)
+            if live(step):
+                corrections(step)
+                bracket(step)
+                sum_products(step, 0)
+            if live(step - 2):
+                transpose_add(step - 2, 2)
+                transpose_add(step - 2, 3)
+            if live(step):
+                sum_products(step, 1)
+            if live(step - 1):
+                scale(step - 1, 0, 0)
+                scale(step - 1, 1, 0)
+            for wp in weights_of(step + 1):
                 regroup_weights(wp)
-            if live(step - LAG_MULTIPLY):
-                multiply(step - LAG_MULTIPLY)
-            if live(step - LAG_TRANSPOSE):
-                for c in range(PASSES // 2):
-                    transpose_add(step - LAG_TRANSPOSE, c)
-            if live(new):
-                to_tokens(new)
+            if live(step + 2):
+                load_g(step + 2)
+            if live(step + 3):
+                load_t(step + 3)
+            for wp in weights_of(step + 2):
+                load_weights(wp)

@@ -55,6 +55,7 @@ def tile_capsulenetwork_pb_v_kernel(tc, p, Wr, s, grad_out, out):
         t_pool = sbuf("t_pool", 5)
         g_pool = sbuf("g_pool", 4)
         prods = sbuf("prods", 2)
+        scratch = sbuf("scratch", 1)
         small = sbuf("small", 2)
         scaled = sbuf("scaled", 2)
         rounded = sbuf("rounded", 2)
@@ -136,11 +137,15 @@ def tile_capsulenetwork_pb_v_kernel(tc, p, Wr, s, grad_out, out):
             tiles["tt8", n] = tt8
 
         def t_times_g(n):
-            tg = prods.tile([P, CAPS_CHUNK, OUT_DIM], F32, name="tg")
+            tg = scratch.tile([P, CAPS_CHUNK, OUT_DIM], F32, name="tg")
             nc.gpsimd.tensor_tensor(
                 out=tg[:].rearrange("b j o -> b (j o)"), in0=tiles["t", n][:], in1=tiles["g", n][:], op=ALU.mult
             )
-            tiles["tg", n] = tg
+            tg8 = prods.tile([P, CAPS_CHUNK, OUT_DIM // 2], F32, name="tg8")
+            nc.gpsimd.tensor_tensor(
+                out=tg8[:], in0=tg[:, :, : OUT_DIM // 2], in1=tg[:, :, OUT_DIM // 2 :], op=ALU.add
+            )
+            tiles["tg8", n] = tg8
 
         def sum_squares(n):
             q_ps = psum_q.tile([P, P], F32, name="q_ps")
@@ -156,10 +161,11 @@ def tile_capsulenetwork_pb_v_kernel(tc, p, Wr, s, grad_out, out):
             if part == 0:
                 dot_ps = psum_dot.tile([P, P], F32, name="dot_ps")
                 tiles["dot", n] = dot_ps
-            for o in range(part * OUT_DIM // 2, (part + 1) * OUT_DIM // 2):
+            width = OUT_DIM // 2
+            for o in range(part * width // 2, (part + 1) * width // 2):
                 nc.tensor.matmul(
-                    out=tiles["dot", n][:], lhsT=tiles["tg", n][:, :, o], rhs=ident[:],
-                    start=(o == 0), stop=(o == OUT_DIM - 1), is_transpose=True,
+                    out=tiles["dot", n][:], lhsT=tiles["tg8", n][:, :, o], rhs=ident[:],
+                    start=(o == 0), stop=(o == width - 1), is_transpose=True,
                 )
 
         def roots(n):

@@ -35,6 +35,8 @@ CAPS_PASS = K_PASS // OUT_DIM
 QUADS = OUT_DIM // PACK
 W_STEP = 2
 
+NATURAL = (False, True)
+
 FLOPS = 2 * BATCH * CAPS * OUT_DIM * NI
 BYTES = BATCH * CAPS * OUT_DIM * (4 + 2) + NI * CAPS * OUT_DIM * 2 + BATCH * NI * 4
 
@@ -108,7 +110,7 @@ def tile_capsulenetwork_pb_v_kernel(tc, p, Wr, s, grad_out, out):
 
         def regroup_weights(wp):
             w_grouped = w_stage.tile([P, N_PRIM, IN_DIM, PACK], BF16, name="w_grouped", align_bytes=64)
-            nc.scalar.copy(
+            nc.vector.tensor_copy(
                 out=w_grouped[:],
                 in_=tiles["w_loaded", wp][:].rearrange("row n (slot i) -> row n i slot", slot=PACK),
             )
@@ -238,32 +240,41 @@ def tile_capsulenetwork_pb_v_kernel(tc, p, Wr, s, grad_out, out):
 
         def scale(n, which, half):
             name = ("hg", "ct")[which]
-            planes = scaled.tile([P, HALF, PACK, P], F32, name=name)
-            tiles[name, n, half] = planes
             some = slice(half * HALF, (half + 1) * HALF)
-            nc.vector.tensor_tensor(
-                out=planes[:].rearrange("b c slot (j quad) -> b c j quad slot", quad=QUADS),
-                in0=tiles[("g", "t")[which], n][:].rearrange(
-                    "b (c j quad slot) -> b c j quad slot", c=PASSES, quad=QUADS, slot=PACK
-                )[:, some],
-                in1=tiles["by_token", n][:, which, :]
+            in0 = tiles[("g", "t")[which], n][:].rearrange(
+                "b (c j quad slot) -> b c j quad slot", c=PASSES, quad=QUADS, slot=PACK
+            )[:, some]
+            in1 = (
+                tiles["by_token", n][:, which, :]
                 .rearrange("b (c j) -> b c j", c=PASSES)[:, some]
                 .unsqueeze(3)
                 .unsqueeze(4)
-                .to_broadcast([P, HALF, CAPS_PASS, QUADS, PACK]),
-                op=ALU.mult,
+                .to_broadcast([P, HALF, CAPS_PASS, QUADS, PACK])
             )
+            if NATURAL[which]:
+                product = scaled.tile([P, HALF, P, PACK], F32, name=name)
+                out_ap = product[:].rearrange("b c (j quad) slot -> b c j quad slot", quad=QUADS)
+            else:
+                product = scaled.tile([P, HALF, PACK, P], F32, name=name)
+                out_ap = product[:].rearrange("b c slot (j quad) -> b c j quad slot", quad=QUADS)
+            tiles[name, n, half] = product
+            nc.vector.tensor_tensor(out=out_ap, in0=in0, in1=in1, op=ALU.mult)
+
+        def plane(name, which, n, half, ch, slot):
+            if NATURAL[which]:
+                return tiles[name, n, half][:, ch, :, slot]
+            return tiles[name, n, half][:, ch, slot, :]
 
         def transpose_add(n, c):
             half, ch = divmod(c, HALF)
             ds_t = psum_ds.tile([P, PACK, P], F32, name="ds_t")
             for slot in range(PACK):
                 nc.tensor.matmul(
-                    out=ds_t[:, slot, :], lhsT=tiles["hg", n, half][:, ch, slot, :], rhs=ident[:],
+                    out=ds_t[:, slot, :], lhsT=plane("hg", 0, n, half, ch, slot), rhs=ident[:],
                     start=True, stop=False, is_transpose=True,
                 )
                 nc.tensor.matmul(
-                    out=ds_t[:, slot, :], lhsT=tiles["ct", n, half][:, ch, slot, :], rhs=ident[:],
+                    out=ds_t[:, slot, :], lhsT=plane("ct", 1, n, half, ch, slot), rhs=ident[:],
                     start=False, stop=True, is_transpose=True,
                 )
             if c == 0:

@@ -36,6 +36,8 @@ QUADS = OUT_DIM // PACK
 W_STEP = 2
 
 NATURAL = (False, True)
+W_START = 1
+MX_START = W_START + 10
 
 FLOPS = 2 * BATCH * CAPS * OUT_DIM * NI
 BYTES = BATCH * CAPS * OUT_DIM * (4 + 2) + NI * CAPS * OUT_DIM * 2 + BATCH * NI * 4
@@ -52,8 +54,8 @@ def tile_capsulenetwork_pb_v_kernel(tc, p, Wr, s, grad_out, out):
             return stack.enter_context(tc.psum_pool(name=name, bufs=bufs))
 
         const = sbuf("const", 1)
-        w_raw = sbuf("w_raw", 2 * W_STEP)
-        w_stage = sbuf("w_stage", 2 * W_STEP)
+        w_raw = sbuf("w_raw", W_PASSES)
+        w_stage = sbuf("w_stage", 3)
         t_pool = sbuf("t_pool", 5)
         g_pool = sbuf("g_pool", 4)
         prods = sbuf("prods", 2)
@@ -61,7 +63,7 @@ def tile_capsulenetwork_pb_v_kernel(tc, p, Wr, s, grad_out, out):
         small = sbuf("small", 2)
         scaled = sbuf("scaled", 2)
         rounded = sbuf("rounded", 2)
-        coded = sbuf("coded", 2)
+        coded = sbuf("coded", MX_START - 2)
         results = sbuf("results", 2)
         psum_q = psum("psum_q", 1)
         psum_dot = psum("psum_dot", 1)
@@ -105,12 +107,12 @@ def tile_capsulenetwork_pb_v_kernel(tc, p, Wr, s, grad_out, out):
 
         def load_weights(wp):
             w_loaded = w_raw.tile([P, N_PRIM, PACK * IN_DIM], BF16, name="w_loaded")
-            nc.sync.dma_start(out=w_loaded[:], in_=w_view[wp])
+            nc.scalar.dma_start(out=w_loaded[:], in_=w_view[wp])
             tiles["w_loaded", wp] = w_loaded
 
         def regroup_weights(wp):
             w_grouped = w_stage.tile([P, N_PRIM, IN_DIM, PACK], BF16, name="w_grouped", align_bytes=64)
-            nc.vector.tensor_copy(
+            nc.scalar.copy(
                 out=w_grouped[:],
                 in_=tiles["w_loaded", wp][:].rearrange("row n (slot i) -> row n i slot", slot=PACK),
             )
@@ -319,10 +321,11 @@ def tile_capsulenetwork_pb_v_kernel(tc, p, Wr, s, grad_out, out):
         def live(n):
             return 0 <= n < N_CHUNKS
 
-        def weights_of(step):
-            return [wp for wp in range(step * W_STEP, (step + 1) * W_STEP) if 0 <= wp < W_PASSES]
+        def mx_step(n):
+            return max(n + 3, MX_START + n // HALVES)
 
         for step in range(-3, N_CHUNKS + 3):
+            due = [n for n in range(N_CHUNKS) if mx_step(n) == step]
             if live(step + 1):
                 halve_squares(step + 1)
             if live(step):
@@ -333,15 +336,15 @@ def tile_capsulenetwork_pb_v_kernel(tc, p, Wr, s, grad_out, out):
                 transpose_add(step - 2, 1)
             if live(step - 3):
                 quantise(step - 3)
-            for wp in weights_of(step):
-                quantise_weights(wp)
+            if 0 <= step - W_START - 2 < W_PASSES:
+                quantise_weights(step - W_START - 2)
             if live(step - 1):
                 dot_ru(step - 1)
                 coefficient(step - 1)
             if live(step):
                 denominator(step)
-            if live(step - 3):
-                multiply(step - 3)
+            for n in due[0:1]:
+                multiply(n)
             if live(step - 1):
                 to_tokens(step - 1)
             if live(step - 2):
@@ -356,25 +359,29 @@ def tile_capsulenetwork_pb_v_kernel(tc, p, Wr, s, grad_out, out):
                 t_times_g(step + 1)
             if live(step + 2):
                 squares(step + 2)
-            if live(step - 3):
-                store(step - 3)
+            if 0 <= step - W_START < W_PASSES:
+                regroup_weights(step - W_START)
+            for n in due[0:1]:
+                store(n)
             if live(step):
                 corrections(step)
                 bracket(step)
                 sum_products(step, 0)
+            for n in due[1:2]:
+                multiply(n)
             if live(step - 2):
                 transpose_add(step - 2, 2)
                 transpose_add(step - 2, 3)
+            for n in due[1:2]:
+                store(n)
             if live(step):
                 sum_products(step, 1)
             if live(step - 1):
                 scale(step - 1, 0, 0)
                 scale(step - 1, 1, 0)
-            for wp in weights_of(step + 1):
-                regroup_weights(wp)
             if live(step + 2):
                 load_g(step + 2)
             if live(step + 3):
                 load_t(step + 3)
-            for wp in weights_of(step + 2):
-                load_weights(wp)
+            if 0 <= step - W_START + 3 < W_PASSES:
+                load_weights(step - W_START + 3)

@@ -39,6 +39,8 @@ NATURAL = (False, True)
 W_START = 1
 MX_START = W_START + 10
 
+V_FIRST = 2
+
 FLOPS = 2 * BATCH * CAPS * OUT_DIM * NI
 BYTES = BATCH * CAPS * OUT_DIM * (4 + 2) + NI * CAPS * OUT_DIM * 2 + BATCH * NI * 4
 
@@ -141,12 +143,13 @@ def tile_capsulenetwork_pb_v_kernel(tc, p, Wr, s, grad_out, out):
             tiles["tt8", n] = tt8
 
         def t_times_g(n):
+            engine = nc.vector if n < V_FIRST else nc.gpsimd
             tg = scratch.tile([P, CAPS_CHUNK, OUT_DIM], F32, name="tg")
-            nc.gpsimd.tensor_tensor(
+            engine.tensor_tensor(
                 out=tg[:].rearrange("b j o -> b (j o)"), in0=tiles["t", n][:], in1=tiles["g", n][:], op=ALU.mult
             )
             tg8 = prods.tile([P, CAPS_CHUNK, OUT_DIM // 2], F32, name="tg8")
-            nc.gpsimd.tensor_tensor(
+            engine.tensor_tensor(
                 out=tg8[:], in0=tg[:, :, : OUT_DIM // 2], in1=tg[:, :, OUT_DIM // 2 :], op=ALU.add
             )
             tiles["tg8", n] = tg8

@@ -36,9 +36,27 @@ QUADS = OUT_DIM // PACK
 W_STEP = 2
 
 NATURAL = (False, True)
-W_START = 1
+W_START = 0
 MX_START = W_START + 10
 
+T_AHEAD = 5
+G_AHEAD = 5
+TG_BUFS = 2
+QL = 3
+HALVE_LATE = False
+SCB = 2
+COEF_G = True
+PB = 3
+SQ = 3
+REG_LATE = 0
+TT_PAIRS = 8
+PLAIN_FROM = 0
+PLAIN_TO = 0
+PLAIN_Q = 2
+PLAIN_DOT = 2
+PLAIN_TOK = True
+PLAIN_DS = 0
+TG_PAIRS = 4
 V_FIRST = 2
 
 FLOPS = 2 * BATCH * CAPS * OUT_DIM * NI
@@ -56,16 +74,16 @@ def tile_capsulenetwork_pb_v_kernel(tc, p, Wr, s, grad_out, out):
             return stack.enter_context(tc.psum_pool(name=name, bufs=bufs))
 
         const = sbuf("const", 1)
-        w_raw = sbuf("w_raw", W_PASSES)
+        w_raw = sbuf("w_raw", 4)
         w_stage = sbuf("w_stage", 3)
-        t_pool = sbuf("t_pool", 5)
-        g_pool = sbuf("g_pool", 4)
-        prods = sbuf("prods", 2)
-        scratch = sbuf("scratch", 1)
+        t_pool = sbuf("t_pool", T_AHEAD)
+        g_pool = sbuf("g_pool", G_AHEAD)
+        prods = sbuf("prods", PB)
+        scratch = sbuf("scratch", TG_BUFS)
         small = sbuf("small", 2)
-        scaled = sbuf("scaled", 2)
-        rounded = sbuf("rounded", 2)
-        coded = sbuf("coded", MX_START - 2)
+        scaled = sbuf("scaled", SCB)
+        rounded = sbuf("rounded", QL)
+        coded = sbuf("coded", MX_START + 1 - QL)
         results = sbuf("results", 2)
         psum_q = psum("psum_q", 1)
         psum_dot = psum("psum_dot", 1)
@@ -78,8 +96,6 @@ def tile_capsulenetwork_pb_v_kernel(tc, p, Wr, s, grad_out, out):
         make_identity(nc, ident[:])
         eps_col = const.tile([P, 1], F32, name="eps_col")
         nc.vector.memset(eps_col[:], SQ_EPS)
-        one_col = const.tile([P, 1], F32, name="one_col")
-        nc.vector.memset(one_col[:], 1.0)
         minus_one_col = const.tile([P, 1], F32, name="minus_one_col")
         nc.vector.memset(minus_one_col[:], -1.0)
         w_codes = const.tile([P, W_PASSES, NI], U32, name="w_codes", align_bytes=64)
@@ -135,12 +151,16 @@ def tile_capsulenetwork_pb_v_kernel(tc, p, Wr, s, grad_out, out):
             tiles["tt", n] = tt
 
         def halve_squares(n):
+            if TT_PAIRS == 0:
+                return
             tt = tiles["tt", n]
-            tt8 = prods.tile([P, CAPS_CHUNK, OUT_DIM // 2], F32, name="tt8")
+            tt_low = prods.tile([P, CAPS_CHUNK, TT_PAIRS], F32, name="tt_low")
             nc.vector.tensor_tensor(
-                out=tt8[:], in0=tt[:, :, : OUT_DIM // 2], in1=tt[:, :, OUT_DIM // 2 :], op=ALU.add
+                out=tt_low[:], in0=tt[:, :, :TT_PAIRS], in1=tt[:, :, TT_PAIRS : 2 * TT_PAIRS], op=ALU.add
             )
-            tiles["tt8", n] = tt8
+            tiles["tt_planes", n] = [tt_low[:, :, o] for o in range(TT_PAIRS)] + [
+                tt[:, :, o] for o in range(2 * TT_PAIRS, OUT_DIM)
+            ]
 
         def t_times_g(n):
             engine = nc.vector if n < V_FIRST else nc.gpsimd
@@ -148,55 +168,67 @@ def tile_capsulenetwork_pb_v_kernel(tc, p, Wr, s, grad_out, out):
             engine.tensor_tensor(
                 out=tg[:].rearrange("b j o -> b (j o)"), in0=tiles["t", n][:], in1=tiles["g", n][:], op=ALU.mult
             )
-            tg8 = prods.tile([P, CAPS_CHUNK, OUT_DIM // 2], F32, name="tg8")
+            if TG_PAIRS == 0:
+                tiles["tg_planes", n] = [tg[:, :, o] for o in range(OUT_DIM)]
+                return
+            tg_low = prods.tile([P, CAPS_CHUNK, TG_PAIRS], F32, name="tg_low")
             engine.tensor_tensor(
-                out=tg8[:], in0=tg[:, :, : OUT_DIM // 2], in1=tg[:, :, OUT_DIM // 2 :], op=ALU.add
+                out=tg_low[:], in0=tg[:, :, :TG_PAIRS], in1=tg[:, :, TG_PAIRS : 2 * TG_PAIRS], op=ALU.add
             )
-            tiles["tg8", n] = tg8
+            tiles["tg_planes", n] = [tg[:, :, o] for o in range(2 * TG_PAIRS, OUT_DIM)] + [
+                tg_low[:, :, o] for o in range(TG_PAIRS)
+            ]
+
+        def turn(ps, plane_o, first, last, plain=False):
+            if plain:
+                nc.tensor.matmul(out=ps, lhsT=plane_o, rhs=ident[:], start=first, stop=last)
+            else:
+                nc.tensor.matmul(out=ps, lhsT=plane_o, rhs=ident[:], start=first, stop=last, is_transpose=True)
+
+        def spread(o, total, some):
+            return (o + 1) * some // total > o * some // total
+
+        def warm(n):
+            return PLAIN_FROM <= n < PLAIN_TO
 
         def sum_squares(n):
             q_ps = psum_q.tile([P, P], F32, name="q_ps")
-            width = OUT_DIM // 2
-            for o in range(width):
-                nc.tensor.matmul(
-                    out=q_ps[:], lhsT=tiles["tt8", n][:, :, o], rhs=ident[:],
-                    start=(o == 0), stop=(o == width - 1), is_transpose=True,
-                )
+            planes = tiles["tt_planes", n] if TT_PAIRS else [tiles["tt", n][:, :, o] for o in range(OUT_DIM)]
+            for o, plane_o in enumerate(planes):
+                turn(q_ps[:], plane_o, o == 0, o == len(planes) - 1, warm(n) and spread(o, len(planes), PLAIN_Q))
             tiles["q", n] = q_ps
 
         def sum_products(n, part):
             if part == 0:
                 dot_ps = psum_dot.tile([P, P], F32, name="dot_ps")
                 tiles["dot", n] = dot_ps
-            width = OUT_DIM // 2
-            for o in range(part * width // 2, (part + 1) * width // 2):
-                nc.tensor.matmul(
-                    out=tiles["dot", n][:], lhsT=tiles["tg8", n][:, :, o], rhs=ident[:],
-                    start=(o == 0), stop=(o == width - 1), is_transpose=True,
+            planes = tiles["tg_planes", n]
+            for o in range(part * len(planes) // 2, (part + 1) * len(planes) // 2):
+                turn(
+                    tiles["dot", n][:], planes[o], o == 0, o == len(planes) - 1,
+                    warm(n) and spread(o, len(planes), PLAIN_DOT),
                 )
 
         def roots(n):
             q = tiles["q", n][:]
             root = small.tile([P, P], F32, name="root")
             nc.scalar.activation(out=root[:], in_=q, func=ACT.Sqrt, bias=eps_col[:])
-            den_q1 = small.tile([P, 2, P], F32, name="den_q1")
-            nc.scalar.activation(out=den_q1[:, 1, :], in_=q, func=ACT.Identity, bias=one_col[:])
             tiles["root", n] = root
-            tiles["den_q1", n] = den_q1
 
         def denominator(n):
+            den = small.tile([P, P], F32, name="den")
             nc.vector.scalar_tensor_tensor(
-                out=tiles["den_q1", n][:, 0, :], in0=tiles["q", n][:], scalar=1.0, in1=tiles["root", n][:],
-                op0=ALU.add, op1=ALU.mult,
+                out=den[:], in0=tiles["q", n][:], scalar=1.0, in1=tiles["root", n][:], op0=ALU.add, op1=ALU.mult
             )
+            tiles["den", n] = den
 
         def invert(n):
-            ru_u = small.tile([P, 2, P], F32, name="ru_u")
-            nc.vector.reciprocal(out=ru_u[:], in_=tiles["den_q1", n][:])
-            tiles["ru_u", n] = ru_u
+            ru = small.tile([P, P], F32, name="ru")
+            nc.vector.reciprocal(out=ru[:], in_=tiles["den", n][:])
+            tiles["ru", n] = ru
 
         def r_and_h(n):
-            ru = tiles["ru_u", n][:, 0, :]
+            ru = tiles["ru", n][:]
             r = small.tile([P, P], F32, name="r")
             nc.vector.scalar_tensor_tensor(
                 out=r[:], in0=tiles["q", n][:], scalar=1.0, in1=ru, op0=ALU.add, op1=ALU.mult
@@ -207,32 +239,34 @@ def tile_capsulenetwork_pb_v_kernel(tc, p, Wr, s, grad_out, out):
             tiles["h_coef", n] = h_coef
 
         def corrections(n):
-            two_u_less_1 = small.tile([P, P], F32, name="two_u_less_1")
-            nc.scalar.activation(
-                out=two_u_less_1[:], in_=tiles["ru_u", n][:, 1, :], func=ACT.Identity, scale=2.0,
-                bias=minus_one_col[:],
-            )
             eps_rr = small.tile([P, P], F32, name="eps_rr")
             nc.scalar.activation(out=eps_rr[:], in_=tiles["r", n][:], func=ACT.Square, scale=SQ_EPS**0.5)
-            tiles["two_u_less_1", n] = two_u_less_1
-            tiles["eps_rr", n] = eps_rr
+            minus_qrr = small.tile([P, P], F32, name="minus_qrr")
+            nc.scalar.activation(out=minus_qrr[:], in_=eps_rr[:], func=ACT.Identity, bias=minus_one_col[:])
+            tiles["minus_qrr", n] = minus_qrr
+
+        def unit(n):
+            u = small.tile([P, P], F32, name="u")
+            nc.vector.tensor_tensor(out=u[:], in0=tiles["root", n][:], in1=tiles["ru", n][:], op=ALU.mult)
+            tiles["u", n] = u
 
         def bracket(n):
             in_brackets = small.tile([P, P], F32, name="in_brackets")
-            nc.gpsimd.tensor_tensor(
-                out=in_brackets[:], in0=tiles["two_u_less_1", n][:], in1=tiles["eps_rr", n][:], op=ALU.add
+            nc.vector.scalar_tensor_tensor(
+                out=in_brackets[:], in0=tiles["u", n][:], scalar=2.0, in1=tiles["minus_qrr", n][:],
+                op0=ALU.mult, op1=ALU.add,
             )
             tiles["in_brackets", n] = in_brackets
 
         def dot_ru(n):
             dru = small.tile([P, P], F32, name="dru")
             nc.vector.tensor_tensor(
-                out=dru[:], in0=tiles["dot", n][:], in1=tiles["ru_u", n][:, 0, :], op=ALU.mult
+                out=dru[:], in0=tiles["dot", n][:], in1=tiles["ru", n][:], op=ALU.mult
             )
             tiles["dru", n] = dru
 
         def coefficient(n):
-            nc.gpsimd.tensor_tensor(
+            (nc.gpsimd if COEF_G else nc.vector).tensor_tensor(
                 out=tiles["h_coef", n][:, 1, :], in0=tiles["in_brackets", n][:], in1=tiles["dru", n][:],
                 op=ALU.mult,
             )
@@ -240,7 +274,7 @@ def tile_capsulenetwork_pb_v_kernel(tc, p, Wr, s, grad_out, out):
         def to_tokens(n):
             by_token = psum_factors.tile([P, 2, P], F32, name="by_token")
             for which in range(2):
-                nc.tensor.transpose(out=by_token[:, which, :], in_=tiles["h_coef", n][:, which, :], identity=ident[:])
+                turn(by_token[:, which, :], tiles["h_coef", n][:, which, :], True, True, warm(n) and PLAIN_TOK)
             tiles["by_token", n] = by_token
 
         def scale(n, which, half):
@@ -274,13 +308,10 @@ def tile_capsulenetwork_pb_v_kernel(tc, p, Wr, s, grad_out, out):
             half, ch = divmod(c, HALF)
             ds_t = psum_ds.tile([P, PACK, P], F32, name="ds_t")
             for slot in range(PACK):
-                nc.tensor.matmul(
-                    out=ds_t[:, slot, :], lhsT=plane("hg", 0, n, half, ch, slot), rhs=ident[:],
-                    start=True, stop=False, is_transpose=True,
-                )
-                nc.tensor.matmul(
-                    out=ds_t[:, slot, :], lhsT=plane("ct", 1, n, half, ch, slot), rhs=ident[:],
-                    start=False, stop=True, is_transpose=True,
+                turn(ds_t[:, slot, :], plane("hg", 0, n, half, ch, slot), True, False)
+                turn(
+                    ds_t[:, slot, :], plane("ct", 1, n, half, ch, slot), False, True,
+                    warm(n) and spread(slot, PACK, PLAIN_DS),
                 )
             if c == 0:
                 grouped = rounded.tile([P, PASSES, P, PACK], BF16, name="grouped", align_bytes=64)
@@ -325,66 +356,73 @@ def tile_capsulenetwork_pb_v_kernel(tc, p, Wr, s, grad_out, out):
             return 0 <= n < N_CHUNKS
 
         def mx_step(n):
-            return max(n + 3, MX_START + n // HALVES)
+            return max(n + QL, MX_START + n // HALVES)
 
+        for n in range(T_AHEAD):
+            load_t(n)
+            if n < G_AHEAD:
+                load_g(n)
         for step in range(-3, N_CHUNKS + 3):
             due = [n for n in range(N_CHUNKS) if mx_step(n) == step]
-            if live(step + 1):
-                halve_squares(step + 1)
             if live(step):
-                sum_squares(step)
-                roots(step)
-            if live(step - 2):
-                transpose_add(step - 2, 0)
-                transpose_add(step - 2, 1)
-            if live(step - 3):
-                quantise(step - 3)
+                unit(step)
+                dot_ru(step)
+            if live(step - QL):
+                quantise(step - QL)
             if 0 <= step - W_START - 2 < W_PASSES:
                 quantise_weights(step - W_START - 2)
-            if live(step - 1):
-                dot_ru(step - 1)
-                coefficient(step - 1)
+            if live(step + 2) and not HALVE_LATE:
+                halve_squares(step + 2)
             if live(step):
-                denominator(step)
-            for n in due[0:1]:
-                multiply(n)
-            if live(step - 1):
-                to_tokens(step - 1)
-            if live(step - 2):
-                scale(step - 2, 0, 1)
-            if live(step):
-                invert(step)
-            if live(step - 2):
-                scale(step - 2, 1, 1)
-            if live(step):
-                r_and_h(step)
+                bracket(step)
+                coefficient(step)
             if live(step + 1):
-                t_times_g(step + 1)
+                sum_squares(step + 1)
+                roots(step + 1)
             if live(step + 2):
-                squares(step + 2)
+                if HALVE_LATE:
+                    halve_squares(step + 2)
+                t_times_g(step + 2)
+            if live(step - 1):
+                transpose_add(step - 1, 0)
+                transpose_add(step - 1, 1)
+            if live(step):
+                to_tokens(step)
+            if live(step + SQ):
+                squares(step + SQ)
             if 0 <= step - W_START < W_PASSES:
                 regroup_weights(step - W_START)
             for n in due[0:1]:
-                store(n)
+                multiply(n)
+            if live(step - 1):
+                scale(step - 1, 0, 1)
+            if live(step + 1):
+                denominator(step + 1)
+            if live(step - 1):
+                scale(step - 1, 1, 1)
+            if live(step + 1):
+                invert(step + 1)
+                sum_products(step + 1, 0)
+                sum_products(step + 1, 1)
             if live(step):
-                corrections(step)
-                bracket(step)
-                sum_products(step, 0)
+                scale(step, 0, 0)
+            if live(step + 1):
+                r_and_h(step + 1)
+                corrections(step + 1)
+            if live(step):
+                scale(step, 1, 0)
+            for n in due[0:1]:
+                store(n)
             for n in due[1:2]:
                 multiply(n)
-            if live(step - 2):
-                transpose_add(step - 2, 2)
-                transpose_add(step - 2, 3)
+            if live(step - 1):
+                transpose_add(step - 1, 2)
+                transpose_add(step - 1, 3)
             for n in due[1:2]:
                 store(n)
-            if live(step):
-                sum_products(step, 1)
-            if live(step - 1):
-                scale(step - 1, 0, 0)
-                scale(step - 1, 1, 0)
-            if live(step + 2):
-                load_g(step + 2)
-            if live(step + 3):
-                load_t(step + 3)
+            if live(step - 1) and live(step - 1 + G_AHEAD):
+                load_g(step - 1 + G_AHEAD)
+            if live(step - 1) and live(step - 1 + T_AHEAD):
+                load_t(step - 1 + T_AHEAD)
             if 0 <= step - W_START + 3 < W_PASSES:
                 load_weights(step - W_START + 3)

@@ -41,22 +41,24 @@ MX_START = W_START + 10
 
 T_AHEAD = 5
 G_AHEAD = 5
+PLANES = True
 TG_BUFS = 2
 QL = 3
 HALVE_LATE = False
-SCB = 2
+SCB = 3
 COEF_G = True
-PB = 3
-SQ = 3
+PB = 2
+SQ = 2
 REG_LATE = 0
-TT_PAIRS = 8
+S_EARLY = -9
+TT_PAIRS = 0
 PLAIN_FROM = 0
 PLAIN_TO = 0
 PLAIN_Q = 2
 PLAIN_DOT = 2
 PLAIN_TOK = True
 PLAIN_DS = 0
-TG_PAIRS = 4
+TG_PAIRS = 6
 V_FIRST = 2
 
 FLOPS = 2 * BATCH * CAPS * OUT_DIM * NI
@@ -144,11 +146,20 @@ def tile_capsulenetwork_pb_v_kernel(tc, p, Wr, s, grad_out, out):
             )
 
         def squares(n):
-            tt = prods.tile([P, CAPS_CHUNK, OUT_DIM], F32, name="tt")
-            nc.scalar.activation(
-                out=tt[:].rearrange("b j o -> b (j o)"), in_=tiles["t", n][:], func=ACT.Square
-            )
-            tiles["tt", n] = tt
+            if PLANES:
+                ttp = prods.tile([P, QUADS, PACK, CAPS_CHUNK], F32, name="tt")
+                nc.scalar.activation(
+                    out=ttp[:].rearrange("b quad slot j -> b quad j slot"),
+                    in_=tiles["t", n][:].rearrange("b (j quad slot) -> b quad j slot", quad=QUADS, slot=PACK),
+                    func=ACT.Square,
+                )
+                tiles["tt", n] = ttp[:].rearrange("b quad slot j -> b j (quad slot)")
+            else:
+                tt = prods.tile([P, CAPS_CHUNK, OUT_DIM], F32, name="tt")
+                nc.scalar.activation(
+                    out=tt[:].rearrange("b j o -> b (j o)"), in_=tiles["t", n][:], func=ACT.Square
+                )
+                tiles["tt", n] = tt
 
         def halve_squares(n):
             if TT_PAIRS == 0:
@@ -382,18 +393,17 @@ def tile_capsulenetwork_pb_v_kernel(tc, p, Wr, s, grad_out, out):
             if live(step + 2):
                 if HALVE_LATE:
                     halve_squares(step + 2)
-                t_times_g(step + 2)
+                if step + 2 >= V_FIRST:
+                    t_times_g(step + 2)
             if live(step - 1):
                 transpose_add(step - 1, 0)
                 transpose_add(step - 1, 1)
             if live(step):
                 to_tokens(step)
-            if live(step + SQ):
+            if step > S_EARLY and live(step + SQ):
                 squares(step + SQ)
-            if 0 <= step - W_START < W_PASSES:
+            if not REG_LATE and 0 <= step - W_START < W_PASSES:
                 regroup_weights(step - W_START)
-            for n in due[0:1]:
-                multiply(n)
             if live(step - 1):
                 scale(step - 1, 0, 1)
             if live(step + 1):
@@ -409,16 +419,20 @@ def tile_capsulenetwork_pb_v_kernel(tc, p, Wr, s, grad_out, out):
             if live(step + 1):
                 r_and_h(step + 1)
                 corrections(step + 1)
+            if step <= S_EARLY and live(step + SQ):
+                squares(step + SQ)
             if live(step):
                 scale(step, 1, 0)
-            for n in due[0:1]:
-                store(n)
-            for n in due[1:2]:
-                multiply(n)
+            if 0 <= step + 2 < V_FIRST:
+                t_times_g(step + 2)
             if live(step - 1):
                 transpose_add(step - 1, 2)
                 transpose_add(step - 1, 3)
-            for n in due[1:2]:
+            if REG_LATE and 0 <= step - W_START < W_PASSES:
+                regroup_weights(step - W_START)
+            for n in due:
+                multiply(n)
+            for n in due:
                 store(n)
             if live(step - 1) and live(step - 1 + G_AHEAD):
                 load_g(step - 1 + G_AHEAD)

@@ -45,11 +45,17 @@ PLANES = True
 TG_BUFS = 2
 QL = 3
 HALVE_LATE = False
-SCB = 3
+SCB = 2
 COEF_G = True
 PB = 2
 SQ = 2
-REG_LATE = 0
+REG_LATE = 1
+FIRST_PIECES = 2
+WD = 3
+MXR = 2
+MXM = 1
+DSB = 3
+ADDED = 2
 S_EARLY = -9
 TT_PAIRS = 0
 PLAIN_FROM = 0
@@ -58,7 +64,7 @@ PLAIN_Q = 2
 PLAIN_DOT = 2
 PLAIN_TOK = True
 PLAIN_DS = 0
-TG_PAIRS = 6
+TG_PAIRS = 2
 V_FIRST = 2
 
 FLOPS = 2 * BATCH * CAPS * OUT_DIM * NI
@@ -90,8 +96,8 @@ def tile_capsulenetwork_pb_v_kernel(tc, p, Wr, s, grad_out, out):
         psum_q = psum("psum_q", 1)
         psum_dot = psum("psum_dot", 1)
         psum_factors = psum("psum_factors", 2)
-        psum_ds = psum("psum_ds", 3)
-        psum_acc = psum("psum_acc", 1)
+        psum_ds = psum("psum_ds", DSB)
+        psum_acc = psum("psum_acc", 4 - DSB)
         stack.enter_context(tc.manual_schedule())
 
         ident = const.tile([P, P], F32, name="ident")
@@ -116,7 +122,15 @@ def tile_capsulenetwork_pb_v_kernel(tc, p, Wr, s, grad_out, out):
         def load_t(n):
             tokens, caps = rows_of(n)
             t_sb = t_pool.tile([P, COLS], F32, name="t_sb")
-            nc.sync.dma_start(out=t_sb[:], in_=s[tokens, caps, :].rearrange("b j o -> b (j o)"))
+            pieces = FIRST_PIECES if n == 0 else 1
+            wide = CAPS_CHUNK // pieces
+            for piece in range(pieces):
+                nc.sync.dma_start(
+                    out=t_sb[:, piece * wide * OUT_DIM : (piece + 1) * wide * OUT_DIM],
+                    in_=s[tokens, caps.start + piece * wide : caps.start + (piece + 1) * wide, :].rearrange(
+                        "b j o -> b (j o)"
+                    ),
+                )
             tiles["t", n] = t_sb
 
         def load_g(n):
@@ -148,11 +162,17 @@ def tile_capsulenetwork_pb_v_kernel(tc, p, Wr, s, grad_out, out):
         def squares(n):
             if PLANES:
                 ttp = prods.tile([P, QUADS, PACK, CAPS_CHUNK], F32, name="tt")
-                nc.scalar.activation(
-                    out=ttp[:].rearrange("b quad slot j -> b quad j slot"),
-                    in_=tiles["t", n][:].rearrange("b (j quad slot) -> b quad j slot", quad=QUADS, slot=PACK),
-                    func=ACT.Square,
-                )
+                pieces = FIRST_PIECES if n == 0 else 1
+                wide = CAPS_CHUNK // pieces
+                for piece in range(pieces):
+                    some = slice(piece * wide, (piece + 1) * wide)
+                    nc.scalar.activation(
+                        out=ttp[:, :, :, some].rearrange("b quad slot j -> b quad j slot"),
+                        in_=tiles["t", n][:].rearrange("b (j quad slot) -> b quad j slot", quad=QUADS, slot=PACK)[
+                            :, :, some
+                        ],
+                        func=ACT.Square,
+                    )
                 tiles["tt", n] = ttp[:].rearrange("b quad slot j -> b j (quad slot)")
             else:
                 tt = prods.tile([P, CAPS_CHUNK, OUT_DIM], F32, name="tt")
@@ -301,8 +321,8 @@ def tile_capsulenetwork_pb_v_kernel(tc, p, Wr, s, grad_out, out):
                 .unsqueeze(4)
                 .to_broadcast([P, HALF, CAPS_PASS, QUADS, PACK])
             )
-            if NATURAL[which]:
-                product = scaled.tile([P, HALF, P, PACK], F32, name=name)
+            if NATURAL[which] or (half == 0 and ADDED):
+                product = scaled.tile([P, HALF, P, PACK], F32, name=name + "_k")
                 out_ap = product[:].rearrange("b c (j quad) slot -> b c j quad slot", quad=QUADS)
             else:
                 product = scaled.tile([P, HALF, PACK, P], F32, name=name)
@@ -310,8 +330,30 @@ def tile_capsulenetwork_pb_v_kernel(tc, p, Wr, s, grad_out, out):
             tiles[name, n, half] = product
             nc.vector.tensor_tensor(out=out_ap, in0=in0, in1=in1, op=ALU.mult)
 
+        def add(n):
+            ds_words = scaled.tile([P, ADDED, P, PACK], BF16, name="ds_words", align_bytes=64)
+            nc.vector.tensor_tensor(
+                out=ds_words[:], in0=tiles["hg", n, 0][:, :ADDED], in1=tiles["ct", n, 0][:, :ADDED], op=ALU.add
+            )
+            tiles["ds_words", n] = ds_words
+
+        def transpose_words(n):
+            words = tiles["ds_words", n][:].rearrange("b c row slot -> b (c row slot)").bitcast(F32)
+            ds_t = psum_ds.tile([P, 2, 2, P], F32, name="ds_t")
+            for c in range(ADDED):
+                for u in range(2):
+                    turn(ds_t[:, c, u, :], words.rearrange("b (c row u) -> b c row u", u=2, c=ADDED)[:, c, :, u], True, True)
+            if ADDED == 2:
+                grouped = rounded.tile([P, PASSES, P, PACK], BF16, name="grouped", align_bytes=64)
+                tiles["grouped", n] = grouped
+            nc.scalar.copy(
+                out=tiles["grouped", n][:, :ADDED].rearrange("row c b slot -> row (c b slot)").bitcast(F32)
+                .rearrange("row (c b u) -> row c b u", u=2, c=ADDED),
+                in_=ds_t[:, :ADDED].rearrange("row c u b -> row c b u"),
+            )
+
         def plane(name, which, n, half, ch, slot):
-            if NATURAL[which]:
+            if NATURAL[which] or (half == 0 and ADDED):
                 return tiles[name, n, half][:, ch, :, slot]
             return tiles[name, n, half][:, ch, slot, :]
 
@@ -324,7 +366,7 @@ def tile_capsulenetwork_pb_v_kernel(tc, p, Wr, s, grad_out, out):
                     ds_t[:, slot, :], plane("ct", 1, n, half, ch, slot), False, True,
                     warm(n) and spread(slot, PACK, PLAIN_DS),
                 )
-            if c == 0:
+            if c == ADDED and ADDED < HALF:
                 grouped = rounded.tile([P, PASSES, P, PACK], BF16, name="grouped", align_bytes=64)
                 tiles["grouped", n] = grouped
             nc.scalar.copy(out=tiles["grouped", n][:, c], in_=ds_t[:].rearrange("row slot b -> row b slot"))
@@ -367,7 +409,7 @@ def tile_capsulenetwork_pb_v_kernel(tc, p, Wr, s, grad_out, out):
             return 0 <= n < N_CHUNKS
 
         def mx_step(n):
-            return max(n + QL, MX_START + n // HALVES)
+            return max(n + QL, MX_START + n // MXR)
 
         for n in range(T_AHEAD):
             load_t(n)
@@ -384,6 +426,8 @@ def tile_capsulenetwork_pb_v_kernel(tc, p, Wr, s, grad_out, out):
                 quantise_weights(step - W_START - 2)
             if live(step + 2) and not HALVE_LATE:
                 halve_squares(step + 2)
+            if ADDED and live(step - 1):
+                add(step - 1)
             if live(step):
                 bracket(step)
                 coefficient(step)
@@ -396,8 +440,10 @@ def tile_capsulenetwork_pb_v_kernel(tc, p, Wr, s, grad_out, out):
                 if step + 2 >= V_FIRST:
                     t_times_g(step + 2)
             if live(step - 1):
-                transpose_add(step - 1, 0)
-                transpose_add(step - 1, 1)
+                for c in range(ADDED, HALF):
+                    transpose_add(step - 1, c)
+                if ADDED:
+                    transpose_words(step - 1)
             if live(step):
                 to_tokens(step)
             if step > S_EARLY and live(step + SQ):
@@ -414,6 +460,9 @@ def tile_capsulenetwork_pb_v_kernel(tc, p, Wr, s, grad_out, out):
                 invert(step + 1)
                 sum_products(step + 1, 0)
                 sum_products(step + 1, 1)
+            for n in due[:MXM]:
+                multiply(n)
+                store(n)
             if live(step):
                 scale(step, 0, 0)
             if live(step + 1):
@@ -430,13 +479,12 @@ def tile_capsulenetwork_pb_v_kernel(tc, p, Wr, s, grad_out, out):
                 transpose_add(step - 1, 3)
             if REG_LATE and 0 <= step - W_START < W_PASSES:
                 regroup_weights(step - W_START)
-            for n in due:
+            for n in due[MXM:]:
                 multiply(n)
-            for n in due:
                 store(n)
             if live(step - 1) and live(step - 1 + G_AHEAD):
                 load_g(step - 1 + G_AHEAD)
             if live(step - 1) and live(step - 1 + T_AHEAD):
                 load_t(step - 1 + T_AHEAD)
-            if 0 <= step - W_START + 3 < W_PASSES:
-                load_weights(step - W_START + 3)
+            if 0 <= step - W_START + WD < W_PASSES:
+                load_weights(step - W_START + WD)

@@ -37,7 +37,7 @@ W_STEP = 2
 
 NATURAL = (False, True)
 W_START = 0
-MX_START = W_START + 10
+MX_START = W_START + 9
 
 T_AHEAD = 5
 G_AHEAD = 5
@@ -55,7 +55,9 @@ WD = 3
 MXR = 2
 MXM = 1
 DSB = 3
-ADDED = 2
+ADD_EARLY = 1
+ADD_LATE = 2
+ADD_FROM = 8
 S_EARLY = -9
 TT_PAIRS = 0
 PLAIN_FROM = 0
@@ -321,7 +323,7 @@ def tile_capsulenetwork_pb_v_kernel(tc, p, Wr, s, grad_out, out):
                 .unsqueeze(4)
                 .to_broadcast([P, HALF, CAPS_PASS, QUADS, PACK])
             )
-            if NATURAL[which] or (half == 0 and ADDED):
+            if NATURAL[which] or (half == 0 and added(n)):
                 product = scaled.tile([P, HALF, P, PACK], F32, name=name + "_k")
                 out_ap = product[:].rearrange("b c (j quad) slot -> b c j quad slot", quad=QUADS)
             else:
@@ -330,30 +332,36 @@ def tile_capsulenetwork_pb_v_kernel(tc, p, Wr, s, grad_out, out):
             tiles[name, n, half] = product
             nc.vector.tensor_tensor(out=out_ap, in0=in0, in1=in1, op=ALU.mult)
 
+        def added(n):
+            return ADD_LATE if n >= ADD_FROM else ADD_EARLY
+
         def add(n):
-            ds_words = scaled.tile([P, ADDED, P, PACK], BF16, name="ds_words", align_bytes=64)
+            ds_words = scaled.tile([P, added(n), P, PACK], BF16, name="ds_words", align_bytes=64)
             nc.vector.tensor_tensor(
-                out=ds_words[:], in0=tiles["hg", n, 0][:, :ADDED], in1=tiles["ct", n, 0][:, :ADDED], op=ALU.add
+                out=ds_words[:], in0=tiles["hg", n, 0][:, :added(n)], in1=tiles["ct", n, 0][:, :added(n)], op=ALU.add
             )
             tiles["ds_words", n] = ds_words
+
+        def grouped_of(n):
+            if ("grouped", n) not in tiles:
+                grouped = rounded.tile([P, PASSES, P, PACK], BF16, name="grouped", align_bytes=64)
+                tiles["grouped", n] = grouped
+            return tiles["grouped", n]
 
         def transpose_words(n):
             words = tiles["ds_words", n][:].rearrange("b c row slot -> b (c row slot)").bitcast(F32)
             ds_t = psum_ds.tile([P, 2, 2, P], F32, name="ds_t")
-            for c in range(ADDED):
+            for c in range(added(n)):
                 for u in range(2):
-                    turn(ds_t[:, c, u, :], words.rearrange("b (c row u) -> b c row u", u=2, c=ADDED)[:, c, :, u], True, True)
-            if ADDED == 2:
-                grouped = rounded.tile([P, PASSES, P, PACK], BF16, name="grouped", align_bytes=64)
-                tiles["grouped", n] = grouped
+                    turn(ds_t[:, c, u, :], words.rearrange("b (c row u) -> b c row u", u=2, c=added(n))[:, c, :, u], True, True)
             nc.scalar.copy(
-                out=tiles["grouped", n][:, :ADDED].rearrange("row c b slot -> row (c b slot)").bitcast(F32)
-                .rearrange("row (c b u) -> row c b u", u=2, c=ADDED),
-                in_=ds_t[:, :ADDED].rearrange("row c u b -> row c b u"),
+                out=grouped_of(n)[:, :added(n)].rearrange("row c b slot -> row (c b slot)").bitcast(F32)
+                .rearrange("row (c b u) -> row c b u", u=2, c=added(n)),
+                in_=ds_t[:, :added(n)].rearrange("row c u b -> row c b u"),
             )
 
         def plane(name, which, n, half, ch, slot):
-            if NATURAL[which] or (half == 0 and ADDED):
+            if NATURAL[which] or (half == 0 and added(n)):
                 return tiles[name, n, half][:, ch, :, slot]
             return tiles[name, n, half][:, ch, slot, :]
 
@@ -366,10 +374,20 @@ def tile_capsulenetwork_pb_v_kernel(tc, p, Wr, s, grad_out, out):
                     ds_t[:, slot, :], plane("ct", 1, n, half, ch, slot), False, True,
                     warm(n) and spread(slot, PACK, PLAIN_DS),
                 )
-            if c == ADDED and ADDED < HALF:
-                grouped = rounded.tile([P, PASSES, P, PACK], BF16, name="grouped", align_bytes=64)
-                tiles["grouped", n] = grouped
-            nc.scalar.copy(out=tiles["grouped", n][:, c], in_=ds_t[:].rearrange("row slot b -> row b slot"))
+            nc.scalar.copy(out=grouped_of(n)[:, c], in_=ds_t[:].rearrange("row slot b -> row b slot"))
+
+        def quantise_half(n, half):
+            some = slice(half * HALF, (half + 1) * HALF)
+            if half == 0:
+                codes = coded.tile([P, PASSES, P], U32, name="codes", align_bytes=64)
+                scales = coded.tile([P, PASSES, P], U8, name="scales", align_bytes=64)
+                tiles["codes", n] = codes
+                tiles["scales", n] = scales
+            nc.vector.quantize_mx(
+                out=tiles["codes", n][:, some].rearrange("row c b -> row (c b)").bitcast(E5M2_X4),
+                scales=tiles["scales", n][:, some].rearrange("row c b -> row (c b)"),
+                in_=tiles["grouped", n][:, some].rearrange("row c b slot -> row (c b slot)"),
+            )
 
         def quantise(n):
             codes = coded.tile([P, PASSES, P], U32, name="codes", align_bytes=64)
@@ -382,12 +400,12 @@ def tile_capsulenetwork_pb_v_kernel(tc, p, Wr, s, grad_out, out):
             tiles["codes", n] = codes
             tiles["scales", n] = scales
 
-        def multiply(n):
+        def multiply(n, some=range(PASSES)):
             block, half = divmod(n, HALVES)
-            if half == 0:
+            if half == 0 and 0 in some:
                 acc = psum_acc.tile([P, NI], F32, name="acc")
                 tiles["acc", block] = acc
-            for c in range(PASSES):
+            for c in some:
                 nc.tensor.matmul_mx(
                     out=tiles["acc", block][:],
                     lhsT=tiles["codes", n][:, c, :].bitcast(E5M2_X4),
@@ -420,13 +438,13 @@ def tile_capsulenetwork_pb_v_kernel(tc, p, Wr, s, grad_out, out):
             if live(step):
                 unit(step)
                 dot_ru(step)
-            if live(step - QL):
+            if live(step - QL) and step - QL < N_CHUNKS - 1:
                 quantise(step - QL)
             if 0 <= step - W_START - 2 < W_PASSES:
                 quantise_weights(step - W_START - 2)
             if live(step + 2) and not HALVE_LATE:
                 halve_squares(step + 2)
-            if ADDED and live(step - 1):
+            if live(step - 1):
                 add(step - 1)
             if live(step):
                 bracket(step)
@@ -440,10 +458,9 @@ def tile_capsulenetwork_pb_v_kernel(tc, p, Wr, s, grad_out, out):
                 if step + 2 >= V_FIRST:
                     t_times_g(step + 2)
             if live(step - 1):
-                for c in range(ADDED, HALF):
+                for c in range(added(step - 1), HALF):
                     transpose_add(step - 1, c)
-                if ADDED:
-                    transpose_words(step - 1)
+                transpose_words(step - 1)
             if live(step):
                 to_tokens(step)
             if step > S_EARLY and live(step + SQ):
@@ -460,7 +477,7 @@ def tile_capsulenetwork_pb_v_kernel(tc, p, Wr, s, grad_out, out):
                 invert(step + 1)
                 sum_products(step + 1, 0)
                 sum_products(step + 1, 1)
-            for n in due[:MXM]:
+            for n in due[:MXM] if step < N_CHUNKS - 1 + QL else []:
                 multiply(n)
                 store(n)
             if live(step):
@@ -479,6 +496,12 @@ def tile_capsulenetwork_pb_v_kernel(tc, p, Wr, s, grad_out, out):
                 transpose_add(step - 1, 3)
             if REG_LATE and 0 <= step - W_START < W_PASSES:
                 regroup_weights(step - W_START)
+            if step == N_CHUNKS - 1 + QL:
+                for half in range(2):
+                    quantise_half(N_CHUNKS - 1, half)
+                    multiply(N_CHUNKS - 1, range(half * HALF, (half + 1) * HALF))
+                store(N_CHUNKS - 1)
+                due = []
             for n in due[MXM:]:
                 multiply(n)
                 store(n)

@@ -50,10 +50,11 @@ COEF_G = True
 PB = 2
 SQ = 2
 REG_LATE = 1
+WB = 4
 FIRST_PIECES = 2
 WD = 3
 MXR = 2
-MXM = 1
+MXM = 2
 DSB = 3
 ADD_EARLY = 1
 ADD_LATE = 2
@@ -66,7 +67,8 @@ PLAIN_Q = 2
 PLAIN_DOT = 2
 PLAIN_TOK = True
 PLAIN_DS = 0
-TG_PAIRS = 2
+TG_EARLY = 2
+TG_LATE = 4
 V_FIRST = 2
 
 FLOPS = 2 * BATCH * CAPS * OUT_DIM * NI
@@ -84,7 +86,7 @@ def tile_capsulenetwork_pb_v_kernel(tc, p, Wr, s, grad_out, out):
             return stack.enter_context(tc.psum_pool(name=name, bufs=bufs))
 
         const = sbuf("const", 1)
-        w_raw = sbuf("w_raw", 4)
+        w_raw = sbuf("w_raw", WB)
         w_stage = sbuf("w_stage", 3)
         t_pool = sbuf("t_pool", T_AHEAD)
         g_pool = sbuf("g_pool", G_AHEAD)
@@ -149,8 +151,8 @@ def tile_capsulenetwork_pb_v_kernel(tc, p, Wr, s, grad_out, out):
         def regroup_weights(wp):
             w_grouped = w_stage.tile([P, N_PRIM, IN_DIM, PACK], BF16, name="w_grouped", align_bytes=64)
             nc.scalar.copy(
-                out=w_grouped[:],
-                in_=tiles["w_loaded", wp][:].rearrange("row n (slot i) -> row n i slot", slot=PACK),
+                out=w_grouped[:].rearrange("row n (c i) slot -> row n c slot i", c=IN_DIM // PACK),
+                in_=tiles["w_loaded", wp][:].rearrange("row n (slot c i) -> row n c slot i", slot=PACK, c=IN_DIM // PACK),
             )
             tiles["w_grouped", wp] = w_grouped
 
@@ -201,15 +203,15 @@ def tile_capsulenetwork_pb_v_kernel(tc, p, Wr, s, grad_out, out):
             engine.tensor_tensor(
                 out=tg[:].rearrange("b j o -> b (j o)"), in0=tiles["t", n][:], in1=tiles["g", n][:], op=ALU.mult
             )
-            if TG_PAIRS == 0:
+            if tg_pairs(n) == 0:
                 tiles["tg_planes", n] = [tg[:, :, o] for o in range(OUT_DIM)]
                 return
-            tg_low = prods.tile([P, CAPS_CHUNK, TG_PAIRS], F32, name="tg_low")
+            tg_low = prods.tile([P, CAPS_CHUNK, tg_pairs(n)], F32, name="tg_low")
             engine.tensor_tensor(
-                out=tg_low[:], in0=tg[:, :, :TG_PAIRS], in1=tg[:, :, TG_PAIRS : 2 * TG_PAIRS], op=ALU.add
+                out=tg_low[:], in0=tg[:, :, :tg_pairs(n)], in1=tg[:, :, tg_pairs(n) : 2 * tg_pairs(n)], op=ALU.add
             )
-            tiles["tg_planes", n] = [tg[:, :, o] for o in range(2 * TG_PAIRS, OUT_DIM)] + [
-                tg_low[:, :, o] for o in range(TG_PAIRS)
+            tiles["tg_planes", n] = [tg[:, :, o] for o in range(2 * tg_pairs(n), OUT_DIM)] + [
+                tg_low[:, :, o] for o in range(tg_pairs(n))
             ]
 
         def turn(ps, plane_o, first, last, plain=False):
@@ -331,6 +333,9 @@ def tile_capsulenetwork_pb_v_kernel(tc, p, Wr, s, grad_out, out):
                 out_ap = product[:].rearrange("b c slot (j quad) -> b c j quad slot", quad=QUADS)
             tiles[name, n, half] = product
             nc.vector.tensor_tensor(out=out_ap, in0=in0, in1=in1, op=ALU.mult)
+
+        def tg_pairs(n):
+            return TG_LATE if n >= ADD_FROM else TG_EARLY
 
         def added(n):
             return ADD_LATE if n >= ADD_FROM else ADD_EARLY
@@ -509,5 +514,6 @@ def tile_capsulenetwork_pb_v_kernel(tc, p, Wr, s, grad_out, out):
                 load_g(step - 1 + G_AHEAD)
             if live(step - 1) and live(step - 1 + T_AHEAD):
                 load_t(step - 1 + T_AHEAD)
-            if 0 <= step - W_START + WD < W_PASSES:
-                load_weights(step - W_START + WD)
+            for wp in range(W_PASSES):
+                if step == max(wp + W_START - WD, -3):
+                    load_weights(wp)

@@ -50,12 +50,14 @@ COEF_G = True
 PB = 2
 SQ = 2
 REG_LATE = 1
+V_CAPS = 0
 WB = 4
 FIRST_PIECES = 2
 WD = 3
 MXR = 2
 MXM = 2
-DSB = 3
+DSB = 2
+QB = 2
 ADD_EARLY = 1
 ADD_LATE = 2
 ADD_FROM = 8
@@ -67,8 +69,8 @@ PLAIN_Q = 2
 PLAIN_DOT = 2
 PLAIN_TOK = True
 PLAIN_DS = 0
-TG_EARLY = 2
-TG_LATE = 4
+TG_EARLY = 4
+TG_LATE = 6
 V_FIRST = 2
 
 FLOPS = 2 * BATCH * CAPS * OUT_DIM * NI
@@ -97,19 +99,19 @@ def tile_capsulenetwork_pb_v_kernel(tc, p, Wr, s, grad_out, out):
         rounded = sbuf("rounded", QL)
         coded = sbuf("coded", MX_START + 1 - QL)
         results = sbuf("results", 2)
-        psum_q = psum("psum_q", 1)
+        psum_q = psum("psum_q", QB)
         psum_dot = psum("psum_dot", 1)
         psum_factors = psum("psum_factors", 2)
         psum_ds = psum("psum_ds", DSB)
-        psum_acc = psum("psum_acc", 4 - DSB)
+        psum_acc = psum("psum_acc", 5 - DSB - QB)
         stack.enter_context(tc.manual_schedule())
 
         ident = const.tile([P, P], F32, name="ident")
         make_identity(nc, ident[:])
         eps_col = const.tile([P, 1], F32, name="eps_col")
         nc.vector.memset(eps_col[:], SQ_EPS)
-        minus_one_col = const.tile([P, 1], F32, name="minus_one_col")
-        nc.vector.memset(minus_one_col[:], -1.0)
+        one_col = const.tile([P, 1], F32, name="one_col")
+        nc.vector.memset(one_col[:], 1.0)
         w_codes = const.tile([P, W_PASSES, NI], U32, name="w_codes", align_bytes=64)
         w_scales = const.tile([P, W_PASSES, NI], U8, name="w_scales", align_bytes=64)
         w_view = Wr.rearrange(
@@ -197,22 +199,33 @@ def tile_capsulenetwork_pb_v_kernel(tc, p, Wr, s, grad_out, out):
                 tt[:, :, o] for o in range(2 * TT_PAIRS, OUT_DIM)
             ]
 
-        def t_times_g(n):
-            engine = nc.vector if n < V_FIRST else nc.gpsimd
-            tg = scratch.tile([P, CAPS_CHUNK, OUT_DIM], F32, name="tg")
+        def products_of(n):
+            if ("tg", n) not in tiles:
+                tg = scratch.tile([P, CAPS_CHUNK, OUT_DIM], F32, name="tg")
+                tiles["tg", n] = tg
+            return tiles["tg", n]
+
+        def v_caps(n):
+            return CAPS_CHUNK if n < V_FIRST else V_CAPS
+
+        def t_times_g(n, engine, caps):
+            some = slice(caps.start * OUT_DIM, caps.stop * OUT_DIM)
             engine.tensor_tensor(
-                out=tg[:].rearrange("b j o -> b (j o)"), in0=tiles["t", n][:], in1=tiles["g", n][:], op=ALU.mult
+                out=products_of(n)[:].rearrange("b j o -> b (j o)")[:, some], in0=tiles["t", n][:, some],
+                in1=tiles["g", n][:, some], op=ALU.mult,
             )
-            if tg_pairs(n) == 0:
-                tiles["tg_planes", n] = [tg[:, :, o] for o in range(OUT_DIM)]
-                return
-            tg_low = prods.tile([P, CAPS_CHUNK, tg_pairs(n)], F32, name="tg_low")
-            engine.tensor_tensor(
-                out=tg_low[:], in0=tg[:, :, :tg_pairs(n)], in1=tg[:, :, tg_pairs(n) : 2 * tg_pairs(n)], op=ALU.add
-            )
-            tiles["tg_planes", n] = [tg[:, :, o] for o in range(2 * tg_pairs(n), OUT_DIM)] + [
-                tg_low[:, :, o] for o in range(tg_pairs(n))
-            ]
+
+        def halve_products(n):
+            tg = products_of(n)
+            pairs = tg_pairs(n)
+            planes = [tg[:, :, o] for o in range(2 * pairs, OUT_DIM)]
+            if pairs:
+                tg_low = prods.tile([P, CAPS_CHUNK, pairs], F32, name="tg_low")
+                nc.vector.tensor_tensor(
+                    out=tg_low[:], in0=tg[:, :, :pairs], in1=tg[:, :, pairs : 2 * pairs], op=ALU.add
+                )
+                planes += [tg_low[:, :, o] for o in range(pairs)]
+            tiles["tg_planes", n] = planes
 
         def turn(ps, plane_o, first, last, plain=False):
             if plain:
@@ -246,57 +259,44 @@ def tile_capsulenetwork_pb_v_kernel(tc, p, Wr, s, grad_out, out):
 
         def roots(n):
             q = tiles["q", n][:]
-            root = small.tile([P, P], F32, name="root")
-            nc.scalar.activation(out=root[:], in_=q, func=ACT.Sqrt, bias=eps_col[:])
-            tiles["root", n] = root
-
-        def denominator(n):
-            den = small.tile([P, P], F32, name="den")
-            nc.vector.scalar_tensor_tensor(
-                out=den[:], in0=tiles["q", n][:], scalar=1.0, in1=tiles["root", n][:], op0=ALU.add, op1=ALU.mult
-            )
-            tiles["den", n] = den
-
-        def invert(n):
-            ru = small.tile([P, P], F32, name="ru")
-            nc.vector.reciprocal(out=ru[:], in_=tiles["den", n][:])
-            tiles["ru", n] = ru
-
-        def r_and_h(n):
-            ru = tiles["ru", n][:]
             r = small.tile([P, P], F32, name="r")
-            nc.vector.scalar_tensor_tensor(
-                out=r[:], in0=tiles["q", n][:], scalar=1.0, in1=ru, op0=ALU.add, op1=ALU.mult
-            )
-            h_coef = small.tile([P, 2, P], F32, name="h_coef")
-            nc.vector.tensor_tensor(out=h_coef[:, 0, :], in0=tiles["q", n][:], in1=ru, op=ALU.mult)
-            tiles["r", n] = r
-            tiles["h_coef", n] = h_coef
-
-        def corrections(n):
+            nc.scalar.activation(out=r[:], in_=q, func=ACT.Abs_reciprocal_sqrt, bias=eps_col[:])
+            root_u = small.tile([P, P], F32, name="root_u")
+            nc.scalar.activation(out=root_u[:], in_=q, func=ACT.Abs_reciprocal_sqrt, bias=one_col[:])
             eps_rr = small.tile([P, P], F32, name="eps_rr")
-            nc.scalar.activation(out=eps_rr[:], in_=tiles["r", n][:], func=ACT.Square, scale=SQ_EPS**0.5)
-            minus_qrr = small.tile([P, P], F32, name="minus_qrr")
-            nc.scalar.activation(out=minus_qrr[:], in_=eps_rr[:], func=ACT.Identity, bias=minus_one_col[:])
-            tiles["minus_qrr", n] = minus_qrr
+            nc.scalar.activation(out=eps_rr[:], in_=r[:], func=ACT.Square, scale=SQ_EPS**0.5)
+            two_u = small.tile([P, P], F32, name="two_u")
+            nc.scalar.activation(out=two_u[:], in_=root_u[:], func=ACT.Square, scale=2.0**0.5)
+            tiles["r", n] = r
+            tiles["two_u", n] = two_u
+            tiles["eps_rr", n] = eps_rr
 
-        def unit(n):
-            u = small.tile([P, P], F32, name="u")
-            nc.vector.tensor_tensor(out=u[:], in0=tiles["root", n][:], in1=tiles["ru", n][:], op=ALU.mult)
-            tiles["u", n] = u
+        def r_times_u(n):
+            two_ru = small.tile([P, P], F32, name="two_ru")
+            nc.vector.tensor_tensor(out=two_ru[:], in0=tiles["r", n][:], in1=tiles["two_u", n][:], op=ALU.mult)
+            tiles["two_ru", n] = two_ru
+
+        def h_factor(n):
+            h_coef = small.tile([P, 2, P], F32, name="h_coef")
+            nc.vector.scalar_tensor_tensor(
+                out=h_coef[:, 0, :], in0=tiles["q", n][:], scalar=0.5, in1=tiles["two_ru", n][:],
+                op0=ALU.mult, op1=ALU.mult,
+            )
+            tiles["h_coef", n] = h_coef
 
         def bracket(n):
             in_brackets = small.tile([P, P], F32, name="in_brackets")
             nc.vector.scalar_tensor_tensor(
-                out=in_brackets[:], in0=tiles["u", n][:], scalar=2.0, in1=tiles["minus_qrr", n][:],
-                op0=ALU.mult, op1=ALU.add,
+                out=in_brackets[:], in0=tiles["two_u", n][:], scalar=-1.0, in1=tiles["eps_rr", n][:],
+                op0=ALU.add, op1=ALU.add,
             )
             tiles["in_brackets", n] = in_brackets
 
         def dot_ru(n):
             dru = small.tile([P, P], F32, name="dru")
-            nc.vector.tensor_tensor(
-                out=dru[:], in0=tiles["dot", n][:], in1=tiles["ru", n][:], op=ALU.mult
+            nc.vector.scalar_tensor_tensor(
+                out=dru[:], in0=tiles["dot", n][:], scalar=0.5, in1=tiles["two_ru", n][:],
+                op0=ALU.mult, op1=ALU.mult,
             )
             tiles["dru", n] = dru
 
@@ -441,16 +441,20 @@ def tile_capsulenetwork_pb_v_kernel(tc, p, Wr, s, grad_out, out):
         for step in range(-3, N_CHUNKS + 3):
             due = [n for n in range(N_CHUNKS) if mx_step(n) == step]
             if live(step):
-                unit(step)
-                dot_ru(step)
+                r_times_u(step)
             if live(step - QL) and step - QL < N_CHUNKS - 1:
                 quantise(step - QL)
+            if live(step):
+                h_factor(step)
+                dot_ru(step)
             if 0 <= step - W_START - 2 < W_PASSES:
                 quantise_weights(step - W_START - 2)
-            if live(step + 2) and not HALVE_LATE:
-                halve_squares(step + 2)
             if live(step - 1):
                 add(step - 1)
+            if live(step + 1) and step + 1 >= V_FIRST:
+                halve_products(step + 1)
+            if live(step + 2) and step + 2 >= V_FIRST and V_CAPS:
+                t_times_g(step + 2, nc.vector, slice(CAPS_CHUNK - V_CAPS, CAPS_CHUNK))
             if live(step):
                 bracket(step)
                 coefficient(step)
@@ -460,8 +464,8 @@ def tile_capsulenetwork_pb_v_kernel(tc, p, Wr, s, grad_out, out):
             if live(step + 2):
                 if HALVE_LATE:
                     halve_squares(step + 2)
-                if step + 2 >= V_FIRST:
-                    t_times_g(step + 2)
+                if v_caps(step + 2) < CAPS_CHUNK:
+                    t_times_g(step + 2, nc.gpsimd, slice(0, CAPS_CHUNK - v_caps(step + 2)))
             if live(step - 1):
                 for c in range(added(step - 1), HALF):
                     transpose_add(step - 1, c)
@@ -474,12 +478,9 @@ def tile_capsulenetwork_pb_v_kernel(tc, p, Wr, s, grad_out, out):
                 regroup_weights(step - W_START)
             if live(step - 1):
                 scale(step - 1, 0, 1)
-            if live(step + 1):
-                denominator(step + 1)
             if live(step - 1):
                 scale(step - 1, 1, 1)
             if live(step + 1):
-                invert(step + 1)
                 sum_products(step + 1, 0)
                 sum_products(step + 1, 1)
             for n in due[:MXM] if step < N_CHUNKS - 1 + QL else []:
@@ -487,15 +488,13 @@ def tile_capsulenetwork_pb_v_kernel(tc, p, Wr, s, grad_out, out):
                 store(n)
             if live(step):
                 scale(step, 0, 0)
-            if live(step + 1):
-                r_and_h(step + 1)
-                corrections(step + 1)
             if step <= S_EARLY and live(step + SQ):
                 squares(step + SQ)
             if live(step):
                 scale(step, 1, 0)
             if 0 <= step + 2 < V_FIRST:
-                t_times_g(step + 2)
+                t_times_g(step + 2, nc.vector, slice(0, CAPS_CHUNK))
+                halve_products(step + 2)
             if live(step - 1):
                 transpose_add(step - 1, 2)
                 transpose_add(step - 1, 3)

@@ -28,50 +28,22 @@ CAPS_CHUNK = P
 COLS = CAPS_CHUNK * OUT_DIM
 PASSES = COLS // K_PASS
 HALF = PASSES // 2
-HALVES = CAPS // CAPS_CHUNK
-N_CHUNKS = (BATCH // P) * HALVES
+CHUNKS_BLOCK = CAPS // CAPS_CHUNK
+N_CHUNKS = (BATCH // P) * CHUNKS_BLOCK
+LAST = N_CHUNKS - 1
 W_PASSES = CAPS * OUT_DIM // K_PASS
 CAPS_PASS = K_PASS // OUT_DIM
 QUADS = OUT_DIM // PACK
-W_STEP = 2
 
-NATURAL = (False, True)
-W_START = 0
-MX_START = W_START + 9
+W_AHEAD = 4
+MX_START = W_PASSES + 1
+QUANT_LAG = 3
+CODED = MX_START + 1 - QUANT_LAG
 
-T_AHEAD = 5
-G_AHEAD = 5
-PLANES = True
-TG_BUFS = 2
-QL = 3
-HALVE_LATE = False
-SCB = 2
-COEF_G = True
-PB = 2
-SQ = 2
-REG_LATE = 1
-V_CAPS = 0
-WB = 4
-FIRST_PIECES = 2
-WD = 3
-MXR = 2
-MXM = 2
-DSB = 2
-QB = 2
-ADD_EARLY = 1
-ADD_LATE = 2
-ADD_FROM = 8
-S_EARLY = -9
-TT_PAIRS = 0
-PLAIN_FROM = 0
-PLAIN_TO = 0
-PLAIN_Q = 2
-PLAIN_DOT = 2
-PLAIN_TOK = True
-PLAIN_DS = 0
-TG_EARLY = 4
-TG_LATE = 6
+AHEAD = 5
 V_FIRST = 2
+LATE = 10
+PAIRS_EARLY, PAIRS_LATE = 2, 6
 
 FLOPS = 2 * BATCH * CAPS * OUT_DIM * NI
 BYTES = BATCH * CAPS * OUT_DIM * (4 + 2) + NI * CAPS * OUT_DIM * 2 + BATCH * NI * 4
@@ -88,22 +60,21 @@ def tile_capsulenetwork_pb_v_kernel(tc, p, Wr, s, grad_out, out):
             return stack.enter_context(tc.psum_pool(name=name, bufs=bufs))
 
         const = sbuf("const", 1)
-        w_raw = sbuf("w_raw", WB)
+        w_raw = sbuf("w_raw", W_AHEAD + 1)
         w_stage = sbuf("w_stage", 3)
-        t_pool = sbuf("t_pool", T_AHEAD)
-        g_pool = sbuf("g_pool", G_AHEAD)
-        prods = sbuf("prods", PB)
-        scratch = sbuf("scratch", TG_BUFS)
+        t_pool = sbuf("t_pool", AHEAD)
+        g_pool = sbuf("g_pool", AHEAD)
+        planes_pool = sbuf("planes_pool", 2)
         small = sbuf("small", 2)
-        scaled = sbuf("scaled", SCB)
-        rounded = sbuf("rounded", QL)
-        coded = sbuf("coded", MX_START + 1 - QL)
+        scaled = sbuf("scaled", 2)
+        rounded = sbuf("rounded", QUANT_LAG)
+        coded = sbuf("coded", CODED)
         results = sbuf("results", 2)
-        psum_q = psum("psum_q", QB)
+        psum_q = psum("psum_q", 1)
         psum_dot = psum("psum_dot", 1)
         psum_factors = psum("psum_factors", 2)
-        psum_ds = psum("psum_ds", DSB)
-        psum_acc = psum("psum_acc", 5 - DSB - QB)
+        psum_ds = psum("psum_ds", 2)
+        psum_acc = psum("psum_acc", 2)
         stack.enter_context(tc.manual_schedule())
 
         ident = const.tile([P, P], F32, name="ident")
@@ -121,40 +92,45 @@ def tile_capsulenetwork_pb_v_kernel(tc, p, Wr, s, grad_out, out):
         tiles = {}
 
         def rows_of(n):
-            tokens = slice((n // HALVES) * P, (n // HALVES + 1) * P)
-            caps = slice((n % HALVES) * CAPS_CHUNK, (n % HALVES + 1) * CAPS_CHUNK)
+            tokens = slice((n // CHUNKS_BLOCK) * P, (n // CHUNKS_BLOCK + 1) * P)
+            caps = slice((n % CHUNKS_BLOCK) * CAPS_CHUNK, (n % CHUNKS_BLOCK + 1) * CAPS_CHUNK)
             return tokens, caps
+
+        def pieces_of(n):
+            pieces = 2 if n == 0 else 1
+            wide = CAPS_CHUNK // pieces
+            return [slice(piece * wide, (piece + 1) * wide) for piece in range(pieces)]
 
         def load_t(n):
             tokens, caps = rows_of(n)
-            t_sb = t_pool.tile([P, COLS], F32, name="t_sb")
-            pieces = FIRST_PIECES if n == 0 else 1
-            wide = CAPS_CHUNK // pieces
-            for piece in range(pieces):
+            t_sb = t_pool.tile([P, CAPS_CHUNK, OUT_DIM], F32, name="t_sb")
+            for some in pieces_of(n):
                 nc.sync.dma_start(
-                    out=t_sb[:, piece * wide * OUT_DIM : (piece + 1) * wide * OUT_DIM],
-                    in_=s[tokens, caps.start + piece * wide : caps.start + (piece + 1) * wide, :].rearrange(
-                        "b j o -> b (j o)"
-                    ),
+                    out=t_sb[:, some].rearrange("b j o -> b (j o)"),
+                    in_=s[tokens, caps.start + some.start : caps.start + some.stop, :].rearrange("b j o -> b (j o)"),
                 )
             tiles["t", n] = t_sb
 
         def load_g(n):
             tokens, caps = rows_of(n)
-            g_sb = g_pool.tile([P, COLS], BF16, name="g_sb")
-            nc.sync.dma_start(out=g_sb[:], in_=grad_out[tokens, caps, :].rearrange("b j o -> b (j o)"))
+            g_sb = g_pool.tile([P, CAPS_CHUNK, OUT_DIM], BF16, name="g_sb")
+            nc.sync.dma_start(
+                out=g_sb[:].rearrange("b j o -> b (j o)"),
+                in_=grad_out[tokens, caps, :].rearrange("b j o -> b (j o)"),
+            )
             tiles["g", n] = g_sb
 
         def load_weights(wp):
             w_loaded = w_raw.tile([P, N_PRIM, PACK * IN_DIM], BF16, name="w_loaded")
-            nc.scalar.dma_start(out=w_loaded[:], in_=w_view[wp])
+            queue = nc.sync if wp % 2 else nc.scalar
+            queue.dma_start(out=w_loaded[:], in_=w_view[wp])
             tiles["w_loaded", wp] = w_loaded
 
         def regroup_weights(wp):
             w_grouped = w_stage.tile([P, N_PRIM, IN_DIM, PACK], BF16, name="w_grouped", align_bytes=64)
             nc.scalar.copy(
-                out=w_grouped[:].rearrange("row n (c i) slot -> row n c slot i", c=IN_DIM // PACK),
-                in_=tiles["w_loaded", wp][:].rearrange("row n (slot c i) -> row n c slot i", slot=PACK, c=IN_DIM // PACK),
+                out=w_grouped[:].rearrange("row n (c i) slot -> row n c slot i", i=4),
+                in_=tiles["w_loaded", wp][:].rearrange("row n (slot c i) -> row n c slot i", slot=PACK, i=4),
             )
             tiles["w_grouped", wp] = w_grouped
 
@@ -166,96 +142,50 @@ def tile_capsulenetwork_pb_v_kernel(tc, p, Wr, s, grad_out, out):
             )
 
         def squares(n):
-            if PLANES:
-                ttp = prods.tile([P, QUADS, PACK, CAPS_CHUNK], F32, name="tt")
-                pieces = FIRST_PIECES if n == 0 else 1
-                wide = CAPS_CHUNK // pieces
-                for piece in range(pieces):
-                    some = slice(piece * wide, (piece + 1) * wide)
-                    nc.scalar.activation(
-                        out=ttp[:, :, :, some].rearrange("b quad slot j -> b quad j slot"),
-                        in_=tiles["t", n][:].rearrange("b (j quad slot) -> b quad j slot", quad=QUADS, slot=PACK)[
-                            :, :, some
-                        ],
-                        func=ACT.Square,
-                    )
-                tiles["tt", n] = ttp[:].rearrange("b quad slot j -> b j (quad slot)")
-            else:
-                tt = prods.tile([P, CAPS_CHUNK, OUT_DIM], F32, name="tt")
+            tt = planes_pool.tile([P, QUADS, PACK, CAPS_CHUNK], F32, name="tt")
+            for some in pieces_of(n):
                 nc.scalar.activation(
-                    out=tt[:].rearrange("b j o -> b (j o)"), in_=tiles["t", n][:], func=ACT.Square
+                    out=tt[:, :, :, some].rearrange("b quad slot j -> b quad j slot"),
+                    in_=tiles["t", n][:, some].rearrange("b j (quad slot) -> b quad j slot", quad=QUADS),
+                    func=ACT.Square,
                 )
-                tiles["tt", n] = tt
+            tiles["tt", n] = tt
 
-        def halve_squares(n):
-            if TT_PAIRS == 0:
-                return
-            tt = tiles["tt", n]
-            tt_low = prods.tile([P, CAPS_CHUNK, TT_PAIRS], F32, name="tt_low")
-            nc.vector.tensor_tensor(
-                out=tt_low[:], in0=tt[:, :, :TT_PAIRS], in1=tt[:, :, TT_PAIRS : 2 * TT_PAIRS], op=ALU.add
+        def t_times_g(n, engine):
+            tg = planes_pool.tile([P, CAPS_CHUNK, OUT_DIM], F32, name="tg")
+            engine.tensor_tensor(
+                out=tg[:].rearrange("b j o -> b (j o)"), in0=tiles["t", n][:].rearrange("b j o -> b (j o)"),
+                in1=tiles["g", n][:].rearrange("b j o -> b (j o)"), op=ALU.mult,
             )
-            tiles["tt_planes", n] = [tt_low[:, :, o] for o in range(TT_PAIRS)] + [
-                tt[:, :, o] for o in range(2 * TT_PAIRS, OUT_DIM)
+            tiles["tg", n] = tg
+
+        def add_pairs(n):
+            tg = tiles["tg", n]
+            pairs = PAIRS_LATE if n >= LATE else PAIRS_EARLY
+            tg_sums = planes_pool.tile([P, CAPS_CHUNK, pairs], F32, name="tg_sums")
+            nc.vector.tensor_tensor(
+                out=tg_sums[:], in0=tg[:, :, :pairs], in1=tg[:, :, pairs : 2 * pairs], op=ALU.add
+            )
+            tiles["dot_planes", n] = [tg[:, :, o] for o in range(2 * pairs, OUT_DIM)] + [
+                tg_sums[:, :, o] for o in range(pairs)
             ]
 
-        def products_of(n):
-            if ("tg", n) not in tiles:
-                tg = scratch.tile([P, CAPS_CHUNK, OUT_DIM], F32, name="tg")
-                tiles["tg", n] = tg
-            return tiles["tg", n]
+        def turn(out_ps, columns, start=True, stop=True):
+            nc.tensor.matmul(out=out_ps, lhsT=columns, rhs=ident[:], start=start, stop=stop, is_transpose=True)
 
-        def v_caps(n):
-            return CAPS_CHUNK if n < V_FIRST else V_CAPS
-
-        def t_times_g(n, engine, caps):
-            some = slice(caps.start * OUT_DIM, caps.stop * OUT_DIM)
-            engine.tensor_tensor(
-                out=products_of(n)[:].rearrange("b j o -> b (j o)")[:, some], in0=tiles["t", n][:, some],
-                in1=tiles["g", n][:, some], op=ALU.mult,
-            )
-
-        def halve_products(n):
-            tg = products_of(n)
-            pairs = tg_pairs(n)
-            planes = [tg[:, :, o] for o in range(2 * pairs, OUT_DIM)]
-            if pairs:
-                tg_low = prods.tile([P, CAPS_CHUNK, pairs], F32, name="tg_low")
-                nc.vector.tensor_tensor(
-                    out=tg_low[:], in0=tg[:, :, :pairs], in1=tg[:, :, pairs : 2 * pairs], op=ALU.add
-                )
-                planes += [tg_low[:, :, o] for o in range(pairs)]
-            tiles["tg_planes", n] = planes
-
-        def turn(ps, plane_o, first, last, plain=False):
-            if plain:
-                nc.tensor.matmul(out=ps, lhsT=plane_o, rhs=ident[:], start=first, stop=last)
-            else:
-                nc.tensor.matmul(out=ps, lhsT=plane_o, rhs=ident[:], start=first, stop=last, is_transpose=True)
-
-        def spread(o, total, some):
-            return (o + 1) * some // total > o * some // total
-
-        def warm(n):
-            return PLAIN_FROM <= n < PLAIN_TO
+        def turn_and_add(pool, name, planes):
+            sums = pool.tile([P, P], F32, name=name)
+            for o, plane in enumerate(planes):
+                turn(sums[:], plane, start=(o == 0), stop=(o == len(planes) - 1))
+            return sums
 
         def sum_squares(n):
-            q_ps = psum_q.tile([P, P], F32, name="q_ps")
-            planes = tiles["tt_planes", n] if TT_PAIRS else [tiles["tt", n][:, :, o] for o in range(OUT_DIM)]
-            for o, plane_o in enumerate(planes):
-                turn(q_ps[:], plane_o, o == 0, o == len(planes) - 1, warm(n) and spread(o, len(planes), PLAIN_Q))
-            tiles["q", n] = q_ps
+            tt = tiles["tt", n]
+            planes = [tt[:, quad, slot, :] for quad in range(QUADS) for slot in range(PACK)]
+            tiles["q", n] = turn_and_add(psum_q, "q", planes)
 
-        def sum_products(n, part):
-            if part == 0:
-                dot_ps = psum_dot.tile([P, P], F32, name="dot_ps")
-                tiles["dot", n] = dot_ps
-            planes = tiles["tg_planes", n]
-            for o in range(part * len(planes) // 2, (part + 1) * len(planes) // 2):
-                turn(
-                    tiles["dot", n][:], planes[o], o == 0, o == len(planes) - 1,
-                    warm(n) and spread(o, len(planes), PLAIN_DOT),
-                )
+        def sum_products(n):
+            tiles["dot", n] = turn_and_add(psum_dot, "dot", tiles["dot_planes", n])
 
         def roots(n):
             q = tiles["q", n][:]
@@ -268,21 +198,28 @@ def tile_capsulenetwork_pb_v_kernel(tc, p, Wr, s, grad_out, out):
             two_u = small.tile([P, P], F32, name="two_u")
             nc.scalar.activation(out=two_u[:], in_=root_u[:], func=ACT.Square, scale=2.0**0.5)
             tiles["r", n] = r
-            tiles["two_u", n] = two_u
             tiles["eps_rr", n] = eps_rr
+            tiles["two_u", n] = two_u
 
         def r_times_u(n):
             two_ru = small.tile([P, P], F32, name="two_ru")
             nc.vector.tensor_tensor(out=two_ru[:], in0=tiles["r", n][:], in1=tiles["two_u", n][:], op=ALU.mult)
             tiles["two_ru", n] = two_ru
 
-        def h_factor(n):
-            h_coef = small.tile([P, 2, P], F32, name="h_coef")
+        def half_product(sums, two_ru, product):
             nc.vector.scalar_tensor_tensor(
-                out=h_coef[:, 0, :], in0=tiles["q", n][:], scalar=0.5, in1=tiles["two_ru", n][:],
-                op0=ALU.mult, op1=ALU.mult,
+                out=product, in0=sums[:], scalar=0.5, in1=two_ru[:], op0=ALU.mult, op1=ALU.mult
             )
-            tiles["h_coef", n] = h_coef
+
+        def h_factor(n):
+            factors = small.tile([P, 2, P], F32, name="factors")
+            half_product(tiles["q", n], tiles["two_ru", n], factors[:, 0, :])
+            tiles["factors", n] = factors
+
+        def dot_ru(n):
+            dru = small.tile([P, P], F32, name="dru")
+            half_product(tiles["dot", n], tiles["two_ru", n], dru[:])
+            tiles["dru", n] = dru
 
         def bracket(n):
             in_brackets = small.tile([P, P], F32, name="in_brackets")
@@ -292,138 +229,111 @@ def tile_capsulenetwork_pb_v_kernel(tc, p, Wr, s, grad_out, out):
             )
             tiles["in_brackets", n] = in_brackets
 
-        def dot_ru(n):
-            dru = small.tile([P, P], F32, name="dru")
-            nc.vector.scalar_tensor_tensor(
-                out=dru[:], in0=tiles["dot", n][:], scalar=0.5, in1=tiles["two_ru", n][:],
-                op0=ALU.mult, op1=ALU.mult,
-            )
-            tiles["dru", n] = dru
-
         def coefficient(n):
-            (nc.gpsimd if COEF_G else nc.vector).tensor_tensor(
-                out=tiles["h_coef", n][:, 1, :], in0=tiles["in_brackets", n][:], in1=tiles["dru", n][:],
+            nc.gpsimd.tensor_tensor(
+                out=tiles["factors", n][:, 1, :], in0=tiles["in_brackets", n][:], in1=tiles["dru", n][:],
                 op=ALU.mult,
             )
 
         def to_tokens(n):
             by_token = psum_factors.tile([P, 2, P], F32, name="by_token")
             for which in range(2):
-                turn(by_token[:, which, :], tiles["h_coef", n][:, which, :], True, True, warm(n) and PLAIN_TOK)
+                turn(by_token[:, which, :], tiles["factors", n][:, which, :])
             tiles["by_token", n] = by_token
 
-        def scale(n, which, half):
-            name = ("hg", "ct")[which]
-            some = slice(half * HALF, (half + 1) * HALF)
-            in0 = tiles[("g", "t")[which], n][:].rearrange(
-                "b (c j quad slot) -> b c j quad slot", c=PASSES, quad=QUADS, slot=PACK
-            )[:, some]
-            in1 = (
-                tiles["by_token", n][:, which, :]
-                .rearrange("b (c j) -> b c j", c=PASSES)[:, some]
-                .unsqueeze(3)
-                .unsqueeze(4)
-                .to_broadcast([P, HALF, CAPS_PASS, QUADS, PACK])
-            )
-            if NATURAL[which] or (half == 0 and added(n)):
-                product = scaled.tile([P, HALF, P, PACK], F32, name=name + "_k")
-                out_ap = product[:].rearrange("b c (j quad) slot -> b c j quad slot", quad=QUADS)
-            else:
-                product = scaled.tile([P, HALF, PACK, P], F32, name=name)
-                out_ap = product[:].rearrange("b c slot (j quad) -> b c j quad slot", quad=QUADS)
-            tiles[name, n, half] = product
-            nc.vector.tensor_tensor(out=out_ap, in0=in0, in1=in1, op=ALU.mult)
+        def added_by_vector(n, first):
+            return first < HALF or n == LAST
 
-        def tg_pairs(n):
-            return TG_LATE if n >= ADD_FROM else TG_EARLY
+        def scale(n, first, last):
+            some = slice(first, last)
+            for which, name in enumerate(("hg", "ct")):
+                by_slot = name == "hg" and not added_by_vector(n, first)
+                if by_slot:
+                    product = scaled.tile([P, last - first, PACK, P], F32, name="hg_by_slot")
+                    in_order = product[:].rearrange("b c slot row -> b c row slot")
+                else:
+                    product = scaled.tile([P, last - first, P, PACK], F32, name=name)
+                    in_order = product[:]
+                nc.vector.tensor_tensor(
+                    out=in_order.rearrange("b c (j quad) slot -> b c j quad slot", quad=QUADS),
+                    in0=tiles[("g", "t")[which], n][:].rearrange(
+                        "b (c j) (quad slot) -> b c j quad slot", c=PASSES, quad=QUADS
+                    )[:, some],
+                    in1=tiles["by_token", n][:, which, :]
+                    .rearrange("b (c j) -> b c j", c=PASSES)[:, some]
+                    .unsqueeze(3)
+                    .unsqueeze(4)
+                    .to_broadcast([P, last - first, CAPS_PASS, QUADS, PACK]),
+                    op=ALU.mult,
+                )
+                tiles[name, n, first] = in_order
 
-        def added(n):
-            return ADD_LATE if n >= ADD_FROM else ADD_EARLY
-
-        def add(n):
-            ds_words = scaled.tile([P, added(n), P, PACK], BF16, name="ds_words", align_bytes=64)
+        def add(n, first, last):
+            ds_words = scaled.tile([P, last - first, P, PACK], BF16, name="ds_words", align_bytes=64)
             nc.vector.tensor_tensor(
-                out=ds_words[:], in0=tiles["hg", n, 0][:, :added(n)], in1=tiles["ct", n, 0][:, :added(n)], op=ALU.add
+                out=ds_words[:], in0=tiles["hg", n, first], in1=tiles["ct", n, first], op=ALU.add
             )
-            tiles["ds_words", n] = ds_words
+            tiles["ds_words", n, first] = ds_words
 
-        def grouped_of(n):
-            if ("grouped", n) not in tiles:
+        def transpose_words(n, first, last):
+            count = last - first
+            words = tiles["ds_words", n, first][:].rearrange("b c row slot -> b (c row slot)").bitcast(F32)
+            words = words.rearrange("b (c row pair) -> b c row pair", c=count, pair=2)
+            ds_t = psum_ds.tile([P, count, 2, P], F32, name="ds_t")
+            for c in range(count):
+                for pair in range(2):
+                    turn(ds_t[:, c, pair, :], words[:, c, :, pair])
+            if first == 0:
                 grouped = rounded.tile([P, PASSES, P, PACK], BF16, name="grouped", align_bytes=64)
                 tiles["grouped", n] = grouped
-            return tiles["grouped", n]
-
-        def transpose_words(n):
-            words = tiles["ds_words", n][:].rearrange("b c row slot -> b (c row slot)").bitcast(F32)
-            ds_t = psum_ds.tile([P, 2, 2, P], F32, name="ds_t")
-            for c in range(added(n)):
-                for u in range(2):
-                    turn(ds_t[:, c, u, :], words.rearrange("b (c row u) -> b c row u", u=2, c=added(n))[:, c, :, u], True, True)
             nc.scalar.copy(
-                out=grouped_of(n)[:, :added(n)].rearrange("row c b slot -> row (c b slot)").bitcast(F32)
-                .rearrange("row (c b u) -> row c b u", u=2, c=added(n)),
-                in_=ds_t[:, :added(n)].rearrange("row c u b -> row c b u"),
+                out=tiles["grouped", n][:, first:last].rearrange("row c b slot -> row (c b slot)").bitcast(F32)
+                .rearrange("row (c b pair) -> row c b pair", c=count, pair=2),
+                in_=ds_t[:].rearrange("row c pair b -> row c b pair"),
             )
 
-        def plane(name, which, n, half, ch, slot):
-            if NATURAL[which] or (half == 0 and added(n)):
-                return tiles[name, n, half][:, ch, :, slot]
-            return tiles[name, n, half][:, ch, slot, :]
-
-        def transpose_add(n, c):
-            half, ch = divmod(c, HALF)
-            ds_t = psum_ds.tile([P, PACK, P], F32, name="ds_t")
-            for slot in range(PACK):
-                turn(ds_t[:, slot, :], plane("hg", 0, n, half, ch, slot), True, False)
-                turn(
-                    ds_t[:, slot, :], plane("ct", 1, n, half, ch, slot), False, True,
-                    warm(n) and spread(slot, PACK, PLAIN_DS),
+        def transpose_add(n, first, last):
+            for c in range(last - first):
+                ds_t = psum_ds.tile([P, PACK, P], F32, name="ds_t")
+                for slot in range(PACK):
+                    turn(ds_t[:, slot, :], tiles["hg", n, first][:, c, :, slot], stop=False)
+                    turn(ds_t[:, slot, :], tiles["ct", n, first][:, c, :, slot], start=False)
+                nc.scalar.copy(
+                    out=tiles["grouped", n][:, first + c], in_=ds_t[:].rearrange("row slot b -> row b slot")
                 )
-            nc.scalar.copy(out=grouped_of(n)[:, c], in_=ds_t[:].rearrange("row slot b -> row b slot"))
 
-        def quantise_half(n, half):
-            some = slice(half * HALF, (half + 1) * HALF)
-            if half == 0:
+        def quantise(n, first, last):
+            if first == 0:
                 codes = coded.tile([P, PASSES, P], U32, name="codes", align_bytes=64)
                 scales = coded.tile([P, PASSES, P], U8, name="scales", align_bytes=64)
                 tiles["codes", n] = codes
                 tiles["scales", n] = scales
             nc.vector.quantize_mx(
-                out=tiles["codes", n][:, some].rearrange("row c b -> row (c b)").bitcast(E5M2_X4),
-                scales=tiles["scales", n][:, some].rearrange("row c b -> row (c b)"),
-                in_=tiles["grouped", n][:, some].rearrange("row c b slot -> row (c b slot)"),
+                out=tiles["codes", n][:, first:last].rearrange("row c b -> row (c b)").bitcast(E5M2_X4),
+                scales=tiles["scales", n][:, first:last].rearrange("row c b -> row (c b)"),
+                in_=tiles["grouped", n][:, first:last].rearrange("row c b slot -> row (c b slot)"),
             )
 
-        def quantise(n):
-            codes = coded.tile([P, PASSES, P], U32, name="codes", align_bytes=64)
-            scales = coded.tile([P, PASSES, P], U8, name="scales", align_bytes=64)
-            nc.vector.quantize_mx(
-                out=codes[:].rearrange("row c b -> row (c b)").bitcast(E5M2_X4),
-                scales=scales[:].rearrange("row c b -> row (c b)"),
-                in_=tiles["grouped", n][:].rearrange("row c b slot -> row (c b slot)"),
-            )
-            tiles["codes", n] = codes
-            tiles["scales", n] = scales
-
-        def multiply(n, some=range(PASSES)):
-            block, half = divmod(n, HALVES)
-            if half == 0 and 0 in some:
+        def multiply(n, first, last):
+            block, part = divmod(n, CHUNKS_BLOCK)
+            if part == 0 and first == 0:
                 acc = psum_acc.tile([P, NI], F32, name="acc")
                 tiles["acc", block] = acc
-            for c in some:
+            for c in range(first, last):
+                wp = part * PASSES + c
                 nc.tensor.matmul_mx(
                     out=tiles["acc", block][:],
                     lhsT=tiles["codes", n][:, c, :].bitcast(E5M2_X4),
                     lhsT_scale=tiles["scales", n][:, c, :],
-                    rhs=w_codes[:, half * PASSES + c, :].bitcast(E4M3_X4),
-                    rhs_scale=w_scales[:, half * PASSES + c, :],
-                    start=(half == 0 and c == 0),
-                    stop=(half == HALVES - 1 and c == PASSES - 1),
+                    rhs=w_codes[:, wp, :].bitcast(E4M3_X4),
+                    rhs_scale=w_scales[:, wp, :],
+                    start=(wp == 0),
+                    stop=(wp == W_PASSES - 1),
                 )
 
         def store(n):
-            block, half = divmod(n, HALVES)
-            if half == HALVES - 1:
+            block, part = divmod(n, CHUNKS_BLOCK)
+            if part == CHUNKS_BLOCK - 1:
                 result = results.tile([P, NI], F32, name="result")
                 nc.scalar.mul(out=result[:], in_=tiles["acc", block][:], mul=1.0 / CAPS)
                 nc.scalar.dma_start(out=out[block * P : (block + 1) * P].rearrange("b n i -> b (n i)"), in_=result[:])
@@ -432,87 +342,79 @@ def tile_capsulenetwork_pb_v_kernel(tc, p, Wr, s, grad_out, out):
             return 0 <= n < N_CHUNKS
 
         def mx_step(n):
-            return max(n + QL, MX_START + n // MXR)
+            return max(n + QUANT_LAG, MX_START + n // CHUNKS_BLOCK)
 
-        for n in range(T_AHEAD):
+        def second_half(n):
+            return [(HALF, PASSES)] if n < LAST else [(c, c + 1) for c in range(HALF, PASSES)]
+
+        for n in range(AHEAD):
             load_t(n)
-            if n < G_AHEAD:
-                load_g(n)
-        for step in range(-3, N_CHUNKS + 3):
+            load_g(n)
+        for step in range(-3, N_CHUNKS + QUANT_LAG):
             due = [n for n in range(N_CHUNKS) if mx_step(n) == step]
             if live(step):
                 r_times_u(step)
-            if live(step - QL) and step - QL < N_CHUNKS - 1:
-                quantise(step - QL)
+            if live(step - QUANT_LAG) and step - QUANT_LAG < LAST:
+                quantise(step - QUANT_LAG, 0, PASSES)
             if live(step):
                 h_factor(step)
                 dot_ru(step)
-            if 0 <= step - W_START - 2 < W_PASSES:
-                quantise_weights(step - W_START - 2)
+            if 0 <= step - 2 < W_PASSES:
+                quantise_weights(step - 2)
             if live(step - 1):
-                add(step - 1)
+                add(step - 1, 0, HALF)
             if live(step + 1) and step + 1 >= V_FIRST:
-                halve_products(step + 1)
-            if live(step + 2) and step + 2 >= V_FIRST and V_CAPS:
-                t_times_g(step + 2, nc.vector, slice(CAPS_CHUNK - V_CAPS, CAPS_CHUNK))
+                add_pairs(step + 1)
             if live(step):
                 bracket(step)
                 coefficient(step)
+            if step == 0:
+                to_tokens(0)
             if live(step + 1):
                 sum_squares(step + 1)
-                roots(step + 1)
-            if live(step + 2):
-                if HALVE_LATE:
-                    halve_squares(step + 2)
-                if v_caps(step + 2) < CAPS_CHUNK:
-                    t_times_g(step + 2, nc.gpsimd, slice(0, CAPS_CHUNK - v_caps(step + 2)))
-            if live(step - 1):
-                for c in range(added(step - 1), HALF):
-                    transpose_add(step - 1, c)
-                transpose_words(step - 1)
-            if live(step):
-                to_tokens(step)
-            if step > S_EARLY and live(step + SQ):
-                squares(step + SQ)
-            if not REG_LATE and 0 <= step - W_START < W_PASSES:
-                regroup_weights(step - W_START)
-            if live(step - 1):
-                scale(step - 1, 0, 1)
-            if live(step - 1):
-                scale(step - 1, 1, 1)
+            if step < 1 and live(step + 2):
+                squares(step + 2)
             if live(step + 1):
-                sum_products(step + 1, 0)
-                sum_products(step + 1, 1)
-            for n in due[:MXM] if step < N_CHUNKS - 1 + QL else []:
-                multiply(n)
-                store(n)
-            if live(step):
-                scale(step, 0, 0)
-            if step <= S_EARLY and live(step + SQ):
-                squares(step + SQ)
-            if live(step):
-                scale(step, 1, 0)
-            if 0 <= step + 2 < V_FIRST:
-                t_times_g(step + 2, nc.vector, slice(0, CAPS_CHUNK))
-                halve_products(step + 2)
+                roots(step + 1)
+            if live(step + 2) and step + 2 >= V_FIRST:
+                t_times_g(step + 2, nc.gpsimd)
             if live(step - 1):
-                transpose_add(step - 1, 2)
-                transpose_add(step - 1, 3)
-            if REG_LATE and 0 <= step - W_START < W_PASSES:
-                regroup_weights(step - W_START)
-            if step == N_CHUNKS - 1 + QL:
-                for half in range(2):
-                    quantise_half(N_CHUNKS - 1, half)
-                    multiply(N_CHUNKS - 1, range(half * HALF, (half + 1) * HALF))
-                store(N_CHUNKS - 1)
-                due = []
-            for n in due[MXM:]:
-                multiply(n)
-                store(n)
-            if live(step - 1) and live(step - 1 + G_AHEAD):
-                load_g(step - 1 + G_AHEAD)
-            if live(step - 1) and live(step - 1 + T_AHEAD):
-                load_t(step - 1 + T_AHEAD)
+                transpose_words(step - 1, 0, HALF)
+            if live(step) and step > 0:
+                to_tokens(step)
+            if step >= 1 and live(step + 2):
+                squares(step + 2)
+            if live(step - 1):
+                for first, last in second_half(step - 1):
+                    scale(step - 1, first, last)
+            if live(step + 1):
+                sum_products(step + 1)
+            if step < LAST + QUANT_LAG:
+                for n in due:
+                    multiply(n, 0, PASSES)
+                    store(n)
+            if live(step):
+                scale(step, 0, HALF)
+            if 0 <= step + 2 < V_FIRST:
+                t_times_g(step + 2, nc.vector)
+                add_pairs(step + 2)
+            if live(step - 1):
+                for first, last in second_half(step - 1):
+                    if added_by_vector(step - 1, first):
+                        add(step - 1, first, last)
+                        transpose_words(step - 1, first, last)
+                    else:
+                        transpose_add(step - 1, first, last)
+            if 0 <= step < W_PASSES:
+                regroup_weights(step)
+            if step == LAST + QUANT_LAG:
+                for first, last in [(0, HALF)] + second_half(LAST):
+                    quantise(LAST, first, last)
+                    multiply(LAST, first, last)
+                store(LAST)
             for wp in range(W_PASSES):
-                if step == max(wp + W_START - WD, -3):
+                if step == max(wp - W_AHEAD, -3):
                     load_weights(wp)
+            if live(step - 1) and live(step - 1 + AHEAD):
+                load_g(step - 1 + AHEAD)
+                load_t(step - 1 + AHEAD)

@@ -35,7 +35,7 @@ W_PASSES = CAPS * OUT_DIM // K_PASS
 CAPS_PASS = K_PASS // OUT_DIM
 QUADS = OUT_DIM // PACK
 
-W_AHEAD = 4
+W_AHEAD = 3
 MX_START = W_PASSES + 1
 QUANT_LAG = 3
 CODED = MX_START + 1 - QUANT_LAG
@@ -122,8 +122,7 @@ def tile_capsulenetwork_pb_v_kernel(tc, p, Wr, s, grad_out, out):
 
         def load_weights(wp):
             w_loaded = w_raw.tile([P, N_PRIM, PACK * IN_DIM], BF16, name="w_loaded")
-            queue = nc.sync if wp % 2 else nc.scalar
-            queue.dma_start(out=w_loaded[:], in_=w_view[wp])
+            nc.scalar.dma_start(out=w_loaded[:], in_=w_view[wp])
             tiles["w_loaded", wp] = w_loaded
 
         def regroup_weights(wp):
@@ -413,7 +412,7 @@ def tile_capsulenetwork_pb_v_kernel(tc, p, Wr, s, grad_out, out):
                     multiply(LAST, first, last)
                 store(LAST)
             for wp in range(W_PASSES):
-                if step == max(wp - W_AHEAD, -3):
+                if step == max(wp - W_AHEAD, -2):
                     load_weights(wp)
             if live(step - 1) and live(step - 1 + AHEAD):
                 load_g(step - 1 + AHEAD)

@@ -35,7 +35,7 @@ W_PASSES = CAPS * OUT_DIM // K_PASS
 CAPS_PASS = K_PASS // OUT_DIM
 QUADS = OUT_DIM // PACK
 
-W_AHEAD = 3
+W_AHEAD = 2
 MX_START = W_PASSES + 1
 QUANT_LAG = 3
 CODED = MX_START + 1 - QUANT_LAG
@@ -43,7 +43,7 @@ CODED = MX_START + 1 - QUANT_LAG
 AHEAD = 5
 V_FIRST = 2
 LATE = 10
-PAIRS_EARLY, PAIRS_LATE = 2, 6
+PAIRS = 6
 
 FLOPS = 2 * BATCH * CAPS * OUT_DIM * NI
 BYTES = BATCH * CAPS * OUT_DIM * (4 + 2) + NI * CAPS * OUT_DIM * 2 + BATCH * NI * 4
@@ -160,14 +160,11 @@ def tile_capsulenetwork_pb_v_kernel(tc, p, Wr, s, grad_out, out):
 
         def add_pairs(n):
             tg = tiles["tg", n]
-            pairs = PAIRS_LATE if n >= LATE else PAIRS_EARLY
-            tg_sums = planes_pool.tile([P, CAPS_CHUNK, pairs], F32, name="tg_sums")
+            tg_sums = planes_pool.tile([P, CAPS_CHUNK, PAIRS], F32, name="tg_sums")
             nc.vector.tensor_tensor(
-                out=tg_sums[:], in0=tg[:, :, :pairs], in1=tg[:, :, pairs : 2 * pairs], op=ALU.add
+                out=tg_sums[:], in0=tg[:, :, :PAIRS], in1=tg[:, :, PAIRS : 2 * PAIRS], op=ALU.add
             )
-            tiles["dot_planes", n] = [tg[:, :, o] for o in range(2 * pairs, OUT_DIM)] + [
-                tg_sums[:, :, o] for o in range(pairs)
-            ]
+            tiles["tg_sums", n] = tg_sums
 
         def turn(out_ps, columns, start=True, stop=True):
             nc.tensor.matmul(out=out_ps, lhsT=columns, rhs=ident[:], start=start, stop=stop, is_transpose=True)
@@ -184,7 +181,10 @@ def tile_capsulenetwork_pb_v_kernel(tc, p, Wr, s, grad_out, out):
             tiles["q", n] = turn_and_add(psum_q, "q", planes)
 
         def sum_products(n):
-            tiles["dot", n] = turn_and_add(psum_dot, "dot", tiles["dot_planes", n])
+            pairs = PAIRS if n >= LATE else 0
+            planes = [tiles["tg", n][:, :, o] for o in range(2 * pairs, OUT_DIM)]
+            planes += [tiles["tg_sums", n][:, :, o] for o in range(pairs)]
+            tiles["dot", n] = turn_and_add(psum_dot, "dot", planes)
 
         def roots(n):
             q = tiles["q", n][:]
@@ -362,7 +362,7 @@ def tile_capsulenetwork_pb_v_kernel(tc, p, Wr, s, grad_out, out):
                 quantise_weights(step - 2)
             if live(step - 1):
                 add(step - 1, 0, HALF)
-            if live(step + 1) and step + 1 >= V_FIRST:
+            if LATE <= step + 1 < N_CHUNKS:
                 add_pairs(step + 1)
             if live(step):
                 bracket(step)
@@ -396,7 +396,6 @@ def tile_capsulenetwork_pb_v_kernel(tc, p, Wr, s, grad_out, out):
                 scale(step, 0, HALF)
             if 0 <= step + 2 < V_FIRST:
                 t_times_g(step + 2, nc.vector)
-                add_pairs(step + 2)
             if live(step - 1):
                 for first, last in second_half(step - 1):
                     if added_by_vector(step - 1, first):
@@ -411,9 +410,8 @@ def tile_capsulenetwork_pb_v_kernel(tc, p, Wr, s, grad_out, out):
                     quantise(LAST, first, last)
                     multiply(LAST, first, last)
                 store(LAST)
-            for wp in range(W_PASSES):
-                if step == max(wp - W_AHEAD, -2):
-                    load_weights(wp)
+            if 0 <= step + W_AHEAD < W_PASSES:
+                load_weights(step + W_AHEAD)
             if live(step - 1) and live(step - 1 + AHEAD):
                 load_g(step - 1 + AHEAD)
                 load_t(step - 1 + AHEAD)

from contextlib import ExitStack

import concourse.mybir as mybir
from concourse.masks import make_identity

F32 = mybir.dt.float32
BF16 = mybir.dt.bfloat16
U32 = mybir.dt.uint32
U8 = mybir.dt.uint8
E5M2_X4 = mybir.dt.float8_e5m2_x4
E4M3_X4 = mybir.dt.float8_e4m3fn_x4
ACT = mybir.ActivationFunctionType
ALU = mybir.AluOpType

P = 128
PACK = 4
K_PASS = P * PACK

BATCH = 1024
N_PRIM = 32
IN_DIM = 16
CAPS = 256
OUT_DIM = 16
NI = N_PRIM * IN_DIM
SQ_EPS = 1e-8

CAPS_CHUNK = P
COLS = CAPS_CHUNK * OUT_DIM
PASSES = COLS // K_PASS
HALF = PASSES // 2
CHUNKS_BLOCK = CAPS // CAPS_CHUNK
N_CHUNKS = (BATCH // P) * CHUNKS_BLOCK
LAST = N_CHUNKS - 1
W_PASSES = CAPS * OUT_DIM // K_PASS
CAPS_PASS = K_PASS // OUT_DIM
QUADS = OUT_DIM // PACK

W_AHEAD = 2
MX_START = W_PASSES + 1
QUANT_LAG = 3
CODED = MX_START + 1 - QUANT_LAG

AHEAD = 5
V_FIRST = 2
LATE = 10
PAIRS = 6

FLOPS = 2 * BATCH * CAPS * OUT_DIM * NI
BYTES = BATCH * CAPS * OUT_DIM * (4 + 2) + NI * CAPS * OUT_DIM * 2 + BATCH * NI * 4


def tile_capsulenetwork_pb_v_kernel(tc, p, Wr, s, grad_out, out):
    nc = tc.nc
    with ExitStack() as stack:

        def sbuf(name, bufs):
            return stack.enter_context(tc.tile_pool(name=name, bufs=bufs))

        def psum(name, bufs):
            return stack.enter_context(tc.psum_pool(name=name, bufs=bufs))

        const = sbuf("const", 1)
        w_raw = sbuf("w_raw", W_AHEAD + 1)
        w_stage = sbuf("w_stage", 3)
        t_pool = sbuf("t_pool", AHEAD)
        g_pool = sbuf("g_pool", AHEAD)
        planes_pool = sbuf("planes_pool", 2)
        small = sbuf("small", 2)
        scaled = sbuf("scaled", 2)
        rounded = sbuf("rounded", QUANT_LAG)
        coded = sbuf("coded", CODED)
        results = sbuf("results", 2)
        psum_q = psum("psum_q", 1)
        psum_dot = psum("psum_dot", 1)
        psum_factors = psum("psum_factors", 2)
        psum_ds = psum("psum_ds", 2)
        psum_acc = psum("psum_acc", 2)
        stack.enter_context(tc.manual_schedule())

        ident = const.tile([P, P], F32, name="ident")
        make_identity(nc, ident[:])
        eps_col = const.tile([P, 1], F32, name="eps_col")
        nc.vector.memset(eps_col[:], SQ_EPS)
        one_col = const.tile([P, 1], F32, name="one_col")
        nc.vector.memset(one_col[:], 1.0)
        w_codes = const.tile([P, W_PASSES, NI], U32, name="w_codes", align_bytes=64)
        w_scales = const.tile([P, W_PASSES, NI], U8, name="w_scales", align_bytes=64)
        w_view = Wr.rearrange(
            "n (wp j) (quad slot) i -> wp (j quad) n (slot i)", wp=W_PASSES, quad=QUADS
        )

        tiles = {}

        def rows_of(n):
            tokens = slice((n // CHUNKS_BLOCK) * P, (n // CHUNKS_BLOCK + 1) * P)
            caps = slice((n % CHUNKS_BLOCK) * CAPS_CHUNK, (n % CHUNKS_BLOCK + 1) * CAPS_CHUNK)
            return tokens, caps

        def pieces_of(n):
            pieces = 2 if n == 0 else 1
            wide = CAPS_CHUNK // pieces
            return [slice(piece * wide, (piece + 1) * wide) for piece in range(pieces)]

        def load_t(n):
            tokens, caps = rows_of(n)
            t_sb = t_pool.tile([P, CAPS_CHUNK, OUT_DIM], F32, name="t_sb")
            for some in pieces_of(n):
                nc.sync.dma_start(
                    out=t_sb[:, some].rearrange("b j o -> b (j o)"),
                    in_=s[tokens, caps.start + some.start : caps.start + some.stop, :].rearrange("b j o -> b (j o)"),
                )
            tiles["t", n] = t_sb

        def load_g(n):
            tokens, caps = rows_of(n)
            g_sb = g_pool.tile([P, CAPS_CHUNK, OUT_DIM], BF16, name="g_sb")
            nc.sync.dma_start(
                out=g_sb[:].rearrange("b j o -> b (j o)"),
                in_=grad_out[tokens, caps, :].rearrange("b j o -> b (j o)"),
            )
            tiles["g", n] = g_sb

        def load_weights(wp):
            w_loaded = w_raw.tile([P, N_PRIM, PACK * IN_DIM], BF16, name="w_loaded")
            nc.scalar.dma_start(out=w_loaded[:], in_=w_view[wp])
            tiles["w_loaded", wp] = w_loaded

        def regroup_weights(wp):
            w_grouped = w_stage.tile([P, N_PRIM, IN_DIM, PACK], BF16, name="w_grouped", align_bytes=64)
            nc.scalar.copy(
                out=w_grouped[:].rearrange("row n (c i) slot -> row n c slot i", i=4),
                in_=tiles["w_loaded", wp][:].rearrange("row n (slot c i) -> row n c slot i", slot=PACK, i=4),
            )
            tiles["w_grouped", wp] = w_grouped

        def quantise_weights(wp):
            nc.vector.quantize_mx(
                out=w_codes[:, wp, :].bitcast(E4M3_X4),
                scales=w_scales[:, wp, :],
                in_=tiles["w_grouped", wp][:].rearrange("row n i slot -> row (n i slot)"),
            )

        def squares(n):
            tt = planes_pool.tile([P, QUADS, PACK, CAPS_CHUNK], F32, name="tt")
            for some in pieces_of(n):
                nc.scalar.activation(
                    out=tt[:, :, :, some].rearrange("b quad slot j -> b quad j slot"),
                    in_=tiles["t", n][:, some].rearrange("b j (quad slot) -> b quad j slot", quad=QUADS),
                    func=ACT.Square,
                )
            tiles["tt", n] = tt

        def t_times_g(n, engine):
            tg = planes_pool.tile([P, CAPS_CHUNK, OUT_DIM], F32, name="tg")
            engine.tensor_tensor(
                out=tg[:].rearrange("b j o -> b (j o)"), in0=tiles["t", n][:].rearrange("b j o -> b (j o)"),
                in1=tiles["g", n][:].rearrange("b j o -> b (j o)"), op=ALU.mult,
            )
            tiles["tg", n] = tg

        def add_pairs(n):
            tg = tiles["tg", n]
            tg_sums = planes_pool.tile([P, CAPS_CHUNK, PAIRS], F32, name="tg_sums")
            nc.vector.tensor_tensor(
                out=tg_sums[:], in0=tg[:, :, :PAIRS], in1=tg[:, :, PAIRS : 2 * PAIRS], op=ALU.add
            )
            tiles["tg_sums", n] = tg_sums

        def turn(out_ps, columns, start=True, stop=True):
            nc.tensor.matmul(out=out_ps, lhsT=columns, rhs=ident[:], start=start, stop=stop, is_transpose=True)

        def turn_and_add(pool, name, planes):
            sums = pool.tile([P, P], F32, name=name)
            for o, plane in enumerate(planes):
                turn(sums[:], plane, start=(o == 0), stop=(o == len(planes) - 1))
            return sums

        def sum_squares(n):
            tt = tiles["tt", n]
            planes = [tt[:, quad, slot, :] for quad in range(QUADS) for slot in range(PACK)]
            tiles["q", n] = turn_and_add(psum_q, "q", planes)

        def sum_products(n):
            pairs = PAIRS if n >= LATE else 0
            planes = [tiles["tg", n][:, :, o] for o in range(2 * pairs, OUT_DIM)]
            planes += [tiles["tg_sums", n][:, :, o] for o in range(pairs)]
            tiles["dot", n] = turn_and_add(psum_dot, "dot", planes)

        def roots(n):
            q = tiles["q", n][:]
            r = small.tile([P, P], F32, name="r")
            nc.scalar.activation(out=r[:], in_=q, func=ACT.Abs_reciprocal_sqrt, bias=eps_col[:])
            root_u = small.tile([P, P], F32, name="root_u")
            nc.scalar.activation(out=root_u[:], in_=q, func=ACT.Abs_reciprocal_sqrt, bias=one_col[:])
            eps_rr = small.tile([P, P], F32, name="eps_rr")
            nc.scalar.activation(out=eps_rr[:], in_=r[:], func=ACT.Square, scale=SQ_EPS**0.5)
            two_u = small.tile([P, P], F32, name="two_u")
            nc.scalar.activation(out=two_u[:], in_=root_u[:], func=ACT.Square, scale=2.0**0.5)
            tiles["r", n] = r
            tiles["eps_rr", n] = eps_rr
            tiles["two_u", n] = two_u

        def r_times_u(n):
            two_ru = small.tile([P, P], F32, name="two_ru")
            nc.vector.tensor_tensor(out=two_ru[:], in0=tiles["r", n][:], in1=tiles["two_u", n][:], op=ALU.mult)
            tiles["two_ru", n] = two_ru

        def half_product(sums, two_ru, product):
            nc.vector.scalar_tensor_tensor(
                out=product, in0=sums[:], scalar=0.5, in1=two_ru[:], op0=ALU.mult, op1=ALU.mult
            )

        def h_factor(n):
            factors = small.tile([P, 2, P], F32, name="factors")
            half_product(tiles["q", n], tiles["two_ru", n], factors[:, 0, :])
            tiles["factors", n] = factors

        def dot_ru(n):
            dru = small.tile([P, P], F32, name="dru")
            half_product(tiles["dot", n], tiles["two_ru", n], dru[:])
            tiles["dru", n] = dru

        def bracket(n):
            in_brackets = small.tile([P, P], F32, name="in_brackets")
            nc.vector.scalar_tensor_tensor(
                out=in_brackets[:], in0=tiles["two_u", n][:], scalar=-1.0, in1=tiles["eps_rr", n][:],
                op0=ALU.add, op1=ALU.add,
            )
            tiles["in_brackets", n] = in_brackets

        def coefficient(n):
            nc.gpsimd.tensor_tensor(
                out=tiles["factors", n][:, 1, :], in0=tiles["in_brackets", n][:], in1=tiles["dru", n][:],
                op=ALU.mult,
            )

        def to_tokens(n):
            by_token = psum_factors.tile([P, 2, P], F32, name="by_token")
            for which in range(2):
                turn(by_token[:, which, :], tiles["factors", n][:, which, :])
            tiles["by_token", n] = by_token

        def added_by_vector(n, first):
            return first < HALF or n == LAST

        def scale(n, first, last):
            some = slice(first, last)
            for which, name in enumerate(("hg", "ct")):
                by_slot = name == "hg" and not added_by_vector(n, first)
                if by_slot:
                    product = scaled.tile([P, last - first, PACK, P], F32, name="hg_by_slot")
                    in_order = product[:].rearrange("b c slot row -> b c row slot")
                else:
                    product = scaled.tile([P, last - first, P, PACK], F32, name=name)
                    in_order = product[:]
                nc.vector.tensor_tensor(
                    out=in_order.rearrange("b c (j quad) slot -> b c j quad slot", quad=QUADS),
                    in0=tiles[("g", "t")[which], n][:].rearrange(
                        "b (c j) (quad slot) -> b c j quad slot", c=PASSES, quad=QUADS
                    )[:, some],
                    in1=tiles["by_token", n][:, which, :]
                    .rearrange("b (c j) -> b c j", c=PASSES)[:, some]
                    .unsqueeze(3)
                    .unsqueeze(4)
                    .to_broadcast([P, last - first, CAPS_PASS, QUADS, PACK]),
                    op=ALU.mult,
                )
                tiles[name, n, first] = in_order

        def add(n, first, last):
            ds_words = scaled.tile([P, last - first, P, PACK], BF16, name="ds_words", align_bytes=64)
            nc.vector.tensor_tensor(
                out=ds_words[:], in0=tiles["hg", n, first], in1=tiles["ct", n, first], op=ALU.add
            )
            tiles["ds_words", n, first] = ds_words

        def transpose_words(n, first, last):
            count = last - first
            words = tiles["ds_words", n, first][:].rearrange("b c row slot -> b (c row slot)").bitcast(F32)
            words = words.rearrange("b (c row pair) -> b c row pair", c=count, pair=2)
            ds_t = psum_ds.tile([P, count, 2, P], F32, name="ds_t")
            for c in range(count):
                for pair in range(2):
                    turn(ds_t[:, c, pair, :], words[:, c, :, pair])
            if first == 0:
                grouped = rounded.tile([P, PASSES, P, PACK], BF16, name="grouped", align_bytes=64)
                tiles["grouped", n] = grouped
            nc.scalar.copy(
                out=tiles["grouped", n][:, first:last].rearrange("row c b slot -> row (c b slot)").bitcast(F32)
                .rearrange("row (c b pair) -> row c b pair", c=count, pair=2),
                in_=ds_t[:].rearrange("row c pair b -> row c b pair"),
            )

        def transpose_add(n, first, last):
            for c in range(last - first):
                ds_t = psum_ds.tile([P, PACK, P], F32, name="ds_t")
                for slot in range(PACK):
                    turn(ds_t[:, slot, :], tiles["hg", n, first][:, c, :, slot], stop=False)
                    turn(ds_t[:, slot, :], tiles["ct", n, first][:, c, :, slot], start=False)
                nc.scalar.copy(
                    out=tiles["grouped", n][:, first + c], in_=ds_t[:].rearrange("row slot b -> row b slot")
                )

        def quantise(n, first, last):
            if first == 0:
                codes = coded.tile([P, PASSES, P], U32, name="codes", align_bytes=64)
                scales = coded.tile([P, PASSES, P], U8, name="scales", align_bytes=64)
                tiles["codes", n] = codes
                tiles["scales", n] = scales
            nc.vector.quantize_mx(
                out=tiles["codes", n][:, first:last].rearrange("row c b -> row (c b)").bitcast(E5M2_X4),
                scales=tiles["scales", n][:, first:last].rearrange("row c b -> row (c b)"),
                in_=tiles["grouped", n][:, first:last].rearrange("row c b slot -> row (c b slot)"),
            )

        def multiply(n, first, last):
            block, part = divmod(n, CHUNKS_BLOCK)
            if part == 0 and first == 0:
                acc = psum_acc.tile([P, NI], F32, name="acc")
                tiles["acc", block] = acc
            for c in range(first, last):
                wp = part * PASSES + c
                nc.tensor.matmul_mx(
                    out=tiles["acc", block][:],
                    lhsT=tiles["codes", n][:, c, :].bitcast(E5M2_X4),
                    lhsT_scale=tiles["scales", n][:, c, :],
                    rhs=w_codes[:, wp, :].bitcast(E4M3_X4),
                    rhs_scale=w_scales[:, wp, :],
                    start=(wp == 0),
                    stop=(wp == W_PASSES - 1),
                )

        def store(n):
            block, part = divmod(n, CHUNKS_BLOCK)
            if part == CHUNKS_BLOCK - 1:
                result = results.tile([P, NI], F32, name="result")
                nc.scalar.mul(out=result[:], in_=tiles["acc", block][:], mul=1.0 / CAPS)
                nc.scalar.dma_start(out=out[block * P : (block + 1) * P].rearrange("b n i -> b (n i)"), in_=result[:])

        def live(n):
            return 0 <= n < N_CHUNKS

        def mx_step(n):
            return max(n + QUANT_LAG, MX_START + n // CHUNKS_BLOCK)

        def second_half(n):
            return [(HALF, PASSES)] if n < LAST else [(c, c + 1) for c in range(HALF, PASSES)]

        for n in range(AHEAD):
            load_t(n)
            load_g(n)
        for step in range(-3, N_CHUNKS + QUANT_LAG):
            due = [n for n in range(N_CHUNKS) if mx_step(n) == step]
            if live(step):
                r_times_u(step)
            if live(step - QUANT_LAG) and step - QUANT_LAG < LAST:
                quantise(step - QUANT_LAG, 0, PASSES)
            if live(step):
                h_factor(step)
                dot_ru(step)
            if 0 <= step - 2 < W_PASSES:
                quantise_weights(step - 2)
            if live(step - 1):
                add(step - 1, 0, HALF)
            if LATE <= step + 1 < N_CHUNKS:
                add_pairs(step + 1)
            if live(step):
                bracket(step)
                coefficient(step)
            if step == 0:
                to_tokens(0)
            if live(step + 1):
                sum_squares(step + 1)
            if step < 1 and live(step + 2):
                squares(step + 2)
            if live(step + 1):
                roots(step + 1)
            if live(step + 2) and step + 2 >= V_FIRST:
                t_times_g(step + 2, nc.gpsimd)
            if live(step - 1):
                transpose_words(step - 1, 0, HALF)
            if live(step) and step > 0:
                to_tokens(step)
            if step >= 1 and live(step + 2):
                squares(step + 2)
            if live(step - 1):
                for first, last in second_half(step - 1):
                    scale(step - 1, first, last)
            if live(step + 1):
                sum_products(step + 1)
            if step < LAST + QUANT_LAG:
                for n in due:
                    multiply(n, 0, PASSES)
                    store(n)
            if live(step):
                scale(step, 0, HALF)
            if 0 <= step + 2 < V_FIRST:
                t_times_g(step + 2, nc.vector)
            if live(step - 1):
                for first, last in second_half(step - 1):
                    if added_by_vector(step - 1, first):
                        add(step - 1, first, last)
                        transpose_words(step - 1, first, last)
                    else:
                        transpose_add(step - 1, first, last)
            if 0 <= step < W_PASSES:
                regroup_weights(step)
            if step == LAST + QUANT_LAG:
                for first, last in [(0, HALF)] + second_half(LAST):
                    quantise(LAST, first, last)
                    multiply(LAST, first, last)
                store(LAST)
            if 0 <= step + W_AHEAD < W_PASSES:
                load_weights(step + W_AHEAD)
            if live(step - 1) and live(step - 1 + AHEAD):
                load_g(step - 1 + AHEAD)
                load_t(step - 1 + AHEAD)
